import numpy as np
import ml_dtypes


def mxq(x, axis, fmt="e4m3"):
    dtype, down = {"e4m3": (ml_dtypes.float8_e4m3fn, 7), "e5m2": (ml_dtypes.float8_e5m2, 14)}[fmt]
    v = np.moveaxis(np.asarray(x, np.float32).astype(ml_dtypes.bfloat16).astype(np.float64), axis, -1)
    blocks = v.reshape(v.shape[:-1] + (-1, 32))
    amax = np.abs(blocks).max(-1, keepdims=True)
    byte = np.maximum(np.where(amax > 0, np.frexp(amax)[1] - 1 + 127, 0) - down, 1)
    scale = np.exp2(byte - 127.0)
    codes = (blocks / scale).astype(np.float32).astype(dtype).astype(np.float64)
    return np.moveaxis((codes * scale).reshape(v.shape), -1, axis)


WIDE = False


def mx_kscale(k):
    if not WIDE:
        return np.ones(k)
    levels = np.array([10, -10, 5, -5, 0])
    a = np.random.permutation(np.resize(levels, k // 512 * 4)).reshape(k // 512, 4)
    idx = np.arange(k)
    return np.exp2(a[idx // 512, idx % 128 // 32])


BF16 = ml_dtypes.bfloat16


def bf(x):
    return np.asarray(x, np.float32).astype(BF16)


def f64(x):
    return np.asarray(x).astype(np.float64)


B, D_IN, D_HID, D_OUT, LAT = 1024, 192, 2048, 1024, 16
BN_EPS = 1e-5
L2_EPS = 1e-12


def setup_inputs():
    t = mx_kscale(D_HID)
    col_sd = np.exp(0.4 * np.random.standard_normal(D_HID))
    col_mean = 0.5 * np.random.standard_normal(D_HID)
    return {
        "y_lin": bf(np.random.standard_normal((B, D_HID)) * col_sd + col_mean),
        "gamma": bf((1.0 + 0.2 * np.random.standard_normal(D_HID)) * t),
        "beta": bf(0.3 * np.random.standard_normal(D_HID) * t),
        "W2": bf(np.random.standard_normal((D_OUT, D_HID)) / np.sqrt(D_HID) / t[None, :]),
        "b2": bf(0.2 * np.random.standard_normal(D_OUT)),
    }


def reference(y_lin, gamma, beta, W2, b2):
    y = f64(y_lin)
    mean = np.mean(y, axis=0)
    var = np.mean((y - mean) ** 2, axis=0)
    y = (y - mean) * (1.0 / np.sqrt(var + BN_EPS)) * f64(gamma) + f64(beta)
    a = np.maximum(y, 0.0)
    p = (mxq(a, 1, "e4m3") @ mxq(f64(W2), 1, "e4m3").T) + f64(b2)
    n = np.sqrt(np.sum(p * p, axis=1, keepdims=True))
    return p / np.maximum(n, L2_EPS)

@@ -1,0 +1,180 @@
+from contextlib import ExitStack
+
+import concourse.mybir as mybir
+from concourse.masks import make_identity
+
+F32 = mybir.dt.float32
+BF16 = mybir.dt.bfloat16
+U32 = mybir.dt.uint32
+U8 = mybir.dt.uint8
+FP8X4 = mybir.dt.float8_e4m3fn_x4
+ACT = mybir.ActivationFunctionType
+ALU = mybir.AluOpType
+
+P = 128
+B = 1024
+K = 2048
+N = 1024
+K_PASS = 512
+PASSES = K // K_PASS
+RT = B // P
+NT = N // P
+HALF = 512
+BN_EPS = 1e-5
+INV_L2_EPS = 1e12
+
+FLOPS = 2 * B * K * N
+
+
+def tile_simclr_pa_kernel(tc, y_lin, gamma, beta, W2, b2, out):
+    nc = tc.nc
+    with ExitStack() as ctx:
+        keep = ctx.enter_context(tc.tile_pool(name="keep", bufs=1))
+        planes_pool = ctx.enter_context(tc.tile_pool(name="planes", bufs=2))
+        grp_pool = ctx.enter_context(tc.tile_pool(name="grp", bufs=3))
+        small = ctx.enter_context(tc.tile_pool(name="small", bufs=4))
+        outp = ctx.enter_context(tc.tile_pool(name="outp", bufs=3))
+        psum = ctx.enter_context(tc.psum_pool(name="psum", bufs=2))
+
+        ident = keep.tile([P, P], F32, name="ident")
+        make_identity(nc, ident[:])
+        eps = keep.tile([P, 1], F32, name="eps")
+        nc.vector.memset(eps[:], BN_EPS)
+
+        gam = keep.tile([P, 2 * PASSES, 2], BF16, name="gam")
+        bet = keep.tile([P, 2 * PASSES, 2], BF16, name="bet")
+        nc.scalar.dma_start(out=gam[:], in_=gamma.rearrange("(c p e) -> p c e", p=P, e=2))
+        nc.scalar.dma_start(out=bet[:], in_=beta.rearrange("(c p e) -> p c e", p=P, e=2))
+
+        y_view = y_lin.rearrange("(r p) k -> p r k", p=P)
+        w_view = W2.rearrange("(r p) k -> p r k", p=P)
+        y_sb = []
+        w_sb = []
+        for g in range(PASSES):
+            y_g = keep.tile([P, RT, K_PASS], BF16, name="y%d" % g)
+            nc.sync.dma_start(out=y_g[:], in_=y_view[:, :, g * K_PASS : (g + 1) * K_PASS])
+            y_sb.append(y_g)
+        for g in range(PASSES):
+            w_g = keep.tile([P, NT, K_PASS], BF16, name="w%d" % g)
+            nc.sync.dma_start(out=w_g[:], in_=w_view[:, :, g * K_PASS : (g + 1) * K_PASS])
+            w_sb.append(w_g)
+        b2_bc = keep.tile([P, N], BF16, name="b2_bc")
+        nc.sync.dma_start(out=b2_bc[:], in_=b2.partition_broadcast(P))
+
+        a_codes = keep.tile([P, PASSES, B], U32, name="a_codes", align_bytes=64)
+        a_scales = keep.tile([P, PASSES, B], U8, name="a_scales", align_bytes=64)
+        w_codes = keep.tile([P, PASSES, N], U32, name="w_codes", align_bytes=64)
+        w_scales = keep.tile([P, PASSES, N], U8, name="w_scales", align_bytes=64)
+
+        for g in range(PASSES):
+            planes = planes_pool.tile([P, 4, B], BF16, name="planes")
+            for u in range(2):
+                c = 2 * g + u
+                banks = []
+                for h in range(2):
+                    yT = psum.tile([P, HALF], F32, name="yT", bufs=4)
+                    for j in range(4):
+                        r = 4 * h + j
+                        nc.tensor.transpose(
+                            out=yT[:, j * P : (j + 1) * P],
+                            in_=y_sb[g][:, r, :].bitcast(F32)[:, u * P : (u + 1) * P],
+                            identity=ident[:],
+                        )
+                    banks.append(yT)
+                st = small.tile([P, 4, 6], F32, name="st")
+                for h in range(2):
+                    pairs = banks[h][:].bitcast(BF16)
+                    for j in range(2):
+                        nc.vector.bn_stats(
+                            out=st[:, 2 * h + j, :], in_=pairs[:, j * HALF : (j + 1) * HALF]
+                        )
+                mv = small.tile([P, 2, 2], F32, name="mv")
+                for e in range(2):
+                    nc.vector.bn_aggr(out=mv[:, e, :], in_=st[:, :, 3 * e : 3 * e + 3])
+                rstd = small.tile([P, 2], F32, name="rstd")
+                nc.scalar.activation(
+                    out=rstd[:], in_=mv[:, :, 1], func=ACT.Abs_reciprocal_sqrt, bias=eps[:, 0:1], scale=1.0
+                )
+                sc = small.tile([P, 2], F32, name="sc")
+                nc.vector.tensor_tensor(out=sc[:], in0=rstd[:], in1=gam[:, c, :], op=ALU.mult)
+                ms = small.tile([P, 2], F32, name="ms")
+                nc.vector.tensor_tensor(out=ms[:], in0=mv[:, :, 0], in1=sc[:], op=ALU.mult)
+                bi = small.tile([P, 2], F32, name="bi")
+                nc.vector.tensor_tensor(out=bi[:], in0=bet[:, c, :], in1=ms[:], op=ALU.subtract)
+                for h in range(2):
+                    pairs = banks[h][:].bitcast(BF16).rearrange("p (b e) -> p b e", e=2)
+                    for e in range(2):
+                        nc.scalar.activation(
+                            out=planes[:, 2 * u + e, h * HALF : (h + 1) * HALF],
+                            in_=pairs[:, :, e],
+                            func=ACT.Relu,
+                            bias=bi[:, e : e + 1],
+                            scale=sc[:, e : e + 1],
+                        )
+            groups = []
+            for h in range(2):
+                ag = grp_pool.tile([P, HALF, 4], BF16, name="ag", align_bytes=64)
+                nc.vector.tensor_copy(
+                    out=ag[:].rearrange("p (c i) t -> p c t i", i=4),
+                    in_=planes[:, :, h * HALF : (h + 1) * HALF].rearrange("p t (c i) -> p c t i", i=4),
+                )
+                groups.append(ag)
+            for h in range(2):
+                cols = slice(h * HALF, (h + 1) * HALF)
+                nc.vector.quantize_mx(
+                    out=a_codes[:, g, cols].bitcast(FP8X4),
+                    scales=a_scales[:, g, cols],
+                    in_=groups[h][:].rearrange("p b t -> p (b t)"),
+                )
+
+        for g in range(PASSES):
+            for h in range(2):
+                wg = grp_pool.tile([P, HALF, 4], BF16, name="wg", align_bytes=64)
+                wg_words = wg[:].rearrange("p n t -> p (n t)").bitcast(F32).rearrange("p (n u) -> p n u", u=2)
+                for q in range(2):
+                    wT = psum.tile([P, 2, 2 * P], F32, name="wT", bufs=2)
+                    for j in range(2):
+                        r = 4 * h + 2 * q + j
+                        for u in range(2):
+                            nc.tensor.transpose(
+                                out=wT[:, u, j * P : (j + 1) * P],
+                                in_=w_sb[g][:, r, :].bitcast(F32)[:, u * P : (u + 1) * P],
+                                identity=ident[:],
+                            )
+                    nc.scalar.copy(
+                        out=wg_words[:, q * 2 * P : (q + 1) * 2 * P, :],
+                        in_=wT[:].rearrange("p u n -> p n u"),
+                    )
+                cols = slice(h * HALF, (h + 1) * HALF)
+                nc.vector.quantize_mx(
+                    out=w_codes[:, g, cols].bitcast(FP8X4),
+                    scales=w_scales[:, g, cols],
+                    in_=wg[:].rearrange("p n t -> p (n t)"),
+                )
+
+        for m in range(RT):
+            rows = slice(m * P, (m + 1) * P)
+            pb = outp.tile([P, N], F32, name="pb")
+            for h in range(2):
+                cols = slice(h * HALF, (h + 1) * HALF)
+                acc = psum.tile([P, HALF], F32, name="acc", bufs=2)
+                for g in range(PASSES):
+                    nc.tensor.matmul_mx(
+                        out=acc[:],
+                        lhsT=a_codes[:, g, rows].bitcast(FP8X4),
+                        lhsT_scale=a_scales[:, g, rows],
+                        rhs=w_codes[:, g, cols].bitcast(FP8X4),
+                        rhs_scale=w_scales[:, g, cols],
+                        start=(g == 0),
+                        stop=(g == PASSES - 1),
+                    )
+                nc.vector.tensor_tensor(out=pb[:, cols], in0=acc[:], in1=b2_bc[:, cols], op=ALU.add)
+            sq = outp.tile([P, N], BF16, name="sq", bufs=2)
+            ss = small.tile([P, 1], F32, name="ss")
+            nc.scalar.activation(out=sq[:], in_=pb[:], func=ACT.Square, accum_out=ss[:, 0:1])
+            rn = small.tile([P, 1], F32, name="rn")
+            nc.scalar.activation(out=rn[:], in_=ss[:], func=ACT.Abs_reciprocal_sqrt)
+            rc = small.tile([P, 1], F32, name="rc")
+            nc.vector.tensor_scalar_min(out=rc[:], in0=rn[:], scalar1=INV_L2_EPS)
+            nc.vector.tensor_scalar_mul(out=pb[:], in0=pb[:], scalar1=rc[:, 0:1])
+            nc.sync.dma_start(out=out[rows, :], in_=pb[:])

@@ -17,164 +17,315 @@ K = 2048
 N = 1024
 K_PASS = 512
 PASSES = K // K_PASS
+UNITS = 2 * PASSES
 RT = B // P
 NT = N // P
 HALF = 512
+QUARTER = 256
 BN_EPS = 1e-5
-INV_L2_EPS = 1e12
+L2_EPS_SQ = 1e-24
 
 FLOPS = 2 * B * K * N
+
+PINNED = False
+PB_BUFS = 5
+WG_BUFS = 8
+AG_BUFS = 2
+LOAD_ORDER = [("y", 0), ("y", 1), ("w", 0), ("y", 2), ("w", 1), ("y", 3), ("w", 2), ("w", 3)]
+V_EXTRA = {8: [("WQ", 0, 0), ("WQ", 1, 0), ("WQ", 2, 0), ("RG", 0, 0, "v"), ("RG", 0, 1, "v"), ("RG", 0, 2, "v")]}
+S_EXTRA = {2: [("WX", (0, 0, 0), "s")], 3: [("WX", (0, 0, 1), "s")], 4: [("WX", (1, 0, 0), "s")], 5: [("WX", (1, 0, 1), "s")], 6: [("WX", (2, 0, 0), "s")], 7: [("WX", (2, 0, 1), "s")], 8: [("WX", (3, 0, 0), "s"), ("WX", (3, 0, 1), "s")]}
+PE_EXTRA = {1: [("WT", (0, 0, 0))], 2: [("WT", (0, 0, 1))], 3: [("WT", (1, 0, 0))], 4: [("WT", (1, 0, 1))], 5: [("WT", (2, 0, 0))], 6: [("WT", (2, 0, 1))], 7: [("WT", (3, 0, 0)), ("WT", (3, 0, 1))]}
+TAIL = [("WT", (0, 1, 0)), ("WT", (0, 1, 1)), ("WT", (1, 1, 0)), ("WT", (1, 1, 1)), ("WT", (2, 1, 0)), ("WT", (2, 1, 1)), ("RG", 0, 3, "v"), ("WQ", 3, 0), ("Q", 0), ("WX", (0, 1, 0), "s"), ("WX", (0, 1, 1), "s"), ("WT", (3, 1, 0)), ("WT", (3, 1, 1)), ("WX", (1, 1, 0), "s"), ("WX", (1, 1, 1), "s"), ("WX", (2, 1, 0), "s"), ("WX", (2, 1, 1), "s"), ("WX", (3, 1, 0), "s"), ("WX", (3, 1, 1), "s"), ("RG", 1, 0, "v"), ("RG", 1, 1, "v"), ("RG", 1, 2, "v"), ("RG", 1, 3, "v"), ("MX", 0, 0), ("MX", 1, 0), ("WQ", 0, 1), ("WQ", 1, 1), ("Q", 1), ("WQ", 2, 1), ("WQ", 3, 1), ("MX", 0, 1), ("ADD", 0, 0), ("SQ", 0, 0), ("RG", 2, 0, "v"), ("RG", 2, 1, "v"), ("MX", 1, 1), ("ADD", 1, 0), ("SQ", 1, 0), ("RG", 2, 2, "v"), ("RG", 2, 3, "v"), ("MX", 2, 0), ("ADD", 0, 1), ("SQ", 0, 1), ("Q", 2), ("MX", 2, 1), ("ADD", 1, 1), ("CL", 0), ("SQ", 1, 1), ("RN", 0), ("SCL", 0, 0, 512, "s"), ("RG", 3, 0, "v"), ("RG", 3, 1, "v"), ("MX", 3, 0), ("ADD", 2, 0), ("SQ", 2, 0), ("SCL", 0, 512, 1024, "v"), ("ST", 0, 0, 1024), ("RG", 3, 2, "v"), ("RG", 3, 3, "v"), ("MX", 3, 1), ("ADD", 2, 1), ("CL", 1), ("SQ", 2, 1), ("RN", 1), ("SCL", 1, 0, 512, "s"), ("Q", 3), ("MX", 4, 0), ("ADD", 3, 0), ("SQ", 3, 0), ("SCL", 1, 512, 1024, "v"), ("ST", 1, 0, 1024), ("MX", 4, 1), ("ADD", 3, 1), ("CL", 2), ("SQ", 3, 1), ("RN", 2), ("SCL", 2, 0, 512, "s"), ("MX", 5, 0), ("ADD", 4, 0), ("SQ", 4, 0), ("SCL", 2, 512, 1024, "v"), ("ST", 2, 0, 1024), ("MX", 5, 1), ("ADD", 4, 1), ("CL", 3), ("SQ", 4, 1), ("RN", 3), ("SCL", 3, 0, 512, "s"), ("MX", 6, 0), ("ADD", 5, 0), ("SQ", 5, 0), ("SCL", 3, 512, 1024, "v"), ("ST", 3, 0, 1024), ("MX", 6, 1), ("ADD", 5, 1), ("CL", 4), ("SQ", 5, 1), ("RN", 4), ("SCL", 4, 0, 512, "s"), ("MX", 7, 0), ("ADD", 6, 0), ("SQ", 6, 0), ("SCL", 4, 512, 1024, "v"), ("ST", 4, 0, 1024), ("MX", 7, 1), ("ADD", 6, 1), ("CL", 5), ("SQ", 6, 1), ("RN", 5), ("SCL", 5, 0, 512, "s"), ("ADD", 7, 0), ("SQ", 7, 0), ("SCL", 5, 512, 1024, "v"), ("ST", 5, 0, 1024), ("ADD", 7, 1), ("CL", 6), ("SQ", 7, 1), ("RN", 6), ("SCL", 6, 0, 512, "s"), ("SCL", 6, 512, 1024, "v"), ("ST", 6, 0, 1024), ("CL", 7), ("RN", 7), ("SCL", 7, 0, 512, "s"), ("SCL", 7, 512, 1024, "v"), ("ST", 7, 0, 1024)]
 
 
 def tile_simclr_pa_kernel(tc, y_lin, gamma, beta, W2, b2, out):
     nc = tc.nc
     with ExitStack() as ctx:
         keep = ctx.enter_context(tc.tile_pool(name="keep", bufs=1))
-        planes_pool = ctx.enter_context(tc.tile_pool(name="planes", bufs=2))
-        grp_pool = ctx.enter_context(tc.tile_pool(name="grp", bufs=3))
+        grp_pool = ctx.enter_context(tc.tile_pool(name="grp", bufs=2))
         small = ctx.enter_context(tc.tile_pool(name="small", bufs=4))
-        outp = ctx.enter_context(tc.tile_pool(name="outp", bufs=3))
-        psum = ctx.enter_context(tc.psum_pool(name="psum", bufs=2))
+        outp = ctx.enter_context(tc.tile_pool(name="outp", bufs=PB_BUFS))
+        psum = ctx.enter_context(tc.psum_pool(name="psum", bufs=1))
+        if PINNED:
+            ctx.enter_context(tc.manual_schedule())
+
+        free_banks = list(range(8))
+        taken = [0]
+
+        def take_bank():
+            i = free_banks[taken[0]]
+            taken[0] += 1
+            return i, psum.tile([P, HALF], F32, name="bank%d" % i, tag="bank%d" % i)
+
+        def give_bank(i):
+            free_banks.append(i)
 
         ident = keep.tile([P, P], F32, name="ident")
         make_identity(nc, ident[:])
         eps = keep.tile([P, 1], F32, name="eps")
         nc.vector.memset(eps[:], BN_EPS)
 
-        gam = keep.tile([P, 2 * PASSES, 2], BF16, name="gam")
-        bet = keep.tile([P, 2 * PASSES, 2], BF16, name="bet")
+        gam = keep.tile([P, UNITS, 2], BF16, name="gam")
+        bet = keep.tile([P, UNITS, 2], BF16, name="bet")
         nc.scalar.dma_start(out=gam[:], in_=gamma.rearrange("(c p e) -> p c e", p=P, e=2))
         nc.scalar.dma_start(out=bet[:], in_=beta.rearrange("(c p e) -> p c e", p=P, e=2))
 
         y_view = y_lin.rearrange("(r p) k -> p r k", p=P)
         w_view = W2.rearrange("(r p) k -> p r k", p=P)
-        y_sb = []
-        w_sb = []
-        for g in range(PASSES):
-            y_g = keep.tile([P, RT, K_PASS], BF16, name="y%d" % g)
-            nc.sync.dma_start(out=y_g[:], in_=y_view[:, :, g * K_PASS : (g + 1) * K_PASS])
-            y_sb.append(y_g)
-        for g in range(PASSES):
-            w_g = keep.tile([P, NT, K_PASS], BF16, name="w%d" % g)
-            nc.sync.dma_start(out=w_g[:], in_=w_view[:, :, g * K_PASS : (g + 1) * K_PASS])
-            w_sb.append(w_g)
+        y_sb = {}
+        w_sb = {}
+        for which, g in LOAD_ORDER:
+            k_cols = slice(g * K_PASS, (g + 1) * K_PASS)
+            if which == "y":
+                y_sb[g] = keep.tile([P, RT, K_PASS], BF16, name="y%d" % g)
+                nc.sync.dma_start(out=y_sb[g][:], in_=y_view[:, :, k_cols])
+            else:
+                w_sb[g] = keep.tile([P, NT, K_PASS], BF16, name="w%d" % g)
+                nc.sync.dma_start(out=w_sb[g][:], in_=w_view[:, :, k_cols])
         b2_bc = keep.tile([P, N], BF16, name="b2_bc")
         nc.sync.dma_start(out=b2_bc[:], in_=b2.partition_broadcast(P))
 
-        a_codes = keep.tile([P, PASSES, B], U32, name="a_codes", align_bytes=64)
-        a_scales = keep.tile([P, PASSES, B], U8, name="a_scales", align_bytes=64)
+        planes = keep.tile([P, 4 * PASSES, B], BF16, name="planes")
+        a_codes = keep.tile([P, 4, PASSES, QUARTER], U32, name="a_codes", align_bytes=64)
+        a_scales = keep.tile([P, 4, PASSES, QUARTER], U8, name="a_scales", align_bytes=64)
         w_codes = keep.tile([P, PASSES, N], U32, name="w_codes", align_bytes=64)
         w_scales = keep.tile([P, PASSES, N], U8, name="w_scales", align_bytes=64)
 
-        for g in range(PASSES):
-            planes = planes_pool.tile([P, 4, B], BF16, name="planes")
-            for u in range(2):
-                c = 2 * g + u
-                banks = []
-                for h in range(2):
-                    yT = psum.tile([P, HALF], F32, name="yT", bufs=4)
-                    for j in range(4):
-                        r = 4 * h + j
-                        nc.tensor.transpose(
-                            out=yT[:, j * P : (j + 1) * P],
-                            in_=y_sb[g][:, r, :].bitcast(F32)[:, u * P : (u + 1) * P],
-                            identity=ident[:],
-                        )
-                    banks.append(yT)
-                st = small.tile([P, 4, 6], F32, name="st")
-                for h in range(2):
-                    pairs = banks[h][:].bitcast(BF16)
-                    for j in range(2):
-                        nc.vector.bn_stats(
-                            out=st[:, 2 * h + j, :], in_=pairs[:, j * HALF : (j + 1) * HALF]
-                        )
-                mv = small.tile([P, 2, 2], F32, name="mv")
-                for e in range(2):
-                    nc.vector.bn_aggr(out=mv[:, e, :], in_=st[:, :, 3 * e : 3 * e + 3])
-                rstd = small.tile([P, 2], F32, name="rstd")
+        y_banks = {}
+        stats = {}
+        affine = {}
+        w_banks = {}
+        w_groups = {}
+        a_groups = {}
+
+        def transpose_unit(c):
+            g, u = divmod(c, 2)
+            pair = []
+            for h in range(2):
+                i, yT = take_bank()
+                for j in range(4):
+                    nc.tensor.transpose(
+                        out=yT[:, j * P : (j + 1) * P],
+                        in_=y_sb[g][:, 4 * h + j, :].bitcast(F32)[:, u * P : (u + 1) * P],
+                        identity=ident[:],
+                    )
+                pair.append((i, yT))
+            y_banks[c] = pair
+
+        def stats_half(c, h):
+            if h == 0:
+                stats[c] = small.tile([P, 4, 6], F32, name="st")
+            pairs = y_banks[c][h][1][:].bitcast(BF16)
+            for j in range(2):
+                nc.vector.bn_stats(out=stats[c][:, 2 * h + j, :], in_=pairs[:, j * HALF : (j + 1) * HALF])
+
+        def aggregate(c):
+            mv = small.tile([P, 2, 2], F32, name="mv")
+            for e in range(2):
+                nc.vector.bn_aggr(out=mv[:, e, :], in_=stats[c][:, :, 3 * e : 3 * e + 3])
+            mg = small.tile([P, 2], F32, name="mg")
+            nc.vector.tensor_tensor(out=mg[:], in0=mv[:, :, 0], in1=gam[:, c, :], op=ALU.mult)
+            affine[c] = [mv, mg]
+
+        def rstd_unit(c):
+            rstd = small.tile([P, 2], F32, name="rstd")
+            nc.scalar.activation(
+                out=rstd[:], in_=affine[c][0][:, :, 1], func=ACT.Abs_reciprocal_sqrt, bias=eps[:, 0:1], scale=1.0
+            )
+            affine[c].append(rstd)
+
+        def scale_bias(c):
+            mv, mg, rstd = affine[c]
+            ms = small.tile([P, 2], F32, name="ms")
+            nc.vector.tensor_tensor(out=ms[:], in0=mg[:], in1=rstd[:], op=ALU.mult)
+            sc = small.tile([P, 2], F32, name="sc")
+            nc.vector.tensor_tensor(out=sc[:], in0=rstd[:], in1=gam[:, c, :], op=ALU.mult)
+            bi = small.tile([P, 2], F32, name="bi")
+            nc.vector.tensor_tensor(out=bi[:], in0=bet[:, c, :], in1=ms[:], op=ALU.subtract)
+            affine[c] = [sc, bi]
+
+        def affine_half(c, h):
+            sc, bi = affine[c]
+            i, yT = y_banks[c][h]
+            pairs = yT[:].bitcast(BF16).rearrange("p (b e) -> p b e", e=2)
+            for e in range(2):
                 nc.scalar.activation(
-                    out=rstd[:], in_=mv[:, :, 1], func=ACT.Abs_reciprocal_sqrt, bias=eps[:, 0:1], scale=1.0
+                    out=planes[:, 2 * c + e, h * HALF : (h + 1) * HALF],
+                    in_=pairs[:, :, e],
+                    func=ACT.Relu,
+                    bias=bi[:, e : e + 1],
+                    scale=sc[:, e : e + 1],
                 )
-                sc = small.tile([P, 2], F32, name="sc")
-                nc.vector.tensor_tensor(out=sc[:], in0=rstd[:], in1=gam[:, c, :], op=ALU.mult)
-                ms = small.tile([P, 2], F32, name="ms")
-                nc.vector.tensor_tensor(out=ms[:], in0=mv[:, :, 0], in1=sc[:], op=ALU.mult)
-                bi = small.tile([P, 2], F32, name="bi")
-                nc.vector.tensor_tensor(out=bi[:], in0=bet[:, c, :], in1=ms[:], op=ALU.subtract)
-                for h in range(2):
-                    pairs = banks[h][:].bitcast(BF16).rearrange("p (b e) -> p b e", e=2)
-                    for e in range(2):
-                        nc.scalar.activation(
-                            out=planes[:, 2 * u + e, h * HALF : (h + 1) * HALF],
-                            in_=pairs[:, :, e],
-                            func=ACT.Relu,
-                            bias=bi[:, e : e + 1],
-                            scale=sc[:, e : e + 1],
-                        )
-            groups = []
-            for h in range(2):
-                ag = grp_pool.tile([P, HALF, 4], BF16, name="ag", align_bytes=64)
-                nc.vector.tensor_copy(
-                    out=ag[:].rearrange("p (c i) t -> p c t i", i=4),
-                    in_=planes[:, :, h * HALF : (h + 1) * HALF].rearrange("p t (c i) -> p c t i", i=4),
-                )
-                groups.append(ag)
-            for h in range(2):
-                cols = slice(h * HALF, (h + 1) * HALF)
-                nc.vector.quantize_mx(
-                    out=a_codes[:, g, cols].bitcast(FP8X4),
-                    scales=a_scales[:, g, cols],
-                    in_=groups[h][:].rearrange("p b t -> p (b t)"),
-                )
+            give_bank(i)
 
-        for g in range(PASSES):
-            for h in range(2):
-                wg = grp_pool.tile([P, HALF, 4], BF16, name="wg", align_bytes=64)
-                wg_words = wg[:].rearrange("p n t -> p (n t)").bitcast(F32).rearrange("p (n u) -> p n u", u=2)
-                for q in range(2):
-                    wT = psum.tile([P, 2, 2 * P], F32, name="wT", bufs=2)
-                    for j in range(2):
-                        r = 4 * h + 2 * q + j
-                        for u in range(2):
-                            nc.tensor.transpose(
-                                out=wT[:, u, j * P : (j + 1) * P],
-                                in_=w_sb[g][:, r, :].bitcast(F32)[:, u * P : (u + 1) * P],
-                                identity=ident[:],
-                            )
-                    nc.scalar.copy(
-                        out=wg_words[:, q * 2 * P : (q + 1) * 2 * P, :],
-                        in_=wT[:].rearrange("p u n -> p n u"),
+        def transpose_w(item):
+            g, h, q = item
+            i, wT = take_bank()
+            halves = wT[:].rearrange("p (u n) -> p u n", u=2)
+            for j in range(2):
+                for u in range(2):
+                    nc.tensor.transpose(
+                        out=halves[:, u, j * P : (j + 1) * P],
+                        in_=w_sb[g][:, 4 * h + 2 * q + j, :].bitcast(F32)[:, u * P : (u + 1) * P],
+                        identity=ident[:],
                     )
-                cols = slice(h * HALF, (h + 1) * HALF)
-                nc.vector.quantize_mx(
-                    out=w_codes[:, g, cols].bitcast(FP8X4),
-                    scales=w_scales[:, g, cols],
-                    in_=wg[:].rearrange("p n t -> p (n t)"),
-                )
+            w_banks[item] = (i, halves)
 
-        for m in range(RT):
-            rows = slice(m * P, (m + 1) * P)
-            pb = outp.tile([P, N], F32, name="pb")
-            for h in range(2):
-                cols = slice(h * HALF, (h + 1) * HALF)
-                acc = psum.tile([P, HALF], F32, name="acc", bufs=2)
-                for g in range(PASSES):
-                    nc.tensor.matmul_mx(
-                        out=acc[:],
-                        lhsT=a_codes[:, g, rows].bitcast(FP8X4),
-                        lhsT_scale=a_scales[:, g, rows],
-                        rhs=w_codes[:, g, cols].bitcast(FP8X4),
-                        rhs_scale=w_scales[:, g, cols],
-                        start=(g == 0),
-                        stop=(g == PASSES - 1),
-                    )
-                nc.vector.tensor_tensor(out=pb[:, cols], in0=acc[:], in1=b2_bc[:, cols], op=ALU.add)
-            sq = outp.tile([P, N], BF16, name="sq", bufs=2)
-            ss = small.tile([P, 1], F32, name="ss")
-            nc.scalar.activation(out=sq[:], in_=pb[:], func=ACT.Square, accum_out=ss[:, 0:1])
+        def exit_w(item, engine):
+            g, h, q = item
+            if q == 0:
+                w_groups[(g, h)] = grp_pool.tile([P, HALF, 4], BF16, name="wg", align_bytes=64, bufs=WG_BUFS)
+            wg = w_groups[(g, h)]
+            words = wg[:].rearrange("p n t -> p (n t)").bitcast(F32).rearrange("p (n u) -> p n u", u=2)
+            dst = words[:, q * QUARTER : (q + 1) * QUARTER, :]
+            i, halves = w_banks[item]
+            src = halves.rearrange("p u n -> p n u")
+            if engine == "v":
+                nc.vector.tensor_copy(out=dst, in_=src)
+            else:
+                nc.scalar.copy(out=dst, in_=src)
+            give_bank(i)
+
+        def quantise_w(g, h):
+            cols = slice(h * HALF, (h + 1) * HALF)
+            nc.vector.quantize_mx(
+                out=w_codes[:, g, cols].bitcast(FP8X4),
+                scales=w_scales[:, g, cols],
+                in_=w_groups[(g, h)][:].rearrange("p n t -> p (n t)"),
+            )
+
+        def regroup(bq, g, engine):
+            if bq not in a_groups:
+                a_groups[bq] = grp_pool.tile([P, PASSES, QUARTER, 4], BF16, name="ag", align_bytes=64, bufs=AG_BUFS)
+            dst = a_groups[bq][:, g, :, :].rearrange("p (c i) t -> p c t i", i=4)
+            src = planes[:, 4 * g : 4 * g + 4, bq * QUARTER : (bq + 1) * QUARTER].rearrange("p t (c i) -> p c t i", i=4)
+            if engine == "g":
+                nc.gpsimd.tensor_scalar(out=dst, in0=src, scalar1=1.0, scalar2=0.0, op0=ALU.mult, op1=ALU.add)
+            elif engine == "s":
+                nc.scalar.copy(out=dst, in_=src)
+            else:
+                nc.vector.tensor_copy(out=dst, in_=src)
+
+        def quantise_a(bq):
+            nc.vector.quantize_mx(
+                out=a_codes[:, bq, :, :].rearrange("p g b -> p (g b)").bitcast(FP8X4),
+                scales=a_scales[:, bq, :, :].rearrange("p g b -> p (g b)"),
+                in_=a_groups[bq][:].rearrange("p g b t -> p (g b t)"),
+            )
+
+        accs = {}
+        results = {}
+        norms = {}
+
+        def matmul_tile(m, h):
+            bq, ml = divmod(m, 2)
+            rows = slice(ml * P, (ml + 1) * P)
+            cols = slice(h * HALF, (h + 1) * HALF)
+            i, acc = take_bank()
+            for g in range(PASSES):
+                nc.tensor.matmul_mx(
+                    out=acc[:],
+                    lhsT=a_codes[:, bq, g, rows].bitcast(FP8X4),
+                    lhsT_scale=a_scales[:, bq, g, rows],
+                    rhs=w_codes[:, g, cols].bitcast(FP8X4),
+                    rhs_scale=w_scales[:, g, cols],
+                    start=(g == 0),
+                    stop=(g == PASSES - 1),
+                )
+            accs[(m, h)] = (i, acc)
+
+        def add_bias(m, h):
+            if m not in results:
+                results[m] = outp.tile([P, N], F32, name="pb")
+                norms[m] = small.tile([P, 2], F32, name="ss", bufs=PB_BUFS)
+            cols = slice(h * HALF, (h + 1) * HALF)
+            i, acc = accs[(m, h)]
+            nc.vector.tensor_tensor(out=results[m][:, cols], in0=acc[:], in1=b2_bc[:, cols], op=ALU.add)
+            give_bank(i)
+
+        def sum_squares(m, h):
+            cols = slice(h * HALF, (h + 1) * HALF)
+            sq = outp.tile([P, HALF], BF16, name="sq", bufs=2)
+            nc.scalar.activation(out=sq[:], in_=results[m][:, cols], func=ACT.Square, accum_out=norms[m][:, h : h + 1])
+
+        def clamp_norm(m):
+            cl = small.tile([P, 1], F32, name="cl")
+            nc.vector.tensor_scalar(
+                out=cl[:], in0=norms[m][:, 0:1], scalar1=norms[m][:, 1:2], scalar2=L2_EPS_SQ, op0=ALU.add, op1=ALU.max
+            )
+            norms[m] = cl
+
+        def inverse_norm(m):
             rn = small.tile([P, 1], F32, name="rn")
-            nc.scalar.activation(out=rn[:], in_=ss[:], func=ACT.Abs_reciprocal_sqrt)
-            rc = small.tile([P, 1], F32, name="rc")
-            nc.vector.tensor_scalar_min(out=rc[:], in0=rn[:], scalar1=INV_L2_EPS)
-            nc.vector.tensor_scalar_mul(out=pb[:], in0=pb[:], scalar1=rc[:, 0:1])
-            nc.sync.dma_start(out=out[rows, :], in_=pb[:])
+            nc.scalar.activation(out=rn[:], in_=norms[m][:], func=ACT.Abs_reciprocal_sqrt)
+            norms[m] = rn
+
+        def scale_rows(m, lo, hi, engine):
+            pb = results[m]
+            rn = norms[m]
+            if engine == "s":
+                nc.scalar.activation(out=pb[:, lo:hi], in_=pb[:, lo:hi], func=ACT.Copy, scale=rn[:, 0:1])
+            elif engine == "g":
+                nc.gpsimd.tensor_scalar(
+                    out=pb[:, lo:hi], in0=pb[:, lo:hi], scalar1=rn[:, 0:1], scalar2=0.0, op0=ALU.mult, op1=ALU.add
+                )
+            else:
+                nc.vector.tensor_scalar_mul(out=pb[:, lo:hi], in0=pb[:, lo:hi], scalar1=rn[:, 0:1])
+
+        def store_rows(m, lo, hi):
+            nc.sync.dma_start(out=out[m * P : (m + 1) * P, lo:hi], in_=results[m][:, lo:hi])
+
+        def run(steps):
+            for s in steps:
+                k = s[0]
+                if k == "T":
+                    transpose_unit(s[1])
+                elif k == "WT":
+                    transpose_w(s[1])
+                elif k == "WX":
+                    exit_w(s[1], s[2])
+                elif k == "WQ":
+                    quantise_w(s[1], s[2])
+                elif k == "RG":
+                    regroup(s[1], s[2], s[3])
+                elif k == "Q":
+                    quantise_a(s[1])
+                elif k == "MX":
+                    matmul_tile(s[1], s[2])
+                elif k == "ADD":
+                    add_bias(s[1], s[2])
+                elif k == "SQ":
+                    sum_squares(s[1], s[2])
+                elif k == "CL":
+                    clamp_norm(s[1])
+                elif k == "RN":
+                    inverse_norm(s[1])
+                elif k == "SCL":
+                    scale_rows(s[1], s[2], s[3], s[4])
+                elif k == "ST":
+                    store_rows(s[1], s[2], s[3])
+                else:
+                    raise ValueError(k)
+
+        transpose_unit(0)
+        transpose_unit(1)
+        for c in range(UNITS + 1):
+            if c < UNITS:
+                stats_half(c, 0)
+            if c >= 1:
+                scale_bias(c - 1)
+            if c < UNITS:
+                stats_half(c, 1)
+                aggregate(c)
+            run(V_EXTRA.get(c, ()))
+            if c >= 1:
+                affine_half(c - 1, 0)
+            if c < UNITS:
+                rstd_unit(c)
+            if c >= 1:
+                affine_half(c - 1, 1)
+            run(S_EXTRA.get(c, ()))
+            if c + 2 < UNITS:
+                transpose_unit(c + 2)
+            run(PE_EXTRA.get(c, ()))
+        run(TAIL)

@@ -28,14 +28,15 @@ L2_EPS_SQ = 1e-24
 FLOPS = 2 * B * K * N
 
 PINNED = False
+TY_ENGINE = "s"
 PB_BUFS = 5
 WG_BUFS = 8
-AG_BUFS = 2
+AG_BUFS = 4
 LOAD_ORDER = [("y", 0), ("y", 1), ("w", 0), ("y", 2), ("w", 1), ("y", 3), ("w", 2), ("w", 3)]
-V_EXTRA = {8: [("WQ", 0, 0), ("WQ", 1, 0), ("WQ", 2, 0), ("RG", 0, 0, "v"), ("RG", 0, 1, "v"), ("RG", 0, 2, "v")]}
-S_EXTRA = {2: [("WX", (0, 0, 0), "s")], 3: [("WX", (0, 0, 1), "s")], 4: [("WX", (1, 0, 0), "s")], 5: [("WX", (1, 0, 1), "s")], 6: [("WX", (2, 0, 0), "s")], 7: [("WX", (2, 0, 1), "s")], 8: [("WX", (3, 0, 0), "s"), ("WX", (3, 0, 1), "s")]}
+V_EXTRA = {3: [("RG", 0, 0, "g"), ("RG", 1, 0, "g"), ("RG", 2, 0, "g"), ("RG", 3, 0, "g")], 5: [("RG", 0, 1, "g"), ("RG", 1, 1, "g"), ("RG", 2, 1, "g"), ("RG", 3, 1, "g")], 7: [("RG", 0, 2, "g"), ("RG", 1, 2, "g"), ("RG", 2, 2, "g"), ("RG", 3, 2, "g")], 8: [("WQ", 0, 0), ("WQ", 1, 0), ("WQ", 2, 0)]}
+S_EXTRA = {2: [("WX", (0, 0, 0), "v")], 3: [("WX", (0, 0, 1), "v")], 4: [("WX", (1, 0, 0), "v")], 5: [("WX", (1, 0, 1), "v")], 6: [("WX", (2, 0, 0), "v")], 7: [("WX", (2, 0, 1), "v")], 8: [("WX", (3, 0, 0), "v"), ("WX", (3, 0, 1), "v")]}
 PE_EXTRA = {1: [("WT", (0, 0, 0))], 2: [("WT", (0, 0, 1))], 3: [("WT", (1, 0, 0))], 4: [("WT", (1, 0, 1))], 5: [("WT", (2, 0, 0))], 6: [("WT", (2, 0, 1))], 7: [("WT", (3, 0, 0)), ("WT", (3, 0, 1))]}
-TAIL = [("WT", (0, 1, 0)), ("WT", (0, 1, 1)), ("WT", (1, 1, 0)), ("WT", (1, 1, 1)), ("WT", (2, 1, 0)), ("WT", (2, 1, 1)), ("RG", 0, 3, "v"), ("WQ", 3, 0), ("Q", 0), ("WX", (0, 1, 0), "s"), ("WX", (0, 1, 1), "s"), ("WT", (3, 1, 0)), ("WT", (3, 1, 1)), ("WX", (1, 1, 0), "s"), ("WX", (1, 1, 1), "s"), ("WX", (2, 1, 0), "s"), ("WX", (2, 1, 1), "s"), ("WX", (3, 1, 0), "s"), ("WX", (3, 1, 1), "s"), ("RG", 1, 0, "v"), ("RG", 1, 1, "v"), ("RG", 1, 2, "v"), ("RG", 1, 3, "v"), ("MX", 0, 0), ("MX", 1, 0), ("WQ", 0, 1), ("WQ", 1, 1), ("Q", 1), ("WQ", 2, 1), ("WQ", 3, 1), ("MX", 0, 1), ("ADD", 0, 0), ("SQ", 0, 0), ("RG", 2, 0, "v"), ("RG", 2, 1, "v"), ("MX", 1, 1), ("ADD", 1, 0), ("SQ", 1, 0), ("RG", 2, 2, "v"), ("RG", 2, 3, "v"), ("MX", 2, 0), ("ADD", 0, 1), ("SQ", 0, 1), ("Q", 2), ("MX", 2, 1), ("ADD", 1, 1), ("CL", 0), ("SQ", 1, 1), ("RN", 0), ("SCL", 0, 0, 512, "s"), ("RG", 3, 0, "v"), ("RG", 3, 1, "v"), ("MX", 3, 0), ("ADD", 2, 0), ("SQ", 2, 0), ("SCL", 0, 512, 1024, "v"), ("ST", 0, 0, 1024), ("RG", 3, 2, "v"), ("RG", 3, 3, "v"), ("MX", 3, 1), ("ADD", 2, 1), ("CL", 1), ("SQ", 2, 1), ("RN", 1), ("SCL", 1, 0, 512, "s"), ("Q", 3), ("MX", 4, 0), ("ADD", 3, 0), ("SQ", 3, 0), ("SCL", 1, 512, 1024, "v"), ("ST", 1, 0, 1024), ("MX", 4, 1), ("ADD", 3, 1), ("CL", 2), ("SQ", 3, 1), ("RN", 2), ("SCL", 2, 0, 512, "s"), ("MX", 5, 0), ("ADD", 4, 0), ("SQ", 4, 0), ("SCL", 2, 512, 1024, "v"), ("ST", 2, 0, 1024), ("MX", 5, 1), ("ADD", 4, 1), ("CL", 3), ("SQ", 4, 1), ("RN", 3), ("SCL", 3, 0, 512, "s"), ("MX", 6, 0), ("ADD", 5, 0), ("SQ", 5, 0), ("SCL", 3, 512, 1024, "v"), ("ST", 3, 0, 1024), ("MX", 6, 1), ("ADD", 5, 1), ("CL", 4), ("SQ", 5, 1), ("RN", 4), ("SCL", 4, 0, 512, "s"), ("MX", 7, 0), ("ADD", 6, 0), ("SQ", 6, 0), ("SCL", 4, 512, 1024, "v"), ("ST", 4, 0, 1024), ("MX", 7, 1), ("ADD", 6, 1), ("CL", 5), ("SQ", 6, 1), ("RN", 5), ("SCL", 5, 0, 512, "s"), ("ADD", 7, 0), ("SQ", 7, 0), ("SCL", 5, 512, 1024, "v"), ("ST", 5, 0, 1024), ("ADD", 7, 1), ("CL", 6), ("SQ", 7, 1), ("RN", 6), ("SCL", 6, 0, 512, "s"), ("SCL", 6, 512, 1024, "v"), ("ST", 6, 0, 1024), ("CL", 7), ("RN", 7), ("SCL", 7, 0, 512, "s"), ("SCL", 7, 512, 1024, "v"), ("ST", 7, 0, 1024)]
+TAIL = [("WT", (0, 1, 0)), ("WT", (0, 1, 1)), ("WT", (1, 1, 0)), ("WT", (1, 1, 1)), ("WT", (2, 1, 0)), ("WT", (2, 1, 1)), ("RG", 0, 3, "v"), ("WQ", 3, 0), ("Q", 0), ("WX", (0, 1, 0), "s"), ("WX", (0, 1, 1), "s"), ("WT", (3, 1, 0)), ("WT", (3, 1, 1)), ("WX", (1, 1, 0), "s"), ("WX", (1, 1, 1), "s"), ("WX", (2, 1, 0), "s"), ("WX", (2, 1, 1), "s"), ("WX", (3, 1, 0), "s"), ("WX", (3, 1, 1), "s"), ("RG", 1, 3, "v"), ("MX", 0, 0), ("MX", 1, 0), ("WQ", 0, 1), ("WQ", 1, 1), ("Q", 1), ("WQ", 2, 1), ("WQ", 3, 1), ("MX", 0, 1), ("ADD", 0, 0), ("SQ", 0, 0), ("MX", 1, 1), ("ADD", 1, 0), ("SQ", 1, 0), ("RG", 2, 3, "v"), ("MX", 2, 0), ("ADD", 0, 1), ("SQ", 0, 1), ("Q", 2), ("MX", 2, 1), ("ADD", 1, 1), ("CL", 0), ("SQ", 1, 1), ("RN", 0), ("SCL", 0, 0, 512, "s"), ("SCL", 0, 512, 1024, "v"), ("ST", 0, 0, 1024), ("MX", 3, 0), ("ADD", 2, 0), ("CL", 1), ("SQ", 2, 0), ("RN", 1), ("SCL", 1, 0, 512, "s"), ("SCL", 1, 512, 1024, "v"), ("ST", 1, 0, 1024), ("RG", 3, 3, "v"), ("MX", 3, 1), ("ADD", 2, 1), ("SQ", 2, 1), ("Q", 3), ("MX", 4, 0), ("ADD", 3, 0), ("CL", 2), ("SQ", 3, 0), ("RN", 2), ("SCL", 2, 0, 512, "s"), ("SCL", 2, 512, 1024, "v"), ("ST", 2, 0, 1024), ("MX", 4, 1), ("ADD", 3, 1), ("SQ", 3, 1), ("MX", 5, 0), ("ADD", 4, 0), ("CL", 3), ("SQ", 4, 0), ("RN", 3), ("SCL", 3, 0, 512, "s"), ("SCL", 3, 512, 1024, "v"), ("ST", 3, 0, 1024), ("MX", 5, 1), ("ADD", 4, 1), ("SQ", 4, 1), ("MX", 6, 0), ("ADD", 5, 0), ("CL", 4), ("SQ", 5, 0), ("RN", 4), ("SCL", 4, 0, 512, "s"), ("SCL", 4, 512, 1024, "v"), ("ST", 4, 0, 1024), ("MX", 6, 1), ("ADD", 5, 1), ("SQ", 5, 1), ("MX", 7, 0), ("ADD", 6, 0), ("CL", 5), ("SQ", 6, 0), ("RN", 5), ("SCL", 5, 0, 512, "s"), ("SCL", 5, 512, 1024, "v"), ("ST", 5, 0, 1024), ("MX", 7, 1), ("ADD", 6, 1), ("SQ", 6, 1), ("ADD", 7, 0), ("CL", 6), ("SQ", 7, 0), ("RN", 6), ("SCL", 6, 0, 512, "s"), ("SCL", 6, 512, 1024, "v"), ("ST", 6, 0, 1024), ("ADD", 7, 1), ("SQ", 7, 1), ("CL", 7), ("RN", 7), ("SCL", 7, 0, 512, "s"), ("SCL", 7, 512, 1024, "v"), ("ST", 7, 0, 1024)]
 
 
 def tile_simclr_pa_kernel(tc, y_lin, gamma, beta, W2, b2, out):
@@ -69,6 +70,14 @@ def tile_simclr_pa_kernel(tc, y_lin, gamma, beta, W2, b2, out):
         bet = keep.tile([P, UNITS, 2], BF16, name="bet")
         nc.scalar.dma_start(out=gam[:], in_=gamma.rearrange("(c p e) -> p c e", p=P, e=2))
         nc.scalar.dma_start(out=bet[:], in_=beta.rearrange("(c p e) -> p c e", p=P, e=2))
+
+        gam_f = keep.tile([P, UNITS, 2], F32, name="gam_f")
+        ngam_f = keep.tile([P, UNITS, 2], F32, name="ngam_f")
+        bet_f = keep.tile([P, UNITS, 2], F32, name="bet_f")
+        if TY_ENGINE == "s":
+            nc.vector.tensor_copy(out=gam_f[:], in_=gam[:])
+            nc.vector.tensor_scalar_mul(out=ngam_f[:], in0=gam[:], scalar1=-1.0)
+            nc.vector.tensor_copy(out=bet_f[:], in_=bet[:])
 
         y_view = y_lin.rearrange("(r p) k -> p r k", p=P)
         w_view = W2.rearrange("(r p) k -> p r k", p=P)
@@ -124,7 +133,8 @@ def tile_simclr_pa_kernel(tc, y_lin, gamma, beta, W2, b2, out):
             for e in range(2):
                 nc.vector.bn_aggr(out=mv[:, e, :], in_=stats[c][:, :, 3 * e : 3 * e + 3])
             mg = small.tile([P, 2], F32, name="mg")
-            nc.vector.tensor_tensor(out=mg[:], in0=mv[:, :, 0], in1=gam[:, c, :], op=ALU.mult)
+            if TY_ENGINE == "v":
+                nc.vector.tensor_tensor(out=mg[:], in0=mv[:, :, 0], in1=gam[:, c, :], op=ALU.mult)
             affine[c] = [mv, mg]
 
         def rstd_unit(c):
@@ -136,6 +146,21 @@ def tile_simclr_pa_kernel(tc, y_lin, gamma, beta, W2, b2, out):
 
         def scale_bias(c):
             mv, mg, rstd = affine[c]
+            if TY_ENGINE == "s":
+                sc = small.tile([P, 2], F32, name="sc")
+                nsc = small.tile([P, 2], F32, name="nsc")
+                bi = small.tile([P, 2], F32, name="bi")
+                for e in range(2):
+                    col = slice(e, e + 1)
+                    nc.scalar.activation(out=nsc[:, col], in_=ngam_f[:, c, col], func=ACT.Copy, scale=rstd[:, col])
+                    nc.scalar.activation(out=sc[:, col], in_=gam_f[:, c, col], func=ACT.Copy, scale=rstd[:, col])
+                for e in range(2):
+                    col = slice(e, e + 1)
+                    nc.scalar.activation(
+                        out=bi[:, col], in_=mv[:, e, 0:1], func=ACT.Identity, scale=nsc[:, col], bias=bet_f[:, c, col]
+                    )
+                affine[c] = [sc, bi]
+                return
             ms = small.tile([P, 2], F32, name="ms")
             nc.vector.tensor_tensor(out=ms[:], in0=mg[:], in1=rstd[:], op=ALU.mult)
             sc = small.tile([P, 2], F32, name="sc")

@@ -27,16 +27,12 @@ L2_EPS_SQ = 1e-24
 
 FLOPS = 2 * B * K * N
 
-PINNED = False
+PINNED = True
 TY_ENGINE = "s"
-PB_BUFS = 5
 WG_BUFS = 8
-AG_BUFS = 4
-LOAD_ORDER = [("y", 0), ("y", 1), ("w", 0), ("y", 2), ("w", 1), ("y", 3), ("w", 2), ("w", 3)]
-V_EXTRA = {3: [("RG", 0, 0, "g"), ("RG", 1, 0, "g"), ("RG", 2, 0, "g"), ("RG", 3, 0, "g")], 5: [("RG", 0, 1, "g"), ("RG", 1, 1, "g"), ("RG", 2, 1, "g"), ("RG", 3, 1, "g")], 7: [("RG", 0, 2, "g"), ("RG", 1, 2, "g"), ("RG", 2, 2, "g"), ("RG", 3, 2, "g")], 8: [("WQ", 0, 0), ("WQ", 1, 0), ("WQ", 2, 0)]}
-S_EXTRA = {2: [("WX", (0, 0, 0), "v")], 3: [("WX", (0, 0, 1), "v")], 4: [("WX", (1, 0, 0), "v")], 5: [("WX", (1, 0, 1), "v")], 6: [("WX", (2, 0, 0), "v")], 7: [("WX", (2, 0, 1), "v")], 8: [("WX", (3, 0, 0), "v"), ("WX", (3, 0, 1), "v")]}
-PE_EXTRA = {1: [("WT", (0, 0, 0))], 2: [("WT", (0, 0, 1))], 3: [("WT", (1, 0, 0))], 4: [("WT", (1, 0, 1))], 5: [("WT", (2, 0, 0))], 6: [("WT", (2, 0, 1))], 7: [("WT", (3, 0, 0)), ("WT", (3, 0, 1))]}
-TAIL = [("WT", (0, 1, 0)), ("WT", (0, 1, 1)), ("WT", (1, 1, 0)), ("WT", (1, 1, 1)), ("WT", (2, 1, 0)), ("WT", (2, 1, 1)), ("RG", 0, 3, "v"), ("WQ", 3, 0), ("Q", 0), ("WX", (0, 1, 0), "s"), ("WX", (0, 1, 1), "s"), ("WT", (3, 1, 0)), ("WT", (3, 1, 1)), ("WX", (1, 1, 0), "s"), ("WX", (1, 1, 1), "s"), ("WX", (2, 1, 0), "s"), ("WX", (2, 1, 1), "s"), ("WX", (3, 1, 0), "s"), ("WX", (3, 1, 1), "s"), ("RG", 1, 3, "v"), ("MX", 0, 0), ("MX", 1, 0), ("WQ", 0, 1), ("WQ", 1, 1), ("Q", 1), ("WQ", 2, 1), ("WQ", 3, 1), ("MX", 0, 1), ("ADD", 0, 0), ("SQ", 0, 0), ("MX", 1, 1), ("ADD", 1, 0), ("SQ", 1, 0), ("RG", 2, 3, "v"), ("MX", 2, 0), ("ADD", 0, 1), ("SQ", 0, 1), ("Q", 2), ("MX", 2, 1), ("ADD", 1, 1), ("CL", 0), ("SQ", 1, 1), ("RN", 0), ("SCL", 0, 0, 512, "s"), ("SCL", 0, 512, 1024, "v"), ("ST", 0, 0, 1024), ("MX", 3, 0), ("ADD", 2, 0), ("CL", 1), ("SQ", 2, 0), ("RN", 1), ("SCL", 1, 0, 512, "s"), ("SCL", 1, 512, 1024, "v"), ("ST", 1, 0, 1024), ("RG", 3, 3, "v"), ("MX", 3, 1), ("ADD", 2, 1), ("SQ", 2, 1), ("Q", 3), ("MX", 4, 0), ("ADD", 3, 0), ("CL", 2), ("SQ", 3, 0), ("RN", 2), ("SCL", 2, 0, 512, "s"), ("SCL", 2, 512, 1024, "v"), ("ST", 2, 0, 1024), ("MX", 4, 1), ("ADD", 3, 1), ("SQ", 3, 1), ("MX", 5, 0), ("ADD", 4, 0), ("CL", 3), ("SQ", 4, 0), ("RN", 3), ("SCL", 3, 0, 512, "s"), ("SCL", 3, 512, 1024, "v"), ("ST", 3, 0, 1024), ("MX", 5, 1), ("ADD", 4, 1), ("SQ", 4, 1), ("MX", 6, 0), ("ADD", 5, 0), ("CL", 4), ("SQ", 5, 0), ("RN", 4), ("SCL", 4, 0, 512, "s"), ("SCL", 4, 512, 1024, "v"), ("ST", 4, 0, 1024), ("MX", 6, 1), ("ADD", 5, 1), ("SQ", 5, 1), ("MX", 7, 0), ("ADD", 6, 0), ("CL", 5), ("SQ", 6, 0), ("RN", 5), ("SCL", 5, 0, 512, "s"), ("SCL", 5, 512, 1024, "v"), ("ST", 5, 0, 1024), ("MX", 7, 1), ("ADD", 6, 1), ("SQ", 6, 1), ("ADD", 7, 0), ("CL", 6), ("SQ", 7, 0), ("RN", 6), ("SCL", 6, 0, 512, "s"), ("SCL", 6, 512, 1024, "v"), ("ST", 6, 0, 1024), ("ADD", 7, 1), ("SQ", 7, 1), ("CL", 7), ("RN", 7), ("SCL", 7, 0, 512, "s"), ("SCL", 7, 512, 1024, "v"), ("ST", 7, 0, 1024)]
+LOAD_ORDER = [("piece", 0), ("piece", 1), ("piece", 2), ("piece", 3), ("y", 1), ("w", 0), ("y", 2), ("w", 1), ("y", 3), ("w", 2), ("w", 3)]
+MARK = [-1]
+STEPS = [("T", 0, 0, 0), ("SA", 0, 0), ("T", 0, 1, 1), ("T", 1, 0, 2), ("SA", 0, 1), ("T", 1, 1, 3), ("AG", 0), ("SA", 1, 0), ("R", 0), ("TY", 0), ("AF", 0, 1), ("SA", 1, 1), ("T", 2, 1, 5), ("T", 2, 0, 4), ("AG", 1), ("T", 3, 1, 7), ("SA", 2, 1), ("R", 1), ("T", 3, 0, 6), ("TY", 1), ("AF", 1, 1), ("SA", 2, 0), ("AF", 0, 0), ("RG", 0, 2, "g"), ("SA", 3, 0), ("AF", 1, 0), ("WT", (0, 0, 0), 0), ("SA", 3, 1), ("RG", 0, 3, "g"), ("WX", (0, 0, 0), "s"), ("AG", 2), ("AG", 3), ("T", 4, 1, 2), ("R", 2), ("R", 3), ("TY", 2), ("WT", (0, 0, 1), 3), ("TY", 3), ("RG", 0, 0, "g"), ("SA", 4, 1), ("T", 4, 0, 1), ("AF", 2, 0), ("SA", 4, 0), ("AF", 3, 0), ("T", 5, 1, 4), ("T", 5, 0, 0), ("WX", (0, 0, 1), "v"), ("AF", 2, 1), ("RG", 1, 1, "g"), ("SA", 5, 1), ("AF", 3, 1), ("SA", 5, 0), ("WT", (1, 0, 0), 5), ("RG", 0, 1, "g"), ("WX", (1, 0, 0), "s"), ("T", 6, 0, 3), ("AG", 4), ("AG", 5), ("T", 6, 1, 6), ("R", 4), ("SA", 6, 0), ("TY", 4), ("T", 7, 0, 5), ("R", 5), ("RG", 1, 2, "g"), ("AF", 4, 0), ("WT", (1, 0, 1), 7), ("SA", 6, 1), ("AF", 4, 1), ("T", 7, 1, 1), ("RG", 1, 0, "g"), ("AG", 6), ("WX", (1, 0, 1), "v"), ("R", 6), ("TY", 5), ("SA", 7, 1), ("TY", 6), ("WT", (2, 0, 1), 7), ("AF", 5, 1), ("WT", (2, 0, 0), 2), ("RG", 1, 3, "g"), ("SA", 7, 0), ("AF", 6, 1), ("WT", (3, 0, 1), 4), ("RG", 2, 2, "v"), ("AF", 6, 0), ("Q", 0, 512, 1024), ("AG", 7), ("WX", (3, 0, 1), "v"), ("AF", 5, 0), ("WX", (2, 0, 1), "v"), ("WT", (0, 1, 1), 3), ("WT", (1, 1, 0), 6), ("Q", 0, 0, 512), ("WX", (2, 0, 0), "s"), ("Q", 1, 0, 512), ("WT", (3, 0, 0), 0), ("WT", (3, 1, 1), 4), ("WX", (0, 1, 1), "s"), ("RG", 2, 1, "v"), ("WT", (0, 1, 0), 2), ("R", 7), ("WX", (3, 0, 0), "s"), ("WQ", 0, 0), ("TY", 7), ("RG", 2, 0, "v"), ("WT", (3, 1, 0), 0), ("AF", 7, 0), ("WT", (1, 1, 1), 7), ("WQ", 3, 0), ("Q", 2, 0, 512), ("WX", (0, 1, 0), "s"), ("WT", (2, 1, 0), 5), ("WQ", 1, 0), ("AF", 7, 1), ("MX", 0, 0, 0, 1, 2), ("RG", 3, 1, "v"), ("MX", 0, 0, 1, 2, -1), ("RG", 3, 0, "v"), ("MX", 1, 0, 0, 1, 3), ("WX", (2, 1, 0), "s"), ("WT", (2, 1, 1), 1), ("WQ", 2, 0), ("WX", (1, 1, 0), "s"), ("MX", 1, 0, 1, 2, -1), ("Q", 3, 0, 512), ("MX", 2, 0, 0, 1, 5), ("WX", (1, 1, 1), "s"), ("MX", 0, 0, 2, 3, -1), ("WQ", 0, 1), ("WX", (2, 1, 1), "s"), ("MX", 0, 0, 3, 4, -1), ("RG", 3, 3, "v"), ("MX", 2, 0, 1, 2, -1), ("WX", (3, 1, 0), "s"), ("MX", 1, 0, 2, 3, -1), ("MX", 2, 1, 0, 1, 1), ("WX", (3, 1, 1), "s"), ("WQ", 1, 1), ("MX", 1, 1, 0, 1, 7), ("MX", 1, 0, 3, 4, -1), ("RG", 2, 3, "v"), ("MX", 0, 1, 0, 1, 6), ("MX", 3, 1, 0, 1, 4), ("WQ", 2, 1), ("MX", 2, 1, 1, 2, -1), ("MX", 2, 0, 2, 3, -1), ("Q", 1, 512, 1024), ("MX", 3, 0, 0, 1, 0), ("MX", 3, 1, 1, 2, -1), ("WQ", 3, 1), ("MX", 3, 1, 2, 3, -1), ("MX", 1, 1, 1, 2, -1), ("ADD", 0, 0), ("MX", 2, 1, 2, 3, -1), ("MX", 0, 1, 1, 2, -1), ("ADD", 1, 0), ("MX", 0, 1, 2, 3, -1), ("MX", 0, 1, 3, 4, -1), ("RG", 3, 2, "v"), ("MX", 3, 0, 1, 2, -1), ("SQ", 1, 0), ("MX", 1, 1, 2, 3, -1), ("ADD", 0, 1), ("MX", 1, 1, 3, 4, -1), ("SQ", 0, 0), ("MX", 2, 1, 3, 4, -1), ("Q", 2, 512, 1024), ("MX", 3, 0, 2, 3, -1), ("SQ", 0, 1), ("MX", 2, 0, 3, 4, -1), ("ADD", 1, 1), ("MX", 4, 0, 0, 1, 2), ("MX", 3, 1, 3, 4, -1), ("ADD", 2, 1), ("MX", 5, 0, 0, 1, 6), ("SQ", 1, 1), ("MX", 5, 1, 0, 1, 7), ("ADD", 2, 0), ("MX", 5, 0, 1, 2, -1), ("SQ", 2, 1), ("MX", 6, 1, 0, 1, 1), ("CL", 0), ("ADD", 3, 1), ("MX", 4, 0, 1, 2, -1), ("RN", 0), ("MX", 4, 1, 0, 1, 3), ("SQ", 2, 0), ("Q", 3, 512, 1024), ("MX", 4, 0, 2, 3, -1), ("MX", 3, 0, 3, 4, -1), ("SQ", 3, 1), ("MX", 5, 1, 1, 2, -1), ("CL", 2), ("SCL", 0, 512, 1024, "v"), ("MX", 4, 0, 3, 4, -1), ("CL", 1), ("ADD", 3, 0), ("RN", 2), ("SCL", 0, 0, 512, "s"), ("MX", 5, 0, 2, 3, -1), ("MX", 5, 0, 3, 4, -1), ("SCL", 2, 512, 1024, "v"), ("RN", 1), ("SCL", 2, 0, 512, "s"), ("MX", 4, 1, 1, 2, -1), ("ST", 0, 0, 1024), ("ADD", 4, 0), ("MX", 4, 1, 2, 3, -1), ("SQ", 3, 0), ("MX", 4, 1, 3, 4, -1), ("ST", 2, 0, 1024), ("MX", 6, 1, 1, 2, -1), ("MX", 5, 1, 2, 3, -1), ("SQ", 4, 0), ("ADD", 4, 1), ("MX", 5, 1, 3, 4, -1), ("MX", 6, 0, 0, 1, 5), ("SCL", 1, 0, 512, "s"), ("CL", 3), ("SCL", 1, 512, 1024, "v"), ("MX", 7, 0, 0, 1, 0), ("ADD", 5, 0), ("MX", 6, 0, 1, 2, -1), ("RN", 3), ("SQ", 4, 1), ("MX", 6, 0, 2, 3, -1), ("ST", 1, 0, 1024), ("ADD", 5, 1), ("MX", 6, 0, 3, 4, -1), ("SCL", 3, 0, 512, "s"), ("MX", 7, 0, 1, 2, -1), ("CL", 4), ("MX", 6, 1, 2, 3, -1), ("ADD", 6, 0), ("SQ", 5, 1), ("MX", 7, 1, 0, 1, 4), ("MX", 7, 0, 2, 3, -1), ("SCL", 3, 512, 1024, "v"), ("MX", 7, 1, 1, 2, -1), ("RN", 4), ("SQ", 5, 0), ("SCL", 4, 512, 1024, "v"), ("MX", 6, 1, 3, 4, -1), ("ST", 3, 0, 1024), ("MX", 7, 1, 2, 3, -1), ("SCL", 4, 0, 512, "s"), ("MX", 7, 1, 3, 4, -1), ("CL", 5), ("ADD", 6, 1), ("MX", 7, 0, 3, 4, -1), ("SQ", 6, 0), ("ST", 4, 0, 1024), ("ADD", 7, 0), ("RN", 5), ("SQ", 6, 1), ("ADD", 7, 1), ("SCL", 5, 0, 512, "s"), ("CL", 6), ("SCL", 5, 512, 1024, "v"), ("RN", 6), ("SQ", 7, 1), ("SCL", 6, 512, 1024, "v"), ("ST", 5, 0, 1024), ("SCL", 6, 0, 512, "s"), ("SQ", 7, 0), ("ST", 6, 0, 1024), ("CL", 7), ("RN", 7), ("SCL", 7, 0, 512, "s"), ("SCL", 7, 512, 1024, "v"), ("ST", 7, 0, 1024)]
 
 
 def tile_simclr_pa_kernel(tc, y_lin, gamma, beta, W2, b2, out):
@@ -44,22 +40,17 @@ def tile_simclr_pa_kernel(tc, y_lin, gamma, beta, W2, b2, out):
     with ExitStack() as ctx:
         keep = ctx.enter_context(tc.tile_pool(name="keep", bufs=1))
         grp_pool = ctx.enter_context(tc.tile_pool(name="grp", bufs=2))
-        small = ctx.enter_context(tc.tile_pool(name="small", bufs=4))
-        outp = ctx.enter_context(tc.tile_pool(name="outp", bufs=PB_BUFS))
+        small = ctx.enter_context(tc.tile_pool(name="small", bufs=8))
+        outp = ctx.enter_context(tc.tile_pool(name="outp", bufs=2))
         psum = ctx.enter_context(tc.psum_pool(name="psum", bufs=1))
         if PINNED:
             ctx.enter_context(tc.manual_schedule())
 
-        free_banks = list(range(8))
-        taken = [0]
-
-        def take_bank():
-            i = free_banks[taken[0]]
-            taken[0] += 1
+        def take_bank(i):
             return i, psum.tile([P, HALF], F32, name="bank%d" % i, tag="bank%d" % i)
 
         def give_bank(i):
-            free_banks.append(i)
+            return i
 
         ident = keep.tile([P, P], F32, name="ident")
         make_identity(nc, ident[:])
@@ -85,7 +76,13 @@ def tile_simclr_pa_kernel(tc, y_lin, gamma, beta, W2, b2, out):
         w_sb = {}
         for which, g in LOAD_ORDER:
             k_cols = slice(g * K_PASS, (g + 1) * K_PASS)
-            if which == "y":
+            if which == "piece":
+                c, h = divmod(g, 2)
+                y_sb[("piece", c, h)] = keep.tile([P, 4, QUARTER], BF16, name="yp%d" % g)
+                nc.sync.dma_start(
+                    out=y_sb[("piece", c, h)][:], in_=y_view[:, 4 * h : 4 * h + 4, c * QUARTER : (c + 1) * QUARTER]
+                )
+            elif which == "y":
                 y_sb[g] = keep.tile([P, RT, K_PASS], BF16, name="y%d" % g)
                 nc.sync.dma_start(out=y_sb[g][:], in_=y_view[:, :, k_cols])
             else:
@@ -94,9 +91,12 @@ def tile_simclr_pa_kernel(tc, y_lin, gamma, beta, W2, b2, out):
         b2_bc = keep.tile([P, N], BF16, name="b2_bc")
         nc.sync.dma_start(out=b2_bc[:], in_=b2.partition_broadcast(P))
 
-        planes = keep.tile([P, 4 * PASSES, B], BF16, name="planes")
-        a_codes = keep.tile([P, 4, PASSES, QUARTER], U32, name="a_codes", align_bytes=64)
-        a_scales = keep.tile([P, 4, PASSES, QUARTER], U8, name="a_scales", align_bytes=64)
+        planes = {}
+        for g in range(PASSES):
+            for h in range(2):
+                planes[(g, h)] = keep.tile([P, 4, HALF], BF16, name="planes%d%d" % (g, h))
+        a_codes = keep.tile([P, PASSES, B], U32, name="a_codes", align_bytes=64)
+        a_scales = keep.tile([P, PASSES, B], U8, name="a_scales", align_bytes=64)
         w_codes = keep.tile([P, PASSES, N], U32, name="w_codes", align_bytes=64)
         w_scales = keep.tile([P, PASSES, N], U8, name="w_scales", align_bytes=64)
 
@@ -107,24 +107,22 @@ def tile_simclr_pa_kernel(tc, y_lin, gamma, beta, W2, b2, out):
         w_groups = {}
         a_groups = {}
 
-        def transpose_unit(c):
+        def transpose_unit(c, h, b):
             g, u = divmod(c, 2)
-            pair = []
-            for h in range(2):
-                i, yT = take_bank()
+            if True:
+                i, yT = take_bank(b)
                 for j in range(4):
-                    nc.tensor.transpose(
-                        out=yT[:, j * P : (j + 1) * P],
-                        in_=y_sb[g][:, 4 * h + j, :].bitcast(F32)[:, u * P : (u + 1) * P],
-                        identity=ident[:],
-                    )
-                pair.append((i, yT))
-            y_banks[c] = pair
+                    if ("piece", c, h) in y_sb:
+                        words = y_sb[("piece", c, h)][:, j, :].bitcast(F32)
+                    else:
+                        words = y_sb[g][:, 4 * h + j, :].bitcast(F32)[:, u * P : (u + 1) * P]
+                    nc.tensor.transpose(out=yT[:, j * P : (j + 1) * P], in_=words, identity=ident[:])
+                y_banks[(c, h)] = (i, yT)
 
         def stats_half(c, h):
-            if h == 0:
+            if c not in stats:
                 stats[c] = small.tile([P, 4, 6], F32, name="st")
-            pairs = y_banks[c][h][1][:].bitcast(BF16)
+            pairs = y_banks[(c, h)][1][:].bitcast(BF16)
             for j in range(2):
                 nc.vector.bn_stats(out=stats[c][:, 2 * h + j, :], in_=pairs[:, j * HALF : (j + 1) * HALF])
 
@@ -171,11 +169,11 @@ def tile_simclr_pa_kernel(tc, y_lin, gamma, beta, W2, b2, out):
 
         def affine_half(c, h):
             sc, bi = affine[c]
-            i, yT = y_banks[c][h]
+            i, yT = y_banks[(c, h)]
             pairs = yT[:].bitcast(BF16).rearrange("p (b e) -> p b e", e=2)
             for e in range(2):
                 nc.scalar.activation(
-                    out=planes[:, 2 * c + e, h * HALF : (h + 1) * HALF],
+                    out=planes[(c // 2, h)][:, 2 * (c % 2) + e, :],
                     in_=pairs[:, :, e],
                     func=ACT.Relu,
                     bias=bi[:, e : e + 1],
@@ -183,9 +181,9 @@ def tile_simclr_pa_kernel(tc, y_lin, gamma, beta, W2, b2, out):
                 )
             give_bank(i)
 
-        def transpose_w(item):
+        def transpose_w(item, b):
             g, h, q = item
-            i, wT = take_bank()
+            i, wT = take_bank(b)
             halves = wT[:].rearrange("p (u n) -> p u n", u=2)
             for j in range(2):
                 for u in range(2):
@@ -198,7 +196,7 @@ def tile_simclr_pa_kernel(tc, y_lin, gamma, beta, W2, b2, out):
 
         def exit_w(item, engine):
             g, h, q = item
-            if q == 0:
+            if (g, h) not in w_groups:
                 w_groups[(g, h)] = grp_pool.tile([P, HALF, 4], BF16, name="wg", align_bytes=64, bufs=WG_BUFS)
             wg = w_groups[(g, h)]
             words = wg[:].rearrange("p n t -> p (n t)").bitcast(F32).rearrange("p (n u) -> p n u", u=2)
@@ -219,11 +217,13 @@ def tile_simclr_pa_kernel(tc, y_lin, gamma, beta, W2, b2, out):
                 in_=w_groups[(g, h)][:].rearrange("p n t -> p (n t)"),
             )
 
-        def regroup(bq, g, engine):
-            if bq not in a_groups:
-                a_groups[bq] = grp_pool.tile([P, PASSES, QUARTER, 4], BF16, name="ag", align_bytes=64, bufs=AG_BUFS)
-            dst = a_groups[bq][:, g, :, :].rearrange("p (c i) t -> p c t i", i=4)
-            src = planes[:, 4 * g : 4 * g + 4, bq * QUARTER : (bq + 1) * QUARTER].rearrange("p t (c i) -> p c t i", i=4)
+        def regroup(g, bq, engine):
+            if g not in a_groups:
+                a_groups[g] = grp_pool.tile([P, B, 4], BF16, name="ag", align_bytes=64, bufs=PASSES)
+            rows = slice(bq * QUARTER, (bq + 1) * QUARTER)
+            dst = a_groups[g][:, rows, :].rearrange("p (c i) t -> p c t i", i=4)
+            part = slice((bq % 2) * QUARTER, (bq % 2 + 1) * QUARTER)
+            src = planes[(g, bq // 2)][:, :, part].rearrange("p t (c i) -> p c t i", i=4)
             if engine == "g":
                 nc.gpsimd.tensor_scalar(out=dst, in0=src, scalar1=1.0, scalar2=0.0, op0=ALU.mult, op1=ALU.add)
             elif engine == "s":
@@ -231,47 +231,50 @@ def tile_simclr_pa_kernel(tc, y_lin, gamma, beta, W2, b2, out):
             else:
                 nc.vector.tensor_copy(out=dst, in_=src)
 
-        def quantise_a(bq):
+        def quantise_a(g, lo, hi):
             nc.vector.quantize_mx(
-                out=a_codes[:, bq, :, :].rearrange("p g b -> p (g b)").bitcast(FP8X4),
-                scales=a_scales[:, bq, :, :].rearrange("p g b -> p (g b)"),
-                in_=a_groups[bq][:].rearrange("p g b t -> p (g b t)"),
+                out=a_codes[:, g, lo:hi].bitcast(FP8X4),
+                scales=a_scales[:, g, lo:hi],
+                in_=a_groups[g][:, lo:hi, :].rearrange("p b t -> p (b t)"),
             )
 
         accs = {}
-        results = {}
+        pairs_out = {}
         norms = {}
 
-        def matmul_tile(m, h):
-            bq, ml = divmod(m, 2)
-            rows = slice(ml * P, (ml + 1) * P)
+        def matmul_tile(m, h, g0, g1, b):
+            rows = slice(m * P, (m + 1) * P)
             cols = slice(h * HALF, (h + 1) * HALF)
-            i, acc = take_bank()
-            for g in range(PASSES):
+            if g0 == 0:
+                accs[(m, h)] = take_bank(b)
+            i, acc = accs[(m, h)]
+            for g in range(g0, g1):
                 nc.tensor.matmul_mx(
                     out=acc[:],
-                    lhsT=a_codes[:, bq, g, rows].bitcast(FP8X4),
-                    lhsT_scale=a_scales[:, bq, g, rows],
+                    lhsT=a_codes[:, g, rows].bitcast(FP8X4),
+                    lhsT_scale=a_scales[:, g, rows],
                     rhs=w_codes[:, g, cols].bitcast(FP8X4),
                     rhs_scale=w_scales[:, g, cols],
                     start=(g == 0),
                     stop=(g == PASSES - 1),
                 )
-            accs[(m, h)] = (i, acc)
+
+        def result(m):
+            return pairs_out[m // 2][:, m % 2, :]
 
         def add_bias(m, h):
-            if m not in results:
-                results[m] = outp.tile([P, N], F32, name="pb")
-                norms[m] = small.tile([P, 2], F32, name="ss", bufs=PB_BUFS)
+            if m // 2 not in pairs_out:
+                pairs_out[m // 2] = keep.tile([P, 2, N], F32, name="pb%d" % (m // 2), tag="y%d" % (m // 2))
+            if m not in norms:
+                norms[m] = small.tile([P, 2], F32, name="ss")
             cols = slice(h * HALF, (h + 1) * HALF)
             i, acc = accs[(m, h)]
-            nc.vector.tensor_tensor(out=results[m][:, cols], in0=acc[:], in1=b2_bc[:, cols], op=ALU.add)
-            give_bank(i)
+            nc.vector.tensor_tensor(out=result(m)[:, cols], in0=acc[:], in1=b2_bc[:, cols], op=ALU.add)
 
         def sum_squares(m, h):
             cols = slice(h * HALF, (h + 1) * HALF)
-            sq = outp.tile([P, HALF], BF16, name="sq", bufs=2)
-            nc.scalar.activation(out=sq[:], in_=results[m][:, cols], func=ACT.Square, accum_out=norms[m][:, h : h + 1])
+            sq = outp.tile([P, HALF], BF16, name="sq")
+            nc.scalar.activation(out=sq[:], in_=result(m)[:, cols], func=ACT.Square, accum_out=norms[m][:, h : h + 1])
 
         def clamp_norm(m):
             cl = small.tile([P, 1], F32, name="cl")
@@ -286,7 +289,7 @@ def tile_simclr_pa_kernel(tc, y_lin, gamma, beta, W2, b2, out):
             norms[m] = rn
 
         def scale_rows(m, lo, hi, engine):
-            pb = results[m]
+            pb = result(m)
             rn = norms[m]
             if engine == "s":
                 nc.scalar.activation(out=pb[:, lo:hi], in_=pb[:, lo:hi], func=ACT.Copy, scale=rn[:, 0:1])
@@ -298,59 +301,13 @@ def tile_simclr_pa_kernel(tc, y_lin, gamma, beta, W2, b2, out):
                 nc.vector.tensor_scalar_mul(out=pb[:, lo:hi], in0=pb[:, lo:hi], scalar1=rn[:, 0:1])
 
         def store_rows(m, lo, hi):
-            nc.sync.dma_start(out=out[m * P : (m + 1) * P, lo:hi], in_=results[m][:, lo:hi])
+            nc.sync.dma_start(out=out[m * P : (m + 1) * P, lo:hi], in_=result(m)[:, lo:hi])
 
-        def run(steps):
-            for s in steps:
-                k = s[0]
-                if k == "T":
-                    transpose_unit(s[1])
-                elif k == "WT":
-                    transpose_w(s[1])
-                elif k == "WX":
-                    exit_w(s[1], s[2])
-                elif k == "WQ":
-                    quantise_w(s[1], s[2])
-                elif k == "RG":
-                    regroup(s[1], s[2], s[3])
-                elif k == "Q":
-                    quantise_a(s[1])
-                elif k == "MX":
-                    matmul_tile(s[1], s[2])
-                elif k == "ADD":
-                    add_bias(s[1], s[2])
-                elif k == "SQ":
-                    sum_squares(s[1], s[2])
-                elif k == "CL":
-                    clamp_norm(s[1])
-                elif k == "RN":
-                    inverse_norm(s[1])
-                elif k == "SCL":
-                    scale_rows(s[1], s[2], s[3], s[4])
-                elif k == "ST":
-                    store_rows(s[1], s[2], s[3])
-                else:
-                    raise ValueError(k)
-
-        transpose_unit(0)
-        transpose_unit(1)
-        for c in range(UNITS + 1):
-            if c < UNITS:
-                stats_half(c, 0)
-            if c >= 1:
-                scale_bias(c - 1)
-            if c < UNITS:
-                stats_half(c, 1)
-                aggregate(c)
-            run(V_EXTRA.get(c, ()))
-            if c >= 1:
-                affine_half(c - 1, 0)
-            if c < UNITS:
-                rstd_unit(c)
-            if c >= 1:
-                affine_half(c - 1, 1)
-            run(S_EXTRA.get(c, ()))
-            if c + 2 < UNITS:
-                transpose_unit(c + 2)
-            run(PE_EXTRA.get(c, ()))
-        run(TAIL)
+        table = {
+            "T": transpose_unit, "SA": stats_half, "AG": aggregate, "R": rstd_unit, "TY": scale_bias, "AF": affine_half,
+            "WT": transpose_w, "WX": exit_w, "WQ": quantise_w, "RG": regroup, "Q": quantise_a, "MX": matmul_tile,
+            "ADD": add_bias, "SQ": sum_squares, "CL": clamp_norm, "RN": inverse_norm, "SCL": scale_rows, "ST": store_rows,
+        }
+        for n, s in enumerate(STEPS):
+            MARK[0] = n
+            table[s[0]](*s[1:])

@@ -18,172 +18,157 @@ N = 1024
 K_PASS = 512
 PASSES = K // K_PASS
 UNITS = 2 * PASSES
-RT = B // P
-NT = N // P
+UNIT_K = K // UNITS
 HALF = 512
 QUARTER = 256
+BANKS = 8
 BN_EPS = 1e-5
 L2_EPS_SQ = 1e-24
 
 FLOPS = 2 * B * K * N
 
-PINNED = True
-TY_ENGINE = "s"
-WG_BUFS = 8
-LOAD_ORDER = [("piece", 0), ("piece", 1), ("piece", 2), ("piece", 3), ("y", 1), ("w", 0), ("y", 2), ("w", 1), ("y", 3), ("w", 2), ("w", 3)]
-MARK = [-1]
-STEPS = [("T", 0, 0, 0), ("SA", 0, 0), ("T", 0, 1, 1), ("T", 1, 0, 2), ("SA", 0, 1), ("T", 1, 1, 3), ("AG", 0), ("SA", 1, 0), ("R", 0), ("TY", 0), ("AF", 0, 1), ("SA", 1, 1), ("T", 2, 1, 5), ("T", 2, 0, 4), ("AG", 1), ("T", 3, 1, 7), ("SA", 2, 1), ("R", 1), ("T", 3, 0, 6), ("TY", 1), ("AF", 1, 1), ("SA", 2, 0), ("AF", 0, 0), ("RG", 0, 2, "g"), ("SA", 3, 0), ("AF", 1, 0), ("WT", (0, 0, 0), 0), ("SA", 3, 1), ("RG", 0, 3, "g"), ("WX", (0, 0, 0), "s"), ("AG", 2), ("AG", 3), ("T", 4, 1, 2), ("R", 2), ("R", 3), ("TY", 2), ("WT", (0, 0, 1), 3), ("TY", 3), ("RG", 0, 0, "g"), ("SA", 4, 1), ("T", 4, 0, 1), ("AF", 2, 0), ("SA", 4, 0), ("AF", 3, 0), ("T", 5, 1, 4), ("T", 5, 0, 0), ("WX", (0, 0, 1), "v"), ("AF", 2, 1), ("RG", 1, 1, "g"), ("SA", 5, 1), ("AF", 3, 1), ("SA", 5, 0), ("WT", (1, 0, 0), 5), ("RG", 0, 1, "g"), ("WX", (1, 0, 0), "s"), ("T", 6, 0, 3), ("AG", 4), ("AG", 5), ("T", 6, 1, 6), ("R", 4), ("SA", 6, 0), ("TY", 4), ("T", 7, 0, 5), ("R", 5), ("RG", 1, 2, "g"), ("AF", 4, 0), ("WT", (1, 0, 1), 7), ("SA", 6, 1), ("AF", 4, 1), ("T", 7, 1, 1), ("RG", 1, 0, "g"), ("AG", 6), ("WX", (1, 0, 1), "v"), ("R", 6), ("TY", 5), ("SA", 7, 1), ("TY", 6), ("WT", (2, 0, 1), 7), ("AF", 5, 1), ("WT", (2, 0, 0), 2), ("RG", 1, 3, "g"), ("SA", 7, 0), ("AF", 6, 1), ("WT", (3, 0, 1), 4), ("RG", 2, 2, "v"), ("AF", 6, 0), ("Q", 0, 512, 1024), ("AG", 7), ("WX", (3, 0, 1), "v"), ("AF", 5, 0), ("WX", (2, 0, 1), "v"), ("WT", (0, 1, 1), 3), ("WT", (1, 1, 0), 6), ("Q", 0, 0, 512), ("WX", (2, 0, 0), "s"), ("Q", 1, 0, 512), ("WT", (3, 0, 0), 0), ("WT", (3, 1, 1), 4), ("WX", (0, 1, 1), "s"), ("RG", 2, 1, "v"), ("WT", (0, 1, 0), 2), ("R", 7), ("WX", (3, 0, 0), "s"), ("WQ", 0, 0), ("TY", 7), ("RG", 2, 0, "v"), ("WT", (3, 1, 0), 0), ("AF", 7, 0), ("WT", (1, 1, 1), 7), ("WQ", 3, 0), ("Q", 2, 0, 512), ("WX", (0, 1, 0), "s"), ("WT", (2, 1, 0), 5), ("WQ", 1, 0), ("AF", 7, 1), ("MX", 0, 0, 0, 1, 2), ("RG", 3, 1, "v"), ("MX", 0, 0, 1, 2, -1), ("RG", 3, 0, "v"), ("MX", 1, 0, 0, 1, 3), ("WX", (2, 1, 0), "s"), ("WT", (2, 1, 1), 1), ("WQ", 2, 0), ("WX", (1, 1, 0), "s"), ("MX", 1, 0, 1, 2, -1), ("Q", 3, 0, 512), ("MX", 2, 0, 0, 1, 5), ("WX", (1, 1, 1), "s"), ("MX", 0, 0, 2, 3, -1), ("WQ", 0, 1), ("WX", (2, 1, 1), "s"), ("MX", 0, 0, 3, 4, -1), ("RG", 3, 3, "v"), ("MX", 2, 0, 1, 2, -1), ("WX", (3, 1, 0), "s"), ("MX", 1, 0, 2, 3, -1), ("MX", 2, 1, 0, 1, 1), ("WX", (3, 1, 1), "s"), ("WQ", 1, 1), ("MX", 1, 1, 0, 1, 7), ("MX", 1, 0, 3, 4, -1), ("RG", 2, 3, "v"), ("MX", 0, 1, 0, 1, 6), ("MX", 3, 1, 0, 1, 4), ("WQ", 2, 1), ("MX", 2, 1, 1, 2, -1), ("MX", 2, 0, 2, 3, -1), ("Q", 1, 512, 1024), ("MX", 3, 0, 0, 1, 0), ("MX", 3, 1, 1, 2, -1), ("WQ", 3, 1), ("MX", 3, 1, 2, 3, -1), ("MX", 1, 1, 1, 2, -1), ("ADD", 0, 0), ("MX", 2, 1, 2, 3, -1), ("MX", 0, 1, 1, 2, -1), ("ADD", 1, 0), ("MX", 0, 1, 2, 3, -1), ("MX", 0, 1, 3, 4, -1), ("RG", 3, 2, "v"), ("MX", 3, 0, 1, 2, -1), ("SQ", 1, 0), ("MX", 1, 1, 2, 3, -1), ("ADD", 0, 1), ("MX", 1, 1, 3, 4, -1), ("SQ", 0, 0), ("MX", 2, 1, 3, 4, -1), ("Q", 2, 512, 1024), ("MX", 3, 0, 2, 3, -1), ("SQ", 0, 1), ("MX", 2, 0, 3, 4, -1), ("ADD", 1, 1), ("MX", 4, 0, 0, 1, 2), ("MX", 3, 1, 3, 4, -1), ("ADD", 2, 1), ("MX", 5, 0, 0, 1, 6), ("SQ", 1, 1), ("MX", 5, 1, 0, 1, 7), ("ADD", 2, 0), ("MX", 5, 0, 1, 2, -1), ("SQ", 2, 1), ("MX", 6, 1, 0, 1, 1), ("CL", 0), ("ADD", 3, 1), ("MX", 4, 0, 1, 2, -1), ("RN", 0), ("MX", 4, 1, 0, 1, 3), ("SQ", 2, 0), ("Q", 3, 512, 1024), ("MX", 4, 0, 2, 3, -1), ("MX", 3, 0, 3, 4, -1), ("SQ", 3, 1), ("MX", 5, 1, 1, 2, -1), ("CL", 2), ("SCL", 0, 512, 1024, "v"), ("MX", 4, 0, 3, 4, -1), ("CL", 1), ("ADD", 3, 0), ("RN", 2), ("SCL", 0, 0, 512, "s"), ("MX", 5, 0, 2, 3, -1), ("MX", 5, 0, 3, 4, -1), ("SCL", 2, 512, 1024, "v"), ("RN", 1), ("SCL", 2, 0, 512, "s"), ("MX", 4, 1, 1, 2, -1), ("ST", 0, 0, 1024), ("ADD", 4, 0), ("MX", 4, 1, 2, 3, -1), ("SQ", 3, 0), ("MX", 4, 1, 3, 4, -1), ("ST", 2, 0, 1024), ("MX", 6, 1, 1, 2, -1), ("MX", 5, 1, 2, 3, -1), ("SQ", 4, 0), ("ADD", 4, 1), ("MX", 5, 1, 3, 4, -1), ("MX", 6, 0, 0, 1, 5), ("SCL", 1, 0, 512, "s"), ("CL", 3), ("SCL", 1, 512, 1024, "v"), ("MX", 7, 0, 0, 1, 0), ("ADD", 5, 0), ("MX", 6, 0, 1, 2, -1), ("RN", 3), ("SQ", 4, 1), ("MX", 6, 0, 2, 3, -1), ("ST", 1, 0, 1024), ("ADD", 5, 1), ("MX", 6, 0, 3, 4, -1), ("SCL", 3, 0, 512, "s"), ("MX", 7, 0, 1, 2, -1), ("CL", 4), ("MX", 6, 1, 2, 3, -1), ("ADD", 6, 0), ("SQ", 5, 1), ("MX", 7, 1, 0, 1, 4), ("MX", 7, 0, 2, 3, -1), ("SCL", 3, 512, 1024, "v"), ("MX", 7, 1, 1, 2, -1), ("RN", 4), ("SQ", 5, 0), ("SCL", 4, 512, 1024, "v"), ("MX", 6, 1, 3, 4, -1), ("ST", 3, 0, 1024), ("MX", 7, 1, 2, 3, -1), ("SCL", 4, 0, 512, "s"), ("MX", 7, 1, 3, 4, -1), ("CL", 5), ("ADD", 6, 1), ("MX", 7, 0, 3, 4, -1), ("SQ", 6, 0), ("ST", 4, 0, 1024), ("ADD", 7, 0), ("RN", 5), ("SQ", 6, 1), ("ADD", 7, 1), ("SCL", 5, 0, 512, "s"), ("CL", 6), ("SCL", 5, 512, 1024, "v"), ("RN", 6), ("SQ", 7, 1), ("SCL", 6, 512, 1024, "v"), ("ST", 5, 0, 1024), ("SCL", 6, 0, 512, "s"), ("SQ", 7, 0), ("ST", 6, 0, 1024), ("CL", 7), ("RN", 7), ("SCL", 7, 0, 512, "s"), ("SCL", 7, 512, 1024, "v"), ("ST", 7, 0, 1024)]
+GPSIMD_PASSES = 2
+TILES_AHEAD = 4
 
 
 def tile_simclr_pa_kernel(tc, y_lin, gamma, beta, W2, b2, out):
     nc = tc.nc
     with ExitStack() as ctx:
         keep = ctx.enter_context(tc.tile_pool(name="keep", bufs=1))
-        grp_pool = ctx.enter_context(tc.tile_pool(name="grp", bufs=2))
-        small = ctx.enter_context(tc.tile_pool(name="small", bufs=8))
-        outp = ctx.enter_context(tc.tile_pool(name="outp", bufs=2))
+        small = ctx.enter_context(tc.tile_pool(name="small", bufs=UNITS))
+        junk = ctx.enter_context(tc.tile_pool(name="junk", bufs=2))
         psum = ctx.enter_context(tc.psum_pool(name="psum", bufs=1))
-        if PINNED:
-            ctx.enter_context(tc.manual_schedule())
 
-        def take_bank(i):
+        free_banks = list(range(BANKS))
+        taken = [0]
+
+        def take_bank():
+            i = free_banks[taken[0]]
+            taken[0] += 1
             return i, psum.tile([P, HALF], F32, name="bank%d" % i, tag="bank%d" % i)
 
         def give_bank(i):
-            return i
+            free_banks.append(i)
 
         ident = keep.tile([P, P], F32, name="ident")
         make_identity(nc, ident[:])
         eps = keep.tile([P, 1], F32, name="eps")
         nc.vector.memset(eps[:], BN_EPS)
-
-        gam = keep.tile([P, UNITS, 2], BF16, name="gam")
-        bet = keep.tile([P, UNITS, 2], BF16, name="bet")
-        nc.scalar.dma_start(out=gam[:], in_=gamma.rearrange("(c p e) -> p c e", p=P, e=2))
-        nc.scalar.dma_start(out=bet[:], in_=beta.rearrange("(c p e) -> p c e", p=P, e=2))
-
-        gam_f = keep.tile([P, UNITS, 2], F32, name="gam_f")
-        ngam_f = keep.tile([P, UNITS, 2], F32, name="ngam_f")
-        bet_f = keep.tile([P, UNITS, 2], F32, name="bet_f")
-        if TY_ENGINE == "s":
-            nc.vector.tensor_copy(out=gam_f[:], in_=gam[:])
-            nc.vector.tensor_scalar_mul(out=ngam_f[:], in0=gam[:], scalar1=-1.0)
-            nc.vector.tensor_copy(out=bet_f[:], in_=bet[:])
+        vec_rows = {}
+        for name in ("gamma", "beta"):
+            vec_rows[name] = keep.tile([P, UNIT_K], BF16, name="%s_rows" % name)
+            nc.vector.memset(vec_rows[name][:].bitcast(F32), 0.0)
 
         y_view = y_lin.rearrange("(r p) k -> p r k", p=P)
         w_view = W2.rearrange("(r p) k -> p r k", p=P)
+        y_first = {}
+        for c in range(2):
+            for h in range(2):
+                y_first[(c, h)] = keep.tile([P, 4, UNIT_K], BF16, name="y_first%d%d" % (c, h))
+                nc.sync.dma_start(
+                    out=y_first[(c, h)][:], in_=y_view[:, 4 * h : 4 * h + 4, c * UNIT_K : (c + 1) * UNIT_K]
+                )
+            if c == 0:
+                nc.sync.dma_start(out=vec_rows["gamma"][0:UNITS, :], in_=gamma.rearrange("(c w) -> c w", w=UNIT_K))
+                nc.sync.dma_start(out=vec_rows["beta"][0:UNITS, :], in_=beta.rearrange("(c w) -> c w", w=UNIT_K))
         y_sb = {}
         w_sb = {}
-        for which, g in LOAD_ORDER:
+        for which, g in (("y", 1), ("w", 0), ("y", 2), ("w", 1), ("y", 3), ("w", 2), ("w", 3)):
             k_cols = slice(g * K_PASS, (g + 1) * K_PASS)
-            if which == "piece":
-                c, h = divmod(g, 2)
-                y_sb[("piece", c, h)] = keep.tile([P, 4, QUARTER], BF16, name="yp%d" % g)
-                nc.sync.dma_start(
-                    out=y_sb[("piece", c, h)][:], in_=y_view[:, 4 * h : 4 * h + 4, c * QUARTER : (c + 1) * QUARTER]
-                )
-            elif which == "y":
-                y_sb[g] = keep.tile([P, RT, K_PASS], BF16, name="y%d" % g)
+            if which == "y":
+                y_sb[g] = keep.tile([P, 8, K_PASS], BF16, name="y%d" % g)
                 nc.sync.dma_start(out=y_sb[g][:], in_=y_view[:, :, k_cols])
             else:
-                w_sb[g] = keep.tile([P, NT, K_PASS], BF16, name="w%d" % g)
+                w_sb[g] = keep.tile([P, 8, K_PASS], BF16, name="w%d" % g)
                 nc.sync.dma_start(out=w_sb[g][:], in_=w_view[:, :, k_cols])
         b2_bc = keep.tile([P, N], BF16, name="b2_bc")
         nc.sync.dma_start(out=b2_bc[:], in_=b2.partition_broadcast(P))
 
+        i, gbT = take_bank()
+        nc.tensor.transpose(out=gbT[:, 0:P], in_=vec_rows["gamma"][:].bitcast(F32), identity=ident[:])
+        nc.tensor.transpose(out=gbT[:, P : 2 * P], in_=vec_rows["beta"][:].bitcast(F32), identity=ident[:])
+        gb = keep.tile([P, 2 * UNITS], F32, name="gb")
+        nc.vector.tensor_copy(
+            out=gb[:].rearrange("p (v c) -> p v c", v=2),
+            in_=gbT[:, 0 : 2 * P].rearrange("p (v w) -> p v w", v=2)[:, :, 0:UNITS],
+        )
+        give_bank(i)
+        gam = gb[:, 0:UNITS].bitcast(BF16).rearrange("p (c e) -> p c e", e=2)
+        bet = gb[:, UNITS : 2 * UNITS].bitcast(BF16).rearrange("p (c e) -> p c e", e=2)
+        gam_f = keep.tile([P, UNITS, 2], F32, name="gam_f")
+        ngam_f = keep.tile([P, UNITS, 2], F32, name="ngam_f")
+        bet_f = keep.tile([P, UNITS, 2], F32, name="bet_f")
+        nc.vector.tensor_copy(out=gam_f[:], in_=gam)
+        nc.vector.tensor_scalar_mul(out=ngam_f[:], in0=gam, scalar1=-1.0)
+        nc.vector.tensor_copy(out=bet_f[:], in_=bet)
+
         planes = {}
+        a_groups = {}
+        w_groups = {}
         for g in range(PASSES):
+            a_groups[g] = keep.tile([P, B, 4], BF16, name="ag%d" % g, align_bytes=64)
             for h in range(2):
                 planes[(g, h)] = keep.tile([P, 4, HALF], BF16, name="planes%d%d" % (g, h))
+                w_groups[(g, h)] = keep.tile([P, HALF, 4], BF16, name="wg%d%d" % (g, h), align_bytes=64)
         a_codes = keep.tile([P, PASSES, B], U32, name="a_codes", align_bytes=64)
         a_scales = keep.tile([P, PASSES, B], U8, name="a_scales", align_bytes=64)
         w_codes = keep.tile([P, PASSES, N], U32, name="w_codes", align_bytes=64)
         w_scales = keep.tile([P, PASSES, N], U8, name="w_scales", align_bytes=64)
 
         y_banks = {}
-        stats = {}
-        affine = {}
-        w_banks = {}
-        w_groups = {}
-        a_groups = {}
 
-        def transpose_unit(c, h, b):
+        def transpose_unit(c):
             g, u = divmod(c, 2)
-            if True:
-                i, yT = take_bank(b)
+            for h in range(2):
+                i, yT = take_bank()
                 for j in range(4):
-                    if ("piece", c, h) in y_sb:
-                        words = y_sb[("piece", c, h)][:, j, :].bitcast(F32)
+                    if g == 0:
+                        words = y_first[(c, h)][:, j, :].bitcast(F32)
                     else:
                         words = y_sb[g][:, 4 * h + j, :].bitcast(F32)[:, u * P : (u + 1) * P]
                     nc.tensor.transpose(out=yT[:, j * P : (j + 1) * P], in_=words, identity=ident[:])
                 y_banks[(c, h)] = (i, yT)
 
-        def stats_half(c, h):
-            if c not in stats:
-                stats[c] = small.tile([P, 4, 6], F32, name="st")
-            pairs = y_banks[(c, h)][1][:].bitcast(BF16)
-            for j in range(2):
-                nc.vector.bn_stats(out=stats[c][:, 2 * h + j, :], in_=pairs[:, j * HALF : (j + 1) * HALF])
-
-        def aggregate(c):
+        def normalise_unit(c):
+            st = small.tile([P, 4, 6], F32, name="st")
+            for h in range(2):
+                pairs = y_banks[(c, h)][1][:].bitcast(BF16)
+                for j in range(2):
+                    nc.vector.bn_stats(out=st[:, 2 * h + j, :], in_=pairs[:, j * HALF : (j + 1) * HALF])
             mv = small.tile([P, 2, 2], F32, name="mv")
             for e in range(2):
-                nc.vector.bn_aggr(out=mv[:, e, :], in_=stats[c][:, :, 3 * e : 3 * e + 3])
-            mg = small.tile([P, 2], F32, name="mg")
-            if TY_ENGINE == "v":
-                nc.vector.tensor_tensor(out=mg[:], in0=mv[:, :, 0], in1=gam[:, c, :], op=ALU.mult)
-            affine[c] = [mv, mg]
-
-        def rstd_unit(c):
+                nc.vector.bn_aggr(out=mv[:, e, :], in_=st[:, :, 3 * e : 3 * e + 3])
             rstd = small.tile([P, 2], F32, name="rstd")
             nc.scalar.activation(
-                out=rstd[:], in_=affine[c][0][:, :, 1], func=ACT.Abs_reciprocal_sqrt, bias=eps[:, 0:1], scale=1.0
+                out=rstd[:], in_=mv[:, :, 1], func=ACT.Abs_reciprocal_sqrt, bias=eps[:, 0:1], scale=1.0
             )
-            affine[c].append(rstd)
-
-        def scale_bias(c):
-            mv, mg, rstd = affine[c]
-            if TY_ENGINE == "s":
-                sc = small.tile([P, 2], F32, name="sc")
-                nsc = small.tile([P, 2], F32, name="nsc")
-                bi = small.tile([P, 2], F32, name="bi")
-                for e in range(2):
-                    col = slice(e, e + 1)
-                    nc.scalar.activation(out=nsc[:, col], in_=ngam_f[:, c, col], func=ACT.Copy, scale=rstd[:, col])
-                    nc.scalar.activation(out=sc[:, col], in_=gam_f[:, c, col], func=ACT.Copy, scale=rstd[:, col])
-                for e in range(2):
-                    col = slice(e, e + 1)
-                    nc.scalar.activation(
-                        out=bi[:, col], in_=mv[:, e, 0:1], func=ACT.Identity, scale=nsc[:, col], bias=bet_f[:, c, col]
-                    )
-                affine[c] = [sc, bi]
-                return
-            ms = small.tile([P, 2], F32, name="ms")
-            nc.vector.tensor_tensor(out=ms[:], in0=mg[:], in1=rstd[:], op=ALU.mult)
             sc = small.tile([P, 2], F32, name="sc")
-            nc.vector.tensor_tensor(out=sc[:], in0=rstd[:], in1=gam[:, c, :], op=ALU.mult)
+            nsc = small.tile([P, 2], F32, name="nsc")
             bi = small.tile([P, 2], F32, name="bi")
-            nc.vector.tensor_tensor(out=bi[:], in0=bet[:, c, :], in1=ms[:], op=ALU.subtract)
-            affine[c] = [sc, bi]
-
-        def affine_half(c, h):
-            sc, bi = affine[c]
-            i, yT = y_banks[(c, h)]
-            pairs = yT[:].bitcast(BF16).rearrange("p (b e) -> p b e", e=2)
             for e in range(2):
+                col = slice(e, e + 1)
+                nc.scalar.activation(out=nsc[:, col], in_=ngam_f[:, c, col], func=ACT.Copy, scale=rstd[:, col])
+                nc.scalar.activation(out=sc[:, col], in_=gam_f[:, c, col], func=ACT.Copy, scale=rstd[:, col])
+            for e in range(2):
+                col = slice(e, e + 1)
                 nc.scalar.activation(
-                    out=planes[(c // 2, h)][:, 2 * (c % 2) + e, :],
-                    in_=pairs[:, :, e],
-                    func=ACT.Relu,
-                    bias=bi[:, e : e + 1],
-                    scale=sc[:, e : e + 1],
+                    out=bi[:, col], in_=mv[:, e, 0:1], func=ACT.Identity, scale=nsc[:, col], bias=bet_f[:, c, col]
                 )
-            give_bank(i)
+            for h in range(2):
+                i, yT = y_banks[(c, h)]
+                pairs = yT[:].bitcast(BF16).rearrange("p (b e) -> p b e", e=2)
+                for e in range(2):
+                    nc.scalar.activation(
+                        out=planes[(c // 2, h)][:, 2 * (c % 2) + e, :],
+                        in_=pairs[:, :, e],
+                        func=ACT.Relu,
+                        bias=bi[:, e : e + 1],
+                        scale=sc[:, e : e + 1],
+                    )
+                give_bank(i)
 
-        def transpose_w(item, b):
-            g, h, q = item
-            i, wT = take_bank(b)
+        def weights_quarter(g, h, q, engine):
+            i, wT = take_bank()
             halves = wT[:].rearrange("p (u n) -> p u n", u=2)
             for j in range(2):
                 for u in range(2):
@@ -192,21 +177,12 @@ def tile_simclr_pa_kernel(tc, y_lin, gamma, beta, W2, b2, out):
                         in_=w_sb[g][:, 4 * h + 2 * q + j, :].bitcast(F32)[:, u * P : (u + 1) * P],
                         identity=ident[:],
                     )
-            w_banks[item] = (i, halves)
-
-        def exit_w(item, engine):
-            g, h, q = item
-            if (g, h) not in w_groups:
-                w_groups[(g, h)] = grp_pool.tile([P, HALF, 4], BF16, name="wg", align_bytes=64, bufs=WG_BUFS)
-            wg = w_groups[(g, h)]
-            words = wg[:].rearrange("p n t -> p (n t)").bitcast(F32).rearrange("p (n u) -> p n u", u=2)
+            words = w_groups[(g, h)][:].rearrange("p n t -> p (n t)").bitcast(F32).rearrange("p (n u) -> p n u", u=2)
             dst = words[:, q * QUARTER : (q + 1) * QUARTER, :]
-            i, halves = w_banks[item]
-            src = halves.rearrange("p u n -> p n u")
-            if engine == "v":
-                nc.vector.tensor_copy(out=dst, in_=src)
+            if engine == "vector":
+                nc.vector.tensor_copy(out=dst, in_=halves.rearrange("p u n -> p n u"))
             else:
-                nc.scalar.copy(out=dst, in_=src)
+                nc.scalar.copy(out=dst, in_=halves.rearrange("p u n -> p n u"))
             give_bank(i)
 
         def quantise_w(g, h):
@@ -217,38 +193,37 @@ def tile_simclr_pa_kernel(tc, y_lin, gamma, beta, W2, b2, out):
                 in_=w_groups[(g, h)][:].rearrange("p n t -> p (n t)"),
             )
 
-        def regroup(g, bq, engine):
-            if g not in a_groups:
-                a_groups[g] = grp_pool.tile([P, B, 4], BF16, name="ag", align_bytes=64, bufs=PASSES)
+        def regroup(g, bq):
             rows = slice(bq * QUARTER, (bq + 1) * QUARTER)
-            dst = a_groups[g][:, rows, :].rearrange("p (c i) t -> p c t i", i=4)
             part = slice((bq % 2) * QUARTER, (bq % 2 + 1) * QUARTER)
-            src = planes[(g, bq // 2)][:, :, part].rearrange("p t (c i) -> p c t i", i=4)
-            if engine == "g":
-                nc.gpsimd.tensor_scalar(out=dst, in0=src, scalar1=1.0, scalar2=0.0, op0=ALU.mult, op1=ALU.add)
-            elif engine == "s":
-                nc.scalar.copy(out=dst, in_=src)
+            src = planes[(g, bq // 2)][:, :, part]
+            dst = a_groups[g][:, rows, :]
+            if g < GPSIMD_PASSES:
+                nc.gpsimd.tensor_scalar(
+                    out=dst, in0=src.rearrange("p t b -> p b t"), scalar1=1.0, scalar2=0.0, op0=ALU.mult, op1=ALU.add
+                )
             else:
-                nc.vector.tensor_copy(out=dst, in_=src)
+                nc.vector.tensor_copy(
+                    out=dst.rearrange("p (c i) t -> p c t i", i=4), in_=src.rearrange("p t (c i) -> p c t i", i=4)
+                )
 
-        def quantise_a(g, lo, hi):
+        def quantise_a(g, h):
+            rows = slice(h * HALF, (h + 1) * HALF)
             nc.vector.quantize_mx(
-                out=a_codes[:, g, lo:hi].bitcast(FP8X4),
-                scales=a_scales[:, g, lo:hi],
-                in_=a_groups[g][:, lo:hi, :].rearrange("p b t -> p (b t)"),
+                out=a_codes[:, g, rows].bitcast(FP8X4),
+                scales=a_scales[:, g, rows],
+                in_=a_groups[g][:, rows, :].rearrange("p b t -> p (b t)"),
             )
 
         accs = {}
-        pairs_out = {}
+        pair_tiles = {}
         norms = {}
 
-        def matmul_tile(m, h, g0, g1, b):
+        def matmul_tile(m, h):
             rows = slice(m * P, (m + 1) * P)
             cols = slice(h * HALF, (h + 1) * HALF)
-            if g0 == 0:
-                accs[(m, h)] = take_bank(b)
-            i, acc = accs[(m, h)]
-            for g in range(g0, g1):
+            i, acc = take_bank()
+            for g in range(PASSES):
                 nc.tensor.matmul_mx(
                     out=acc[:],
                     lhsT=a_codes[:, g, rows].bitcast(FP8X4),
@@ -258,56 +233,71 @@ def tile_simclr_pa_kernel(tc, y_lin, gamma, beta, W2, b2, out):
                     start=(g == 0),
                     stop=(g == PASSES - 1),
                 )
+            accs[(m, h)] = (i, acc)
 
-        def result(m):
-            return pairs_out[m // 2][:, m % 2, :]
+        def rows_of(m):
+            if m // 2 not in pair_tiles:
+                pair_tiles[m // 2] = keep.tile([P, 2, N], F32, name="pb%d" % (m // 2), tag="w%d" % (m // 2))
+            return pair_tiles[m // 2][:, m % 2, :]
 
-        def add_bias(m, h):
-            if m // 2 not in pairs_out:
-                pairs_out[m // 2] = keep.tile([P, 2, N], F32, name="pb%d" % (m // 2), tag="y%d" % (m // 2))
+        def bias_and_squares(m, h):
             if m not in norms:
                 norms[m] = small.tile([P, 2], F32, name="ss")
             cols = slice(h * HALF, (h + 1) * HALF)
             i, acc = accs[(m, h)]
-            nc.vector.tensor_tensor(out=result(m)[:, cols], in0=acc[:], in1=b2_bc[:, cols], op=ALU.add)
+            nc.vector.tensor_tensor(out=rows_of(m)[:, cols], in0=acc[:], in1=b2_bc[:, cols], op=ALU.add)
+            give_bank(i)
+            sq = junk.tile([P, HALF], BF16, name="sq")
+            nc.scalar.activation(out=sq[:], in_=rows_of(m)[:, cols], func=ACT.Square, accum_out=norms[m][:, h : h + 1])
 
-        def sum_squares(m, h):
-            cols = slice(h * HALF, (h + 1) * HALF)
-            sq = outp.tile([P, HALF], BF16, name="sq")
-            nc.scalar.activation(out=sq[:], in_=result(m)[:, cols], func=ACT.Square, accum_out=norms[m][:, h : h + 1])
-
-        def clamp_norm(m):
+        def normalise_rows(m):
+            ss = norms[m]
             cl = small.tile([P, 1], F32, name="cl")
             nc.vector.tensor_scalar(
-                out=cl[:], in0=norms[m][:, 0:1], scalar1=norms[m][:, 1:2], scalar2=L2_EPS_SQ, op0=ALU.add, op1=ALU.max
+                out=cl[:], in0=ss[:, 0:1], scalar1=ss[:, 1:2], scalar2=L2_EPS_SQ, op0=ALU.add, op1=ALU.max
             )
-            norms[m] = cl
-
-        def inverse_norm(m):
             rn = small.tile([P, 1], F32, name="rn")
-            nc.scalar.activation(out=rn[:], in_=norms[m][:], func=ACT.Abs_reciprocal_sqrt)
-            norms[m] = rn
+            nc.scalar.activation(out=rn[:], in_=cl[:], func=ACT.Abs_reciprocal_sqrt)
+            pb = rows_of(m)
+            nc.scalar.activation(out=pb[:, 0:HALF], in_=pb[:, 0:HALF], func=ACT.Copy, scale=rn[:, 0:1])
+            nc.vector.tensor_scalar_mul(out=pb[:, HALF:N], in0=pb[:, HALF:N], scalar1=rn[:, 0:1])
+            nc.sync.dma_start(out=out[m * P : (m + 1) * P, :], in_=pb)
 
-        def scale_rows(m, lo, hi, engine):
-            pb = result(m)
-            rn = norms[m]
-            if engine == "s":
-                nc.scalar.activation(out=pb[:, lo:hi], in_=pb[:, lo:hi], func=ACT.Copy, scale=rn[:, 0:1])
-            elif engine == "g":
-                nc.gpsimd.tensor_scalar(
-                    out=pb[:, lo:hi], in0=pb[:, lo:hi], scalar1=rn[:, 0:1], scalar2=0.0, op0=ALU.mult, op1=ALU.add
-                )
-            else:
-                nc.vector.tensor_scalar_mul(out=pb[:, lo:hi], in0=pb[:, lo:hi], scalar1=rn[:, 0:1])
+        for c in range(3):
+            transpose_unit(c)
+        for c in range(UNITS):
+            normalise_unit(c)
+            if c + 3 < UNITS:
+                transpose_unit(c + 3)
+            g, u = divmod(c, 2)
+            if u == 1:
+                weights_quarter(g, 0, 0, "scalar")
+                weights_quarter(g, 0, 1, "vector")
+                if g < GPSIMD_PASSES:
+                    for bq in range(4):
+                        regroup(g, bq)
+        for g in range(PASSES):
+            quantise_w(g, 0)
+        for h in range(2):
+            for g in range(GPSIMD_PASSES, PASSES):
+                regroup(g, 2 * h)
+                regroup(g, 2 * h + 1)
+            for g in range(PASSES):
+                quantise_a(g, h)
+            if h == 0:
+                for g in range(PASSES):
+                    weights_quarter(g, 1, 0, "scalar")
+                    weights_quarter(g, 1, 1, "scalar")
+                    quantise_w(g, 1)
 
-        def store_rows(m, lo, hi):
-            nc.sync.dma_start(out=out[m * P : (m + 1) * P, lo:hi], in_=result(m)[:, lo:hi])
-
-        table = {
-            "T": transpose_unit, "SA": stats_half, "AG": aggregate, "R": rstd_unit, "TY": scale_bias, "AF": affine_half,
-            "WT": transpose_w, "WX": exit_w, "WQ": quantise_w, "RG": regroup, "Q": quantise_a, "MX": matmul_tile,
-            "ADD": add_bias, "SQ": sum_squares, "CL": clamp_norm, "RN": inverse_norm, "SCL": scale_rows, "ST": store_rows,
-        }
-        for n, s in enumerate(STEPS):
-            MARK[0] = n
-            table[s[0]](*s[1:])
+        tiles = [(m, 0) for m in range(4)] + [(m, 1) for m in range(4)] + [(m, h) for m in range(4, 8) for h in range(2)]
+        finished = {}
+        for n in range(len(tiles) + TILES_AHEAD):
+            if n < len(tiles):
+                matmul_tile(tiles[n][0], tiles[n][1])
+            if n >= TILES_AHEAD:
+                m, h = tiles[n - TILES_AHEAD]
+                bias_and_squares(m, h)
+                finished[m] = finished.get(m, 0) + 1
+                if finished[m] == 2:
+                    normalise_rows(m)

@@ -29,6 +29,12 @@ FLOPS = 2 * B * K * N
 
 GPSIMD_PASSES = 2
 TILES_AHEAD = 4
+W_SECOND_ENGINE = "vector"
+CHAIN_ON_GPSIMD = False
+
+
+def SCALE_ON_GPSIMD(m):
+    return m < 6
 
 
 def tile_simclr_pa_kernel(tc, y_lin, gamma, beta, W2, b2, out):
@@ -145,11 +151,15 @@ def tile_simclr_pa_kernel(tc, y_lin, gamma, beta, W2, b2, out):
             sc = small.tile([P, 2], F32, name="sc")
             nsc = small.tile([P, 2], F32, name="nsc")
             bi = small.tile([P, 2], F32, name="bi")
-            for e in range(2):
+            if CHAIN_ON_GPSIMD:
+                nc.gpsimd.tensor_tensor(out=sc[:], in0=rstd[:], in1=gam_f[:, c, :], op=ALU.mult)
+                nc.gpsimd.tensor_tensor(out=nsc[:], in0=mv[:, :, 0], in1=sc[:], op=ALU.mult)
+                nc.gpsimd.tensor_tensor(out=bi[:], in0=bet_f[:, c, :], in1=nsc[:], op=ALU.subtract)
+            for e in range(0 if CHAIN_ON_GPSIMD else 2):
                 col = slice(e, e + 1)
                 nc.scalar.activation(out=nsc[:, col], in_=ngam_f[:, c, col], func=ACT.Copy, scale=rstd[:, col])
                 nc.scalar.activation(out=sc[:, col], in_=gam_f[:, c, col], func=ACT.Copy, scale=rstd[:, col])
-            for e in range(2):
+            for e in range(0 if CHAIN_ON_GPSIMD else 2):
                 col = slice(e, e + 1)
                 nc.scalar.activation(
                     out=bi[:, col], in_=mv[:, e, 0:1], func=ACT.Identity, scale=nsc[:, col], bias=bet_f[:, c, col]
@@ -259,8 +269,11 @@ def tile_simclr_pa_kernel(tc, y_lin, gamma, beta, W2, b2, out):
             rn = small.tile([P, 1], F32, name="rn")
             nc.scalar.activation(out=rn[:], in_=cl[:], func=ACT.Abs_reciprocal_sqrt)
             pb = rows_of(m)
-            nc.scalar.activation(out=pb[:, 0:HALF], in_=pb[:, 0:HALF], func=ACT.Copy, scale=rn[:, 0:1])
-            nc.vector.tensor_scalar_mul(out=pb[:, HALF:N], in0=pb[:, HALF:N], scalar1=rn[:, 0:1])
+            if SCALE_ON_GPSIMD(m):
+                nc.gpsimd.tensor_scalar(out=pb, in0=pb, scalar1=rn[:, 0:1], scalar2=0.0, op0=ALU.mult, op1=ALU.add)
+            else:
+                nc.scalar.activation(out=pb[:, 0:HALF], in_=pb[:, 0:HALF], func=ACT.Copy, scale=rn[:, 0:1])
+                nc.vector.tensor_scalar_mul(out=pb[:, HALF:N], in0=pb[:, HALF:N], scalar1=rn[:, 0:1])
             nc.sync.dma_start(out=out[m * P : (m + 1) * P, :], in_=pb)
 
         for c in range(3):
@@ -272,7 +285,7 @@ def tile_simclr_pa_kernel(tc, y_lin, gamma, beta, W2, b2, out):
             g, u = divmod(c, 2)
             if u == 1:
                 weights_quarter(g, 0, 0, "scalar")
-                weights_quarter(g, 0, 1, "vector")
+                weights_quarter(g, 0, 1, W_SECOND_ENGINE)
                 if g < GPSIMD_PASSES:
                     for bq in range(4):
                         regroup(g, bq)

@@ -27,14 +27,14 @@ L2_EPS_SQ = 1e-24
 
 FLOPS = 2 * B * K * N
 
-GPSIMD_PASSES = 2
+GPSIMD_PASSES = 3
 TILES_AHEAD = 4
 W_SECOND_ENGINE = "vector"
 CHAIN_ON_GPSIMD = False
 
 
 def SCALE_ON_GPSIMD(m):
-    return m < 6
+    return m < 0
 
 
 def tile_simclr_pa_kernel(tc, y_lin, gamma, beta, W2, b2, out):

@@ -27,14 +27,9 @@ L2_EPS_SQ = 1e-24
 
 FLOPS = 2 * B * K * N
 
-GPSIMD_PASSES = 3
+GPSIMD_PASSES = 2
 TILES_AHEAD = 4
-W_SECOND_ENGINE = "vector"
-CHAIN_ON_GPSIMD = False
-
-
-def SCALE_ON_GPSIMD(m):
-    return m < 0
+SCALAR_COLS = 384
 
 
 def tile_simclr_pa_kernel(tc, y_lin, gamma, beta, W2, b2, out):
@@ -151,15 +146,11 @@ def tile_simclr_pa_kernel(tc, y_lin, gamma, beta, W2, b2, out):
             sc = small.tile([P, 2], F32, name="sc")
             nsc = small.tile([P, 2], F32, name="nsc")
             bi = small.tile([P, 2], F32, name="bi")
-            if CHAIN_ON_GPSIMD:
-                nc.gpsimd.tensor_tensor(out=sc[:], in0=rstd[:], in1=gam_f[:, c, :], op=ALU.mult)
-                nc.gpsimd.tensor_tensor(out=nsc[:], in0=mv[:, :, 0], in1=sc[:], op=ALU.mult)
-                nc.gpsimd.tensor_tensor(out=bi[:], in0=bet_f[:, c, :], in1=nsc[:], op=ALU.subtract)
-            for e in range(0 if CHAIN_ON_GPSIMD else 2):
+            for e in range(2):
                 col = slice(e, e + 1)
                 nc.scalar.activation(out=nsc[:, col], in_=ngam_f[:, c, col], func=ACT.Copy, scale=rstd[:, col])
                 nc.scalar.activation(out=sc[:, col], in_=gam_f[:, c, col], func=ACT.Copy, scale=rstd[:, col])
-            for e in range(0 if CHAIN_ON_GPSIMD else 2):
+            for e in range(2):
                 col = slice(e, e + 1)
                 nc.scalar.activation(
                     out=bi[:, col], in_=mv[:, e, 0:1], func=ACT.Identity, scale=nsc[:, col], bias=bet_f[:, c, col]
@@ -269,12 +260,10 @@ def tile_simclr_pa_kernel(tc, y_lin, gamma, beta, W2, b2, out):
             rn = small.tile([P, 1], F32, name="rn")
             nc.scalar.activation(out=rn[:], in_=cl[:], func=ACT.Abs_reciprocal_sqrt)
             pb = rows_of(m)
-            if SCALE_ON_GPSIMD(m):
-                nc.gpsimd.tensor_scalar(out=pb, in0=pb, scalar1=rn[:, 0:1], scalar2=0.0, op0=ALU.mult, op1=ALU.add)
-            else:
-                nc.scalar.activation(out=pb[:, 0:HALF], in_=pb[:, 0:HALF], func=ACT.Copy, scale=rn[:, 0:1])
-                nc.vector.tensor_scalar_mul(out=pb[:, HALF:N], in0=pb[:, HALF:N], scalar1=rn[:, 0:1])
-            nc.sync.dma_start(out=out[m * P : (m + 1) * P, :], in_=pb)
+            nc.vector.tensor_scalar_mul(out=pb[:, SCALAR_COLS:N], in0=pb[:, SCALAR_COLS:N], scalar1=rn[:, 0:1])
+            nc.sync.dma_start(out=out[m * P : (m + 1) * P, SCALAR_COLS:N], in_=pb[:, SCALAR_COLS:N])
+            nc.scalar.activation(out=pb[:, 0:SCALAR_COLS], in_=pb[:, 0:SCALAR_COLS], func=ACT.Copy, scale=rn[:, 0:1])
+            nc.sync.dma_start(out=out[m * P : (m + 1) * P, 0:SCALAR_COLS], in_=pb[:, 0:SCALAR_COLS])
 
         for c in range(3):
             transpose_unit(c)
@@ -285,7 +274,7 @@ def tile_simclr_pa_kernel(tc, y_lin, gamma, beta, W2, b2, out):
             g, u = divmod(c, 2)
             if u == 1:
                 weights_quarter(g, 0, 0, "scalar")
-                weights_quarter(g, 0, 1, W_SECOND_ENGINE)
+                weights_quarter(g, 0, 1, "vector")
                 if g < GPSIMD_PASSES:
                     for bq in range(4):
                         regroup(g, bq)

@@ -27,9 +27,7 @@ L2_EPS_SQ = 1e-24
 
 FLOPS = 2 * B * K * N
 
-GPSIMD_PASSES = 2
-TILES_AHEAD = 4
-SCALAR_COLS = 384
+SPLIT = (("scalar", 384), ("vector", 640))
 
 
 def tile_simclr_pa_kernel(tc, y_lin, gamma, beta, W2, b2, out):
@@ -39,6 +37,7 @@ def tile_simclr_pa_kernel(tc, y_lin, gamma, beta, W2, b2, out):
         small = ctx.enter_context(tc.tile_pool(name="small", bufs=UNITS))
         junk = ctx.enter_context(tc.tile_pool(name="junk", bufs=2))
         psum = ctx.enter_context(tc.psum_pool(name="psum", bufs=1))
+        ctx.enter_context(tc.manual_schedule())
 
         free_banks = list(range(BANKS))
         taken = [0]
@@ -53,6 +52,8 @@ def tile_simclr_pa_kernel(tc, y_lin, gamma, beta, W2, b2, out):
 
         ident = keep.tile([P, P], F32, name="ident")
         make_identity(nc, ident[:])
+        ones = keep.tile([P, 1], BF16, name="ones")
+        nc.vector.memset(ones[:], 1.0)
         eps = keep.tile([P, 1], F32, name="eps")
         nc.vector.memset(eps[:], BN_EPS)
         vec_rows = {}
@@ -73,233 +74,455 @@ def tile_simclr_pa_kernel(tc, y_lin, gamma, beta, W2, b2, out):
                 nc.sync.dma_start(out=vec_rows["gamma"][0:UNITS, :], in_=gamma.rearrange("(c w) -> c w", w=UNIT_K))
                 nc.sync.dma_start(out=vec_rows["beta"][0:UNITS, :], in_=beta.rearrange("(c w) -> c w", w=UNIT_K))
         y_sb = {}
+        for g in range(1, PASSES):
+            y_sb[g] = keep.tile([P, 8, K_PASS], BF16, name="y%d" % g)
+            nc.sync.dma_start(out=y_sb[g][:], in_=y_view[:, :, g * K_PASS : (g + 1) * K_PASS])
         w_sb = {}
-        for which, g in (("y", 1), ("w", 0), ("y", 2), ("w", 1), ("y", 3), ("w", 2), ("w", 3)):
-            k_cols = slice(g * K_PASS, (g + 1) * K_PASS)
-            if which == "y":
-                y_sb[g] = keep.tile([P, 8, K_PASS], BF16, name="y%d" % g)
-                nc.sync.dma_start(out=y_sb[g][:], in_=y_view[:, :, k_cols])
-            else:
-                w_sb[g] = keep.tile([P, 8, K_PASS], BF16, name="w%d" % g)
-                nc.sync.dma_start(out=w_sb[g][:], in_=w_view[:, :, k_cols])
+        for r in range(0, 8, 2):
+            w_sb[r // 2] = keep.tile([P, 2, K], BF16, name="w%d" % (r // 2))
+            nc.sync.dma_start(out=w_sb[r // 2][:], in_=w_view[:, r : r + 2, :])
         b2_bc = keep.tile([P, N], BF16, name="b2_bc")
         nc.sync.dma_start(out=b2_bc[:], in_=b2.partition_broadcast(P))
 
-        i, gbT = take_bank()
-        nc.tensor.transpose(out=gbT[:, 0:P], in_=vec_rows["gamma"][:].bitcast(F32), identity=ident[:])
-        nc.tensor.transpose(out=gbT[:, P : 2 * P], in_=vec_rows["beta"][:].bitcast(F32), identity=ident[:])
-        gb = keep.tile([P, 2 * UNITS], F32, name="gb")
-        nc.vector.tensor_copy(
-            out=gb[:].rearrange("p (v c) -> p v c", v=2),
-            in_=gbT[:, 0 : 2 * P].rearrange("p (v w) -> p v w", v=2)[:, :, 0:UNITS],
-        )
-        give_bank(i)
-        gam = gb[:, 0:UNITS].bitcast(BF16).rearrange("p (c e) -> p c e", e=2)
-        bet = gb[:, UNITS : 2 * UNITS].bitcast(BF16).rearrange("p (c e) -> p c e", e=2)
-        gam_f = keep.tile([P, UNITS, 2], F32, name="gam_f")
-        ngam_f = keep.tile([P, UNITS, 2], F32, name="ngam_f")
-        bet_f = keep.tile([P, UNITS, 2], F32, name="bet_f")
-        nc.vector.tensor_copy(out=gam_f[:], in_=gam)
-        nc.vector.tensor_scalar_mul(out=ngam_f[:], in0=gam, scalar1=-1.0)
-        nc.vector.tensor_copy(out=bet_f[:], in_=bet)
+        gam_f = keep.tile([P, 2 * UNITS], F32, name="gam_f")
+        bet_f = keep.tile([P, 2 * UNITS], F32, name="bet_f")
+
+        def gamma_beta():
+            i, gbT = take_bank()
+            nc.tensor.transpose(out=gbT[:, 0:P], in_=vec_rows["gamma"][:].bitcast(F32), identity=ident[:])
+            nc.tensor.transpose(out=gbT[:, P : 2 * P], in_=vec_rows["beta"][:].bitcast(F32), identity=ident[:])
+            pairs = gbT[:].bitcast(BF16)
+            nc.vector.tensor_copy(
+                out=gam_f[:], in_=pairs[:, 0 : 2 * UNITS]
+            )
+            nc.vector.tensor_copy(
+                out=bet_f[:], in_=pairs[:, 2 * P : 2 * P + 2 * UNITS]
+            )
+            give_bank(i)
 
         planes = {}
         a_groups = {}
         w_groups = {}
-        for g in range(PASSES):
-            a_groups[g] = keep.tile([P, B, 4], BF16, name="ag%d" % g, align_bytes=64)
-            for h in range(2):
+        for h in range(2):
+            a_all = keep.tile([P, PASSES, HALF, 4], BF16, name="ag%d" % h, align_bytes=64)
+            w_all = keep.tile([P, PASSES, HALF, 4], BF16, name="wg%d" % h, align_bytes=64)
+            for g in range(PASSES):
+                a_groups[(g, h)] = a_all[:, g]
+                w_groups[(g, h)] = w_all[:, g]
                 planes[(g, h)] = keep.tile([P, 4, HALF], BF16, name="planes%d%d" % (g, h))
-                w_groups[(g, h)] = keep.tile([P, HALF, 4], BF16, name="wg%d%d" % (g, h), align_bytes=64)
-        a_codes = keep.tile([P, PASSES, B], U32, name="a_codes", align_bytes=64)
-        a_scales = keep.tile([P, PASSES, B], U8, name="a_scales", align_bytes=64)
-        w_codes = keep.tile([P, PASSES, N], U32, name="w_codes", align_bytes=64)
-        w_scales = keep.tile([P, PASSES, N], U8, name="w_scales", align_bytes=64)
+            a_groups[h], w_groups[h] = a_all, w_all
+        a_codes = keep.tile([P, 2, PASSES, HALF], U32, name="a_codes", align_bytes=64)
+        a_scales = keep.tile([P, 2, PASSES, HALF], U8, name="a_scales", align_bytes=64)
+        w_codes = keep.tile([P, 2, PASSES, HALF], U32, name="w_codes", align_bytes=64)
+        w_scales = keep.tile([P, 2, PASSES, HALF], U8, name="w_scales", align_bytes=64)
 
         y_banks = {}
+        gram_banks = {}
+        factors = {}
 
-        def transpose_unit(c):
+        def y_words(c, r):
             g, u = divmod(c, 2)
-            for h in range(2):
-                i, yT = take_bank()
-                for j in range(4):
-                    if g == 0:
-                        words = y_first[(c, h)][:, j, :].bitcast(F32)
-                    else:
-                        words = y_sb[g][:, 4 * h + j, :].bitcast(F32)[:, u * P : (u + 1) * P]
-                    nc.tensor.transpose(out=yT[:, j * P : (j + 1) * P], in_=words, identity=ident[:])
-                y_banks[(c, h)] = (i, yT)
+            if g == 0:
+                return y_first[(c, r // 4)][:, r % 4, :].bitcast(F32)
+            return y_sb[g][:, r, :].bitcast(F32)[:, u * P : (u + 1) * P]
 
-        def normalise_unit(c):
-            st = small.tile([P, 4, 6], F32, name="st")
-            for h in range(2):
-                pairs = y_banks[(c, h)][1][:].bitcast(BF16)
-                for j in range(2):
-                    nc.vector.bn_stats(out=st[:, 2 * h + j, :], in_=pairs[:, j * HALF : (j + 1) * HALF])
+        def transpose_half(c, h):
+            i, yT = take_bank()
+            for j in range(4):
+                nc.tensor.transpose(out=yT[:, j * P : (j + 1) * P], in_=y_words(c, 4 * h + j), identity=ident[:])
+            y_banks[(c, h)] = (i, yT)
+
+        def gram(g, u):
+            i, gr = take_bank()
+            for e in range(2):
+                for r in range(8):
+                    cols = y_sb[g][:, r, u * UNIT_K + e : (u + 1) * UNIT_K : 2]
+                    nc.tensor.matmul(
+                        out=gr[:, e * P : (e + 1) * P], lhsT=cols, rhs=cols, start=(r == 0), stop=(r == 7)
+                    )
+            gram_banks[(g, u)] = (i, gr)
+
+        def sums(g):
+            i, gr = gram_banks[(g, 1)]
+            for u in range(2):
+                for e in range(2):
+                    at = 2 * P + 2 * u + e
+                    for r in range(8):
+                        cols = y_sb[g][:, r, u * UNIT_K + e : (u + 1) * UNIT_K : 2]
+                        nc.tensor.matmul(
+                            out=gr[:, at : at + 1], lhsT=cols, rhs=ones[:], start=(r == 0), stop=(r == 7)
+                        )
+
+        moments = {}
+
+        def moments_from_gram(g):
+            sm = gram_banks[(g, 1)][1][:, 2 * P : 2 * P + 4]
+            mean = small.tile([P, 4], F32, name="mean")
+            var = small.tile([P, 4], F32, name="var")
+            m2 = small.tile([P, 4], F32, name="m2")
+            for u in range(2):
+                gr = gram_banks[(g, u)][1]
+                for e in range(2):
+                    dg = junk.tile([P, P], BF16, name="dg")
+                    nc.vector.scalar_tensor_tensor(
+                        out=dg[:],
+                        in0=gr[:, e * P : (e + 1) * P],
+                        scalar=1.0 / B,
+                        in1=ident[:],
+                        op0=ALU.mult,
+                        op1=ALU.mult,
+                        accum_out=var[:, 2 * u + e : 2 * u + e + 1],
+                    )
+                if u == 0:
+                    give_bank(gram_banks[(g, u)][0])
+            nc.vector.tensor_scalar_mul(out=mean[:], in0=sm, scalar1=1.0 / B)
+            give_bank(gram_banks[(g, 1)][0])
+            nc.vector.tensor_tensor(out=m2[:], in0=mean[:], in1=mean[:], op=ALU.mult)
+            nc.vector.tensor_tensor(out=var[:], in0=var[:], in1=m2[:], op=ALU.subtract)
+            nc.vector.tensor_scalar_max(out=var[:], in0=var[:], scalar1=0.0)
+            moments[2 * g] = (mean[:], var[:], 4)
+
+        stats = {}
+
+        def stats_half(c, h):
+            if h == 0:
+                stats[c] = small.tile([P, 4, 6], F32, name="st")
+            pairs = y_banks[(c, h)][1][:].bitcast(BF16)
+            for j in range(2):
+                nc.vector.bn_stats(out=stats[c][:, 2 * h + j, :], in_=pairs[:, j * HALF : (j + 1) * HALF])
+
+        def moments_from_stats(c):
+            st = stats[c]
             mv = small.tile([P, 2, 2], F32, name="mv")
             for e in range(2):
                 nc.vector.bn_aggr(out=mv[:, e, :], in_=st[:, :, 3 * e : 3 * e + 3])
-            rstd = small.tile([P, 2], F32, name="rstd")
-            nc.scalar.activation(
-                out=rstd[:], in_=mv[:, :, 1], func=ACT.Abs_reciprocal_sqrt, bias=eps[:, 0:1], scale=1.0
-            )
-            sc = small.tile([P, 2], F32, name="sc")
-            nsc = small.tile([P, 2], F32, name="nsc")
-            bi = small.tile([P, 2], F32, name="bi")
-            for e in range(2):
-                col = slice(e, e + 1)
-                nc.scalar.activation(out=nsc[:, col], in_=ngam_f[:, c, col], func=ACT.Copy, scale=rstd[:, col])
-                nc.scalar.activation(out=sc[:, col], in_=gam_f[:, c, col], func=ACT.Copy, scale=rstd[:, col])
-            for e in range(2):
-                col = slice(e, e + 1)
-                nc.scalar.activation(
-                    out=bi[:, col], in_=mv[:, e, 0:1], func=ACT.Identity, scale=nsc[:, col], bias=bet_f[:, c, col]
-                )
-            for h in range(2):
-                i, yT = y_banks[(c, h)]
-                pairs = yT[:].bitcast(BF16).rearrange("p (b e) -> p b e", e=2)
-                for e in range(2):
-                    nc.scalar.activation(
-                        out=planes[(c // 2, h)][:, 2 * (c % 2) + e, :],
-                        in_=pairs[:, :, e],
-                        func=ACT.Relu,
-                        bias=bi[:, e : e + 1],
-                        scale=sc[:, e : e + 1],
-                    )
-                give_bank(i)
+            moments[c] = (mv[:, :, 0], mv[:, :, 1], 2)
 
-        def weights_quarter(g, h, q, engine):
+        rstds = {}
+
+        def rstd_of(c):
+            mean, var, n = moments[c]
+            rstds[c] = small.tile([P, n], F32, name="rstd%d" % n)
+            nc.scalar.activation(out=rstds[c][:], in_=var, func=ACT.Abs_reciprocal_sqrt, bias=eps[:, 0:1], scale=1.0)
+
+        def factors_of(c):
+            mean, var, n = moments[c]
+            sc = small.tile([P, n], F32, name="sc%d" % n)
+            ms = small.tile([P, n], F32, name="ms%d" % n)
+            bi = small.tile([P, n], F32, name="bi%d" % n)
+            nc.vector.tensor_tensor(out=sc[:], in0=rstds[c][:], in1=gam_f[:, 2 * c : 2 * c + n], op=ALU.mult)
+            nc.vector.tensor_tensor(out=ms[:], in0=mean, in1=sc[:], op=ALU.mult)
+            nc.vector.tensor_tensor(out=bi[:], in0=bet_f[:, 2 * c : 2 * c + n], in1=ms[:], op=ALU.subtract)
+            for j in range(n // 2):
+                factors[c + j] = (sc[:, 2 * j : 2 * j + 2], bi[:, 2 * j : 2 * j + 2])
+
+        def affine(c, h):
+            sc, bi = factors[c]
+            i, yT = y_banks[(c, h)]
+            pairs = yT[:].bitcast(BF16).rearrange("p (b e) -> p b e", e=2)
+            for e in range(2):
+                nc.scalar.activation(
+                    out=planes[(c // 2, h)][:, 2 * (c % 2) + e, :],
+                    in_=pairs[:, :, e],
+                    func=ACT.Relu,
+                    bias=bi[:, e : e + 1],
+                    scale=sc[:, e : e + 1],
+                )
+            give_bank(i)
+
+        w_banks = {}
+
+        def weights_transpose(g, q):
             i, wT = take_bank()
             halves = wT[:].rearrange("p (u n) -> p u n", u=2)
             for j in range(2):
                 for u in range(2):
+                    w0 = g * 2 * P + u * P
                     nc.tensor.transpose(
                         out=halves[:, u, j * P : (j + 1) * P],
-                        in_=w_sb[g][:, 4 * h + 2 * q + j, :].bitcast(F32)[:, u * P : (u + 1) * P],
+                        in_=w_sb[q][:, j, :].bitcast(F32)[:, w0 : w0 + P],
                         identity=ident[:],
                     )
-            words = w_groups[(g, h)][:].rearrange("p n t -> p (n t)").bitcast(F32).rearrange("p (n u) -> p n u", u=2)
-            dst = words[:, q * QUARTER : (q + 1) * QUARTER, :]
+            w_banks[(g, q)] = (i, halves)
+
+        def weights_exit(g, q, engine):
+            i, halves = w_banks[(g, q)]
+            words = (
+                w_groups[(g, q // 2)].rearrange("p n t -> p (n t)").bitcast(F32).rearrange("p (n u) -> p n u", u=2)
+            )
+            dst = words[:, (q % 2) * QUARTER : (q % 2 + 1) * QUARTER, :]
             if engine == "vector":
                 nc.vector.tensor_copy(out=dst, in_=halves.rearrange("p u n -> p n u"))
             else:
                 nc.scalar.copy(out=dst, in_=halves.rearrange("p u n -> p n u"))
             give_bank(i)
 
-        def quantise_w(g, h):
-            cols = slice(h * HALF, (h + 1) * HALF)
+        def quantise(groups, codes, scales, h, g, n):
+            part = slice(g, g + n)
             nc.vector.quantize_mx(
-                out=w_codes[:, g, cols].bitcast(FP8X4),
-                scales=w_scales[:, g, cols],
-                in_=w_groups[(g, h)][:].rearrange("p n t -> p (n t)"),
+                out=codes[:, h, part, :].rearrange("p g n -> p (g n)").bitcast(FP8X4),
+                scales=scales[:, h, part, :].rearrange("p g n -> p (g n)"),
+                in_=groups[h][:, part].rearrange("p g n t -> p (g n t)"),
             )
 
-        def regroup(g, bq):
-            rows = slice(bq * QUARTER, (bq + 1) * QUARTER)
-            part = slice((bq % 2) * QUARTER, (bq % 2 + 1) * QUARTER)
-            src = planes[(g, bq // 2)][:, :, part]
-            dst = a_groups[g][:, rows, :]
-            if g < GPSIMD_PASSES:
-                nc.gpsimd.tensor_scalar(
-                    out=dst, in0=src.rearrange("p t b -> p b t"), scalar1=1.0, scalar2=0.0, op0=ALU.mult, op1=ALU.add
-                )
+        def quantise_w(h, g, n):
+            quantise(w_groups, w_codes, w_scales, h, g, n)
+
+        def quantise_a(h, g, n):
+            quantise(a_groups, a_codes, a_scales, h, g, n)
+
+        def regroup(g, h, engine):
+            src, dst = planes[(g, h)], a_groups[(g, h)]
+            if engine == "gpsimd":
+                for s in range(2):
+                    part = slice(s * QUARTER, (s + 1) * QUARTER)
+                    nc.gpsimd.tensor_scalar(
+                        out=dst[:, part, :],
+                        in0=src[:, :, part].rearrange("p t b -> p b t"),
+                        scalar1=1.0,
+                        scalar2=0.0,
+                        op0=ALU.mult,
+                        op1=ALU.add,
+                    )
             else:
                 nc.vector.tensor_copy(
-                    out=dst.rearrange("p (c i) t -> p c t i", i=4), in_=src.rearrange("p t (c i) -> p c t i", i=4)
+                    out=dst.rearrange("p (c i) t -> p c t i", i=4), in_=src[:].rearrange("p t (c i) -> p c t i", i=4)
                 )
-
-        def quantise_a(g, h):
-            rows = slice(h * HALF, (h + 1) * HALF)
-            nc.vector.quantize_mx(
-                out=a_codes[:, g, rows].bitcast(FP8X4),
-                scales=a_scales[:, g, rows],
-                in_=a_groups[g][:, rows, :].rearrange("p b t -> p (b t)"),
-            )
 
         accs = {}
-        pair_tiles = {}
+        p_tiles = {}
         norms = {}
 
+        def open_tile(m, h):
+            accs[(m, h)] = take_bank()
+
+        def matmul_pass(m, h, g):
+            rows = slice((m % 4) * P, (m % 4 + 1) * P)
+            nc.tensor.matmul_mx(
+                out=accs[(m, h)][1][:],
+                lhsT=a_codes[:, m // 4, g, rows].bitcast(FP8X4),
+                lhsT_scale=a_scales[:, m // 4, g, rows],
+                rhs=w_codes[:, h, g, :].bitcast(FP8X4),
+                rhs_scale=w_scales[:, h, g, :],
+                start=(g == 0),
+                stop=(g == PASSES - 1),
+            )
+
         def matmul_tile(m, h):
-            rows = slice(m * P, (m + 1) * P)
-            cols = slice(h * HALF, (h + 1) * HALF)
-            i, acc = take_bank()
+            open_tile(m, h)
             for g in range(PASSES):
-                nc.tensor.matmul_mx(
-                    out=acc[:],
-                    lhsT=a_codes[:, g, rows].bitcast(FP8X4),
-                    lhsT_scale=a_scales[:, g, rows],
-                    rhs=w_codes[:, g, cols].bitcast(FP8X4),
-                    rhs_scale=w_scales[:, g, cols],
-                    start=(g == 0),
-                    stop=(g == PASSES - 1),
-                )
-            accs[(m, h)] = (i, acc)
+                matmul_pass(m, h, g)
 
-        def rows_of(m):
-            if m // 2 not in pair_tiles:
-                pair_tiles[m // 2] = keep.tile([P, 2, N], F32, name="pb%d" % (m // 2), tag="w%d" % (m // 2))
-            return pair_tiles[m // 2][:, m % 2, :]
-
-        def bias_and_squares(m, h):
+        def add_bias(m, h):
             if m not in norms:
                 norms[m] = small.tile([P, 2], F32, name="ss")
+                if m % 2 == 0:
+                    pair = keep.tile([P, 2, N], F32, name="p%d" % (m // 2), tag="w%d" % (m // 2))
+                    p_tiles[m], p_tiles[m + 1] = pair[:, 0, :], pair[:, 1, :]
             cols = slice(h * HALF, (h + 1) * HALF)
             i, acc = accs[(m, h)]
-            nc.vector.tensor_tensor(out=rows_of(m)[:, cols], in0=acc[:], in1=b2_bc[:, cols], op=ALU.add)
+            nc.vector.tensor_tensor(out=p_tiles[m][:, cols], in0=acc[:], in1=b2_bc[:, cols], op=ALU.add)
             give_bank(i)
-            sq = junk.tile([P, HALF], BF16, name="sq")
-            nc.scalar.activation(out=sq[:], in_=rows_of(m)[:, cols], func=ACT.Square, accum_out=norms[m][:, h : h + 1])
 
-        def normalise_rows(m):
+        def square(m, h):
+            cols = slice(h * HALF, (h + 1) * HALF)
+            sq = junk.tile([P, HALF], BF16, name="sq")
+            nc.scalar.activation(out=sq[:], in_=p_tiles[m][:, cols], func=ACT.Square, accum_out=norms[m][:, h : h + 1])
+
+        inverse = {}
+
+        def inverse_norm(m):
             ss = norms[m]
             cl = small.tile([P, 1], F32, name="cl")
             nc.vector.tensor_scalar(
                 out=cl[:], in0=ss[:, 0:1], scalar1=ss[:, 1:2], scalar2=L2_EPS_SQ, op0=ALU.add, op1=ALU.max
             )
-            rn = small.tile([P, 1], F32, name="rn")
-            nc.scalar.activation(out=rn[:], in_=cl[:], func=ACT.Abs_reciprocal_sqrt)
-            pb = rows_of(m)
-            nc.vector.tensor_scalar_mul(out=pb[:, SCALAR_COLS:N], in0=pb[:, SCALAR_COLS:N], scalar1=rn[:, 0:1])
-            nc.sync.dma_start(out=out[m * P : (m + 1) * P, SCALAR_COLS:N], in_=pb[:, SCALAR_COLS:N])
-            nc.scalar.activation(out=pb[:, 0:SCALAR_COLS], in_=pb[:, 0:SCALAR_COLS], func=ACT.Copy, scale=rn[:, 0:1])
-            nc.sync.dma_start(out=out[m * P : (m + 1) * P, 0:SCALAR_COLS], in_=pb[:, 0:SCALAR_COLS])
+            inverse[m] = small.tile([P, 1], F32, name="rn")
+            nc.scalar.activation(out=inverse[m][:], in_=cl[:], func=ACT.Abs_reciprocal_sqrt)
 
-        for c in range(3):
-            transpose_unit(c)
-        for c in range(UNITS):
-            normalise_unit(c)
-            if c + 3 < UNITS:
-                transpose_unit(c + 3)
-            g, u = divmod(c, 2)
-            if u == 1:
-                weights_quarter(g, 0, 0, "scalar")
-                weights_quarter(g, 0, 1, "vector")
-                if g < GPSIMD_PASSES:
-                    for bq in range(4):
-                        regroup(g, bq)
-        for g in range(PASSES):
-            quantise_w(g, 0)
-        for h in range(2):
-            for g in range(GPSIMD_PASSES, PASSES):
-                regroup(g, 2 * h)
-                regroup(g, 2 * h + 1)
-            for g in range(PASSES):
-                quantise_a(g, h)
-            if h == 0:
-                for g in range(PASSES):
-                    weights_quarter(g, 1, 0, "scalar")
-                    weights_quarter(g, 1, 1, "scalar")
-                    quantise_w(g, 1)
+        def scale_rows(m, shares):
+            pb, rn = p_tiles[m], inverse[m][:, 0:1]
+            start = 0
+            for engine, width in shares:
+                cols = slice(start, start + width)
+                start += width
+                if engine == "scalar":
+                    nc.scalar.activation(out=pb[:, cols], in_=pb[:, cols], func=ACT.Copy, scale=rn)
+                elif engine == "vector":
+                    nc.vector.tensor_scalar_mul(out=pb[:, cols], in0=pb[:, cols], scalar1=rn)
+                else:
+                    nc.gpsimd.tensor_scalar(
+                        out=pb[:, cols], in0=pb[:, cols], scalar1=rn, scalar2=0.0, op0=ALU.mult, op1=ALU.add
+                    )
+                nc.sync.dma_start(out=out[m * P : (m + 1) * P, cols], in_=pb[:, cols])
 
-        tiles = [(m, 0) for m in range(4)] + [(m, 1) for m in range(4)] + [(m, h) for m in range(4, 8) for h in range(2)]
-        finished = {}
-        for n in range(len(tiles) + TILES_AHEAD):
-            if n < len(tiles):
+        transpose_half(0, 0)
+        transpose_half(0, 1)
+        stats_half(0, 0)
+        stats_half(0, 1)
+        transpose_half(1, 0)
+        transpose_half(1, 1)
+        gamma_beta()
+        moments_from_stats(0)
+        rstd_of(0)
+        factors_of(0)
+        affine(0, 0)
+        affine(0, 1)
+        gram(1, 0)
+        gram(1, 1)
+        sums(1)
+        stats_half(1, 0)
+        stats_half(1, 1)
+        moments_from_stats(1)
+        rstd_of(1)
+        factors_of(1)
+        affine(1, 0)
+        transpose_half(2, 0)
+        transpose_half(3, 0)
+        moments_from_gram(1)
+        rstd_of(2)
+        affine(1, 1)
+        regroup(0, 0, "vector")
+        factors_of(2)
+        affine(2, 0)
+        affine(3, 0)
+        gram(2, 0)
+        gram(2, 1)
+        sums(2)
+        transpose_half(2, 1)
+        transpose_half(3, 1)
+        regroup(0, 1, "vector")
+        quantise_a(0, 0, 1)
+        moments_from_gram(2)
+        affine(2, 1)
+        rstd_of(4)
+        factors_of(4)
+        gram(3, 0)
+        gram(3, 1)
+        sums(3)
+        transpose_half(4, 0)
+        transpose_half(5, 0)
+        affine(4, 0)
+        regroup(1, 0, "vector")
+        quantise_a(0, 1, 1)
+        affine(5, 0)
+        moments_from_gram(3)
+        rstd_of(6)
+        weights_transpose(0, 0)
+        weights_transpose(1, 0)
+        weights_exit(0, 0, "vector")
+        transpose_half(6, 0)
+        transpose_half(7, 0)
+        factors_of(6)
+        affine(6, 0)
+        weights_exit(1, 0, "vector")
+        weights_transpose(2, 0)
+        weights_transpose(3, 0)
+        affine(7, 0)
+        weights_exit(2, 0, "vector")
+        weights_exit(3, 0, "vector")
+        weights_transpose(0, 1)
+        weights_transpose(1, 1)
+        weights_exit(0, 1, "scalar")
+        weights_exit(1, 1, "scalar")
+        regroup(2, 0, "vector")
+        weights_transpose(2, 1)
+        weights_transpose(3, 1)
+        weights_exit(2, 1, "scalar")
+        weights_exit(3, 1, "scalar")
+        quantise_a(0, 2, 1)
+        quantise_w(0, 0, 2)
+        affine(3, 1)
+        regroup(3, 0, "vector")
+        weights_transpose(0, 2)
+        weights_transpose(1, 2)
+        weights_exit(0, 2, "scalar")
+        weights_exit(1, 2, "scalar")
+        quantise_w(0, 2, 2)
+        weights_transpose(2, 2)
+        weights_transpose(3, 2)
+        weights_exit(2, 2, "scalar")
+        weights_exit(3, 2, "scalar")
+        quantise_a(0, 3, 1)
+        regroup(1, 1, "vector")
+        weights_transpose(0, 3)
+        weights_transpose(1, 3)
+        weights_exit(0, 3, "scalar")
+        weights_exit(1, 3, "scalar")
+        transpose_half(4, 1)
+        transpose_half(5, 1)
+        affine(4, 1)
+        affine(5, 1)
+        weights_transpose(2, 3)
+        weights_transpose(3, 3)
+        weights_exit(2, 3, "vector")
+        weights_exit(3, 3, "vector")
+        transpose_half(6, 1)
+        transpose_half(7, 1)
+        affine(6, 1)
+        affine(7, 1)
+        open_tile(0, 0)
+        matmul_pass(0, 0, 0)
+        matmul_pass(0, 0, 1)
+        matmul_pass(0, 0, 2)
+        matmul_pass(0, 0, 3)
+        open_tile(1, 0)
+        matmul_pass(1, 0, 0)
+        matmul_pass(1, 0, 1)
+        matmul_pass(1, 0, 2)
+        matmul_pass(1, 0, 3)
+        open_tile(2, 0)
+        matmul_pass(2, 0, 0)
+        matmul_pass(2, 0, 1)
+        matmul_pass(2, 0, 2)
+        matmul_pass(2, 0, 3)
+        open_tile(3, 0)
+        matmul_pass(3, 0, 0)
+        matmul_pass(3, 0, 1)
+        matmul_pass(3, 0, 2)
+        matmul_pass(3, 0, 3)
+        quantise_w(1, 0, 2)
+        open_tile(0, 1)
+        matmul_pass(0, 1, 0)
+        matmul_pass(0, 1, 1)
+        quantise_w(1, 2, 2)
+        matmul_pass(0, 1, 2)
+        matmul_pass(0, 1, 3)
+        open_tile(1, 1)
+        matmul_pass(1, 1, 0)
+        matmul_pass(1, 1, 1)
+        matmul_pass(1, 1, 2)
+        matmul_pass(1, 1, 3)
+        regroup(2, 1, "vector")
+        add_bias(0, 0)
+        square(0, 0)
+        quantise_a(1, 0, 2)
+        open_tile(2, 1)
+        matmul_pass(2, 1, 0)
+        matmul_pass(2, 1, 1)
+        matmul_pass(2, 1, 2)
+        matmul_pass(2, 1, 3)
+        open_tile(3, 1)
+        matmul_pass(3, 1, 0)
+        matmul_pass(3, 1, 1)
+        matmul_pass(3, 1, 2)
+        matmul_pass(3, 1, 3)
+        add_bias(1, 0)
+        square(1, 0)
+        regroup(3, 1, "vector")
+        add_bias(2, 0)
+        square(2, 0)
+        quantise_a(1, 2, 2)
+        add_bias(3, 0)
+        square(3, 0)
+        tiles = [(m, 1) for m in range(4)] + [(m, h) for m in range(4, 8) for h in range(2)]
+        for n in range(len(tiles) + 3):
+            if 4 <= n < len(tiles):
                 matmul_tile(tiles[n][0], tiles[n][1])
-            if n >= TILES_AHEAD:
-                m, h = tiles[n - TILES_AHEAD]
-                bias_and_squares(m, h)
-                finished[m] = finished.get(m, 0) + 1
-                if finished[m] == 2:
-                    normalise_rows(m)
+            if n < len(tiles):
+                add_bias(tiles[n][0], tiles[n][1])
+                square(tiles[n][0], tiles[n][1])
+            if 1 <= n < len(tiles) + 1 and tiles[n - 1][1] == 1:
+                inverse_norm(tiles[n - 1][0])
+            if 2 <= n < len(tiles) + 2 and tiles[n - 2][1] == 1:
+                scale_rows(tiles[n - 2][0], SPLIT)

@@ -10,6 +10,7 @@ U8 = mybir.dt.uint8
 FP8X4 = mybir.dt.float8_e4m3fn_x4
 ACT = mybir.ActivationFunctionType
 ALU = mybir.AluOpType
+AXIS = mybir.AxisListType
 
 P = 128
 B = 1024
@@ -28,6 +29,7 @@ L2_EPS_SQ = 1e-24
 FLOPS = 2 * B * K * N
 
 SPLIT = (("scalar", 384), ("vector", 640))
+GPSIMD = (("gpsimd", 512), ("gpsimd", 512))
 
 
 def tile_simclr_pa_kernel(tc, y_lin, gamma, beta, W2, b2, out):
@@ -87,18 +89,16 @@ def tile_simclr_pa_kernel(tc, y_lin, gamma, beta, W2, b2, out):
         gam_f = keep.tile([P, 2 * UNITS], F32, name="gam_f")
         bet_f = keep.tile([P, 2 * UNITS], F32, name="bet_f")
 
+        misc = {}
+
         def gamma_beta():
-            i, gbT = take_bank()
+            misc["bank"], misc["tile"] = take_bank()
+            gbT = misc["tile"]
             nc.tensor.transpose(out=gbT[:, 0:P], in_=vec_rows["gamma"][:].bitcast(F32), identity=ident[:])
             nc.tensor.transpose(out=gbT[:, P : 2 * P], in_=vec_rows["beta"][:].bitcast(F32), identity=ident[:])
             pairs = gbT[:].bitcast(BF16)
-            nc.vector.tensor_copy(
-                out=gam_f[:], in_=pairs[:, 0 : 2 * UNITS]
-            )
-            nc.vector.tensor_copy(
-                out=bet_f[:], in_=pairs[:, 2 * P : 2 * P + 2 * UNITS]
-            )
-            give_bank(i)
+            nc.scalar.copy(out=gam_f[:], in_=pairs[:, 0 : 2 * UNITS])
+            nc.scalar.copy(out=bet_f[:], in_=pairs[:, 2 * P : 2 * P + 2 * UNITS])
 
         planes = {}
         a_groups = {}
@@ -132,54 +132,62 @@ def tile_simclr_pa_kernel(tc, y_lin, gamma, beta, W2, b2, out):
                 nc.tensor.transpose(out=yT[:, j * P : (j + 1) * P], in_=y_words(c, 4 * h + j), identity=ident[:])
             y_banks[(c, h)] = (i, yT)
 
-        def gram(g, u):
-            i, gr = take_bank()
-            for e in range(2):
-                for r in range(8):
-                    cols = y_sb[g][:, r, u * UNIT_K + e : (u + 1) * UNIT_K : 2]
-                    nc.tensor.matmul(
-                        out=gr[:, e * P : (e + 1) * P], lhsT=cols, rhs=cols, start=(r == 0), stop=(r == 7)
-                    )
-            gram_banks[(g, u)] = (i, gr)
+        moments = {}
+        raw = {}
+        squares = {}
 
-        def sums(g):
-            i, gr = gram_banks[(g, 1)]
+        def gram(g):
+            i, gr = take_bank()
             for u in range(2):
                 for e in range(2):
-                    at = 2 * P + 2 * u + e
+                    at = (2 * u + e) * P
+                    for r in range(8):
+                        cols = y_sb[g][:, r, u * UNIT_K + e : (u + 1) * UNIT_K : 2]
+                        nc.tensor.matmul(out=gr[:, at : at + P], lhsT=cols, rhs=cols, start=(r == 0), stop=(r == 7))
+            gram_banks[g] = (i, gr)
+
+        def sums(g):
+            for u in range(2):
+                for e in range(2):
+                    at = 2 * P + 4 * g + 2 * u + e
                     for r in range(8):
                         cols = y_sb[g][:, r, u * UNIT_K + e : (u + 1) * UNIT_K : 2]
                         nc.tensor.matmul(
-                            out=gr[:, at : at + 1], lhsT=cols, rhs=ones[:], start=(r == 0), stop=(r == 7)
+                            out=misc["tile"][:, at : at + 1], lhsT=cols, rhs=ones[:], start=(r == 0), stop=(r == 7)
                         )
 
-        moments = {}
-
-        def moments_from_gram(g):
-            sm = gram_banks[(g, 1)][1][:, 2 * P : 2 * P + 4]
+        def means(g):
+            at = 2 * P + 4 * g
             mean = small.tile([P, 4], F32, name="mean")
+            sq = small.tile([P, 4], F32, name="sq4")
+            nc.scalar.activation(out=mean[:], in_=misc["tile"][:, at : at + 4], func=ACT.Copy, scale=1.0 / B)
+            nc.scalar.activation(out=sq[:], in_=misc["tile"][:, at : at + 4], func=ACT.Square, scale=1.0 / 32)
+            raw[g] = (mean, sq)
+            if g == PASSES - 1:
+                give_bank(misc["bank"])
+
+        def diagonals(g):
+            i, gr = gram_banks[g]
+            dg = junk.tile([P, 4, P], F32, name="dg")
+            nc.vector.tensor_tensor(
+                out=dg[:],
+                in0=gr[:].rearrange("p (t k) -> p t k", t=4),
+                in1=ident[:].unsqueeze(1).to_broadcast([P, 4, P]),
+                op=ALU.mult,
+            )
+            give_bank(i)
+            ey2 = small.tile([P, 4], F32, name="ey2")
+            nc.vector.tensor_reduce(out=ey2[:], in_=dg[:], op=ALU.add, axis=AXIS.X)
+            squares[g] = ey2
+
+        def variances(g):
+            mean, sq = raw[g]
+            ey2 = squares[g]
             var = small.tile([P, 4], F32, name="var")
-            m2 = small.tile([P, 4], F32, name="m2")
-            for u in range(2):
-                gr = gram_banks[(g, u)][1]
-                for e in range(2):
-                    dg = junk.tile([P, P], BF16, name="dg")
-                    nc.vector.scalar_tensor_tensor(
-                        out=dg[:],
-                        in0=gr[:, e * P : (e + 1) * P],
-                        scalar=1.0 / B,
-                        in1=ident[:],
-                        op0=ALU.mult,
-                        op1=ALU.mult,
-                        accum_out=var[:, 2 * u + e : 2 * u + e + 1],
-                    )
-                if u == 0:
-                    give_bank(gram_banks[(g, u)][0])
-            nc.vector.tensor_scalar_mul(out=mean[:], in0=sm, scalar1=1.0 / B)
-            give_bank(gram_banks[(g, 1)][0])
-            nc.vector.tensor_tensor(out=m2[:], in0=mean[:], in1=mean[:], op=ALU.mult)
-            nc.vector.tensor_tensor(out=var[:], in0=var[:], in1=m2[:], op=ALU.subtract)
-            nc.vector.tensor_scalar_max(out=var[:], in0=var[:], scalar1=0.0)
+            nc.gpsimd.tensor_tensor(out=var[:], in0=ey2[:], in1=sq[:], op=ALU.subtract)
+            nc.gpsimd.tensor_scalar(
+                out=var[:], in0=var[:], scalar1=0.0, scalar2=1.0 / B, op0=ALU.max, op1=ALU.mult
+            )
             moments[2 * g] = (mean[:], var[:], 4)
 
         stats = {}
@@ -210,9 +218,10 @@ def tile_simclr_pa_kernel(tc, y_lin, gamma, beta, W2, b2, out):
             sc = small.tile([P, n], F32, name="sc%d" % n)
             ms = small.tile([P, n], F32, name="ms%d" % n)
             bi = small.tile([P, n], F32, name="bi%d" % n)
-            nc.vector.tensor_tensor(out=sc[:], in0=rstds[c][:], in1=gam_f[:, 2 * c : 2 * c + n], op=ALU.mult)
-            nc.vector.tensor_tensor(out=ms[:], in0=mean, in1=sc[:], op=ALU.mult)
-            nc.vector.tensor_tensor(out=bi[:], in0=bet_f[:, 2 * c : 2 * c + n], in1=ms[:], op=ALU.subtract)
+            eng = nc.vector if n == 2 else nc.gpsimd
+            eng.tensor_tensor(out=sc[:], in0=rstds[c][:], in1=gam_f[:, 2 * c : 2 * c + n], op=ALU.mult)
+            eng.tensor_tensor(out=ms[:], in0=mean, in1=sc[:], op=ALU.mult)
+            eng.tensor_tensor(out=bi[:], in0=bet_f[:, 2 * c : 2 * c + n], in1=ms[:], op=ALU.subtract)
             for j in range(n // 2):
                 factors[c + j] = (sc[:, 2 * j : 2 * j + 2], bi[:, 2 * j : 2 * j + 2])
 
@@ -368,8 +377,7 @@ def tile_simclr_pa_kernel(tc, y_lin, gamma, beta, W2, b2, out):
         factors_of(0)
         affine(0, 0)
         affine(0, 1)
-        gram(1, 0)
-        gram(1, 1)
+        gram(1)
         sums(1)
         stats_half(1, 0)
         stats_half(1, 1)
@@ -379,106 +387,108 @@ def tile_simclr_pa_kernel(tc, y_lin, gamma, beta, W2, b2, out):
         affine(1, 0)
         transpose_half(2, 0)
         transpose_half(3, 0)
-        moments_from_gram(1)
+        diagonals(1)
+        means(1)
+        variances(1)
         rstd_of(2)
         affine(1, 1)
-        regroup(0, 0, "vector")
         factors_of(2)
+        regroup(0, 0, "vector")
         affine(2, 0)
-        affine(3, 0)
-        gram(2, 0)
-        gram(2, 1)
+        gram(2)
         sums(2)
+        regroup(0, 1, "gpsimd")
         transpose_half(2, 1)
-        transpose_half(3, 1)
-        regroup(0, 1, "vector")
-        quantise_a(0, 0, 1)
-        moments_from_gram(2)
+        affine(3, 0)
+        diagonals(2)
+        means(2)
+        variances(2)
+        weights_transpose(0, 0)
+        weights_transpose(1, 0)
         affine(2, 1)
         rstd_of(4)
         factors_of(4)
-        gram(3, 0)
-        gram(3, 1)
+        weights_exit(0, 0, "vector")
+        weights_exit(1, 0, "vector")
+        gram(3)
         sums(3)
         transpose_half(4, 0)
         transpose_half(5, 0)
-        affine(4, 0)
-        regroup(1, 0, "vector")
-        quantise_a(0, 1, 1)
-        affine(5, 0)
-        moments_from_gram(3)
-        rstd_of(6)
-        weights_transpose(0, 0)
-        weights_transpose(1, 0)
-        weights_exit(0, 0, "vector")
-        transpose_half(6, 0)
-        transpose_half(7, 0)
-        factors_of(6)
-        affine(6, 0)
-        weights_exit(1, 0, "vector")
         weights_transpose(2, 0)
         weights_transpose(3, 0)
-        affine(7, 0)
+        affine(4, 0)
+        regroup(1, 0, "vector")
         weights_exit(2, 0, "vector")
+        diagonals(3)
+        means(3)
+        variances(3)
         weights_exit(3, 0, "vector")
+        affine(5, 0)
+        rstd_of(6)
+        factors_of(6)
+        transpose_half(6, 0)
+        transpose_half(7, 0)
         weights_transpose(0, 1)
         weights_transpose(1, 1)
-        weights_exit(0, 1, "scalar")
+        weights_exit(0, 1, "vector")
+        affine(6, 0)
         weights_exit(1, 1, "scalar")
-        regroup(2, 0, "vector")
         weights_transpose(2, 1)
         weights_transpose(3, 1)
-        weights_exit(2, 1, "scalar")
+        affine(7, 0)
+        weights_exit(2, 1, "vector")
         weights_exit(3, 1, "scalar")
-        quantise_a(0, 2, 1)
+        quantise_a(0, 0, 2)
+        regroup(2, 0, "vector")
         quantise_w(0, 0, 2)
-        affine(3, 1)
         regroup(3, 0, "vector")
+        transpose_half(3, 1)
+        affine(3, 1)
+        quantise_a(0, 2, 2)
+        quantise_w(0, 2, 2)
         weights_transpose(0, 2)
         weights_transpose(1, 2)
         weights_exit(0, 2, "scalar")
         weights_exit(1, 2, "scalar")
-        quantise_w(0, 2, 2)
         weights_transpose(2, 2)
         weights_transpose(3, 2)
         weights_exit(2, 2, "scalar")
         weights_exit(3, 2, "scalar")
-        quantise_a(0, 3, 1)
+        transpose_half(4, 1)
         regroup(1, 1, "vector")
+        affine(4, 1)
         weights_transpose(0, 3)
         weights_transpose(1, 3)
+        open_tile(0, 0)
+        open_tile(1, 0)
+        open_tile(2, 0)
+        open_tile(3, 0)
+        matmul_pass(0, 0, 0)
+        matmul_pass(1, 0, 0)
+        matmul_pass(2, 0, 0)
+        matmul_pass(3, 0, 0)
+        matmul_pass(0, 0, 1)
+        matmul_pass(1, 0, 1)
+        matmul_pass(2, 0, 1)
+        matmul_pass(3, 0, 1)
         weights_exit(0, 3, "scalar")
         weights_exit(1, 3, "scalar")
-        transpose_half(4, 1)
-        transpose_half(5, 1)
-        affine(4, 1)
-        affine(5, 1)
         weights_transpose(2, 3)
         weights_transpose(3, 3)
-        weights_exit(2, 3, "vector")
-        weights_exit(3, 3, "vector")
+        weights_exit(2, 3, "scalar")
+        weights_exit(3, 3, "scalar")
+        transpose_half(5, 1)
         transpose_half(6, 1)
         transpose_half(7, 1)
+        affine(5, 1)
         affine(6, 1)
         affine(7, 1)
-        open_tile(0, 0)
-        matmul_pass(0, 0, 0)
-        matmul_pass(0, 0, 1)
         matmul_pass(0, 0, 2)
         matmul_pass(0, 0, 3)
-        open_tile(1, 0)
-        matmul_pass(1, 0, 0)
-        matmul_pass(1, 0, 1)
         matmul_pass(1, 0, 2)
         matmul_pass(1, 0, 3)
-        open_tile(2, 0)
-        matmul_pass(2, 0, 0)
-        matmul_pass(2, 0, 1)
         matmul_pass(2, 0, 2)
         matmul_pass(2, 0, 3)
-        open_tile(3, 0)
-        matmul_pass(3, 0, 0)
-        matmul_pass(3, 0, 1)
         matmul_pass(3, 0, 2)
         matmul_pass(3, 0, 3)
         quantise_w(1, 0, 2)
@@ -493,10 +503,6 @@ def tile_simclr_pa_kernel(tc, y_lin, gamma, beta, W2, b2, out):
         matmul_pass(1, 1, 1)
         matmul_pass(1, 1, 2)
         matmul_pass(1, 1, 3)
-        regroup(2, 1, "vector")
-        add_bias(0, 0)
-        square(0, 0)
-        quantise_a(1, 0, 2)
         open_tile(2, 1)
         matmul_pass(2, 1, 0)
         matmul_pass(2, 1, 1)
@@ -507,12 +513,16 @@ def tile_simclr_pa_kernel(tc, y_lin, gamma, beta, W2, b2, out):
         matmul_pass(3, 1, 1)
         matmul_pass(3, 1, 2)
         matmul_pass(3, 1, 3)
+        regroup(2, 1, "vector")
+        quantise_a(1, 0, 2)
+        regroup(3, 1, "vector")
+        add_bias(0, 0)
+        square(0, 0)
         add_bias(1, 0)
         square(1, 0)
-        regroup(3, 1, "vector")
+        quantise_a(1, 2, 2)
         add_bias(2, 0)
         square(2, 0)
-        quantise_a(1, 2, 2)
         add_bias(3, 0)
         square(3, 0)
         tiles = [(m, 1) for m in range(4)] + [(m, h) for m in range(4, 8) for h in range(2)]
@@ -525,4 +535,4 @@ def tile_simclr_pa_kernel(tc, y_lin, gamma, beta, W2, b2, out):
             if 1 <= n < len(tiles) + 1 and tiles[n - 1][1] == 1:
                 inverse_norm(tiles[n - 1][0])
             if 2 <= n < len(tiles) + 2 and tiles[n - 2][1] == 1:
-                scale_rows(tiles[n - 2][0], SPLIT)
+                scale_rows(tiles[n - 2][0], GPSIMD if tiles[n - 2][0] < 6 else SPLIT)

@@ -29,7 +29,6 @@ L2_EPS_SQ = 1e-24
 FLOPS = 2 * B * K * N
 
 SPLIT = (("scalar", 384), ("vector", 640))
-GPSIMD = (("gpsimd", 512), ("gpsimd", 512))
 
 
 def tile_simclr_pa_kernel(tc, y_lin, gamma, beta, W2, b2, out):
@@ -58,6 +57,8 @@ def tile_simclr_pa_kernel(tc, y_lin, gamma, beta, W2, b2, out):
         nc.vector.memset(ones[:], 1.0)
         eps = keep.tile([P, 1], F32, name="eps")
         nc.vector.memset(eps[:], BN_EPS)
+        warm = keep.tile([P, 1], F32, name="warm")
+        nc.scalar.activation(out=warm[:], in_=eps[:], func=ACT.Abs_reciprocal_sqrt)
         vec_rows = {}
         for name in ("gamma", "beta"):
             vec_rows[name] = keep.tile([P, UNIT_K], BF16, name="%s_rows" % name)
@@ -87,6 +88,7 @@ def tile_simclr_pa_kernel(tc, y_lin, gamma, beta, W2, b2, out):
         nc.sync.dma_start(out=b2_bc[:], in_=b2.partition_broadcast(P))
 
         gam_f = keep.tile([P, 2 * UNITS], F32, name="gam_f")
+        ngam_f = keep.tile([P, 2 * UNITS], F32, name="ngam_f")
         bet_f = keep.tile([P, 2 * UNITS], F32, name="bet_f")
 
         misc = {}
@@ -98,6 +100,7 @@ def tile_simclr_pa_kernel(tc, y_lin, gamma, beta, W2, b2, out):
             nc.tensor.transpose(out=gbT[:, P : 2 * P], in_=vec_rows["beta"][:].bitcast(F32), identity=ident[:])
             pairs = gbT[:].bitcast(BF16)
             nc.scalar.copy(out=gam_f[:], in_=pairs[:, 0 : 2 * UNITS])
+            nc.scalar.activation(out=ngam_f[:], in_=pairs[:, 0 : 2 * UNITS], func=ACT.Copy, scale=-1.0)
             nc.scalar.copy(out=bet_f[:], in_=pairs[:, 2 * P : 2 * P + 2 * UNITS])
 
         planes = {}
@@ -133,6 +136,12 @@ def tile_simclr_pa_kernel(tc, y_lin, gamma, beta, W2, b2, out):
             y_banks[(c, h)] = (i, yT)
 
         moments = {}
+        mgns = {}
+
+        def offsets(c, mean, n):
+            mgns[c] = small.tile([P, n], F32, name="mgn%d" % n)
+            nc.gpsimd.tensor_tensor(out=mgns[c][:], in0=mean, in1=ngam_f[:, 2 * c : 2 * c + n], op=ALU.mult)
+
         raw = {}
         squares = {}
 
@@ -163,6 +172,7 @@ def tile_simclr_pa_kernel(tc, y_lin, gamma, beta, W2, b2, out):
             nc.scalar.activation(out=mean[:], in_=misc["tile"][:, at : at + 4], func=ACT.Copy, scale=1.0 / B)
             nc.scalar.activation(out=sq[:], in_=misc["tile"][:, at : at + 4], func=ACT.Square, scale=1.0 / 32)
             raw[g] = (mean, sq)
+            offsets(2 * g, mean[:], 4)
             if g == PASSES - 1:
                 give_bank(misc["bank"])
 
@@ -205,6 +215,7 @@ def tile_simclr_pa_kernel(tc, y_lin, gamma, beta, W2, b2, out):
             for e in range(2):
                 nc.vector.bn_aggr(out=mv[:, e, :], in_=st[:, :, 3 * e : 3 * e + 3])
             moments[c] = (mv[:, :, 0], mv[:, :, 1], 2)
+            offsets(c, mv[:, :, 0], 2)
 
         rstds = {}
 
@@ -215,13 +226,23 @@ def tile_simclr_pa_kernel(tc, y_lin, gamma, beta, W2, b2, out):
 
         def factors_of(c):
             mean, var, n = moments[c]
+            rstd, mgn = rstds[c], mgns[c]
+            at = slice(2 * c, 2 * c + n)
             sc = small.tile([P, n], F32, name="sc%d" % n)
-            ms = small.tile([P, n], F32, name="ms%d" % n)
             bi = small.tile([P, n], F32, name="bi%d" % n)
-            eng = nc.vector if n == 2 else nc.gpsimd
-            eng.tensor_tensor(out=sc[:], in0=rstds[c][:], in1=gam_f[:, 2 * c : 2 * c + n], op=ALU.mult)
-            eng.tensor_tensor(out=ms[:], in0=mean, in1=sc[:], op=ALU.mult)
-            eng.tensor_tensor(out=bi[:], in0=bet_f[:, 2 * c : 2 * c + n], in1=ms[:], op=ALU.subtract)
+            if n == 2:
+                for e in range(2):
+                    col = slice(e, e + 1)
+                    k_col = slice(2 * c + e, 2 * c + e + 1)
+                    nc.scalar.activation(out=sc[:, col], in_=gam_f[:, k_col], func=ACT.Copy, scale=rstd[:, col])
+                    nc.scalar.activation(
+                        out=bi[:, col], in_=mgn[:, col], func=ACT.Identity, scale=rstd[:, col], bias=bet_f[:, k_col]
+                    )
+            else:
+                ms = small.tile([P, n], F32, name="ms")
+                nc.gpsimd.tensor_tensor(out=sc[:], in0=rstd[:], in1=gam_f[:, at], op=ALU.mult)
+                nc.gpsimd.tensor_tensor(out=ms[:], in0=rstd[:], in1=mgn[:], op=ALU.mult)
+                nc.gpsimd.tensor_tensor(out=bi[:], in0=bet_f[:, at], in1=ms[:], op=ALU.add)
             for j in range(n // 2):
                 factors[c + j] = (sc[:, 2 * j : 2 * j + 2], bi[:, 2 * j : 2 * j + 2])
 
@@ -343,7 +364,7 @@ def tile_simclr_pa_kernel(tc, y_lin, gamma, beta, W2, b2, out):
         def inverse_norm(m):
             ss = norms[m]
             cl = small.tile([P, 1], F32, name="cl")
-            nc.vector.tensor_scalar(
+            nc.gpsimd.tensor_scalar(
                 out=cl[:], in0=ss[:, 0:1], scalar1=ss[:, 1:2], scalar2=L2_EPS_SQ, op0=ALU.add, op1=ALU.max
             )
             inverse[m] = small.tile([P, 1], F32, name="rn")
@@ -382,50 +403,50 @@ def tile_simclr_pa_kernel(tc, y_lin, gamma, beta, W2, b2, out):
         stats_half(1, 0)
         stats_half(1, 1)
         moments_from_stats(1)
+        means(1)
         rstd_of(1)
         factors_of(1)
         affine(1, 0)
         transpose_half(2, 0)
         transpose_half(3, 0)
         diagonals(1)
-        means(1)
         variances(1)
         rstd_of(2)
-        affine(1, 1)
         factors_of(2)
+        affine(1, 1)
         regroup(0, 0, "vector")
         affine(2, 0)
         gram(2)
-        sums(2)
-        regroup(0, 1, "gpsimd")
         transpose_half(2, 1)
-        affine(3, 0)
-        diagonals(2)
+        sums(2)
         means(2)
+        affine(3, 0)
+        regroup(0, 1, "vector")
+        diagonals(2)
         variances(2)
         weights_transpose(0, 0)
         weights_transpose(1, 0)
-        affine(2, 1)
         rstd_of(4)
         factors_of(4)
-        weights_exit(0, 0, "vector")
-        weights_exit(1, 0, "vector")
+        affine(2, 1)
         gram(3)
         sums(3)
+        weights_exit(0, 0, "vector")
+        weights_exit(1, 0, "vector")
         transpose_half(4, 0)
         transpose_half(5, 0)
         weights_transpose(2, 0)
         weights_transpose(3, 0)
         affine(4, 0)
+        means(3)
         regroup(1, 0, "vector")
         weights_exit(2, 0, "vector")
         diagonals(3)
-        means(3)
         variances(3)
-        weights_exit(3, 0, "vector")
         affine(5, 0)
         rstd_of(6)
         factors_of(6)
+        weights_exit(3, 0, "vector")
         transpose_half(6, 0)
         transpose_half(7, 0)
         weights_transpose(0, 1)
@@ -444,8 +465,8 @@ def tile_simclr_pa_kernel(tc, y_lin, gamma, beta, W2, b2, out):
         regroup(3, 0, "vector")
         transpose_half(3, 1)
         affine(3, 1)
-        quantise_a(0, 2, 2)
         quantise_w(0, 2, 2)
+        quantise_a(0, 2, 2)
         weights_transpose(0, 2)
         weights_transpose(1, 2)
         weights_exit(0, 2, "scalar")
@@ -535,4 +556,4 @@ def tile_simclr_pa_kernel(tc, y_lin, gamma, beta, W2, b2, out):
             if 1 <= n < len(tiles) + 1 and tiles[n - 1][1] == 1:
                 inverse_norm(tiles[n - 1][0])
             if 2 <= n < len(tiles) + 2 and tiles[n - 2][1] == 1:
-                scale_rows(tiles[n - 2][0], GPSIMD if tiles[n - 2][0] < 6 else SPLIT)
+                scale_rows(tiles[n - 2][0], SPLIT)

@@ -137,10 +137,12 @@ def tile_simclr_pa_kernel(tc, y_lin, gamma, beta, W2, b2, out):
 
         moments = {}
         mgns = {}
+        mean_of = {}
 
-        def offsets(c, mean, n):
+        def offsets(c):
+            mean, n = mean_of[c]
             mgns[c] = small.tile([P, n], F32, name="mgn%d" % n)
-            nc.gpsimd.tensor_tensor(out=mgns[c][:], in0=mean, in1=ngam_f[:, 2 * c : 2 * c + n], op=ALU.mult)
+            nc.vector.tensor_tensor(out=mgns[c][:], in0=mean, in1=ngam_f[:, 2 * c : 2 * c + n], op=ALU.mult)
 
         raw = {}
         squares = {}
@@ -172,7 +174,7 @@ def tile_simclr_pa_kernel(tc, y_lin, gamma, beta, W2, b2, out):
             nc.scalar.activation(out=mean[:], in_=misc["tile"][:, at : at + 4], func=ACT.Copy, scale=1.0 / B)
             nc.scalar.activation(out=sq[:], in_=misc["tile"][:, at : at + 4], func=ACT.Square, scale=1.0 / 32)
             raw[g] = (mean, sq)
-            offsets(2 * g, mean[:], 4)
+            mean_of[2 * g] = (mean[:], 4)
             if g == PASSES - 1:
                 give_bank(misc["bank"])
 
@@ -194,11 +196,9 @@ def tile_simclr_pa_kernel(tc, y_lin, gamma, beta, W2, b2, out):
             mean, sq = raw[g]
             ey2 = squares[g]
             var = small.tile([P, 4], F32, name="var")
-            nc.gpsimd.tensor_tensor(out=var[:], in0=ey2[:], in1=sq[:], op=ALU.subtract)
-            nc.gpsimd.tensor_scalar(
-                out=var[:], in0=var[:], scalar1=0.0, scalar2=1.0 / B, op0=ALU.max, op1=ALU.mult
-            )
-            moments[2 * g] = (mean[:], var[:], 4)
+            nc.vector.tensor_tensor(out=var[:], in0=ey2[:], in1=sq[:], op=ALU.subtract)
+            nc.scalar.activation(out=var[:], in_=var[:], func=ACT.Relu, scale=1.0 / B)
+            moments[2 * g] = (var[:], 4)
 
         stats = {}
 
@@ -214,35 +214,28 @@ def tile_simclr_pa_kernel(tc, y_lin, gamma, beta, W2, b2, out):
             mv = small.tile([P, 2, 2], F32, name="mv")
             for e in range(2):
                 nc.vector.bn_aggr(out=mv[:, e, :], in_=st[:, :, 3 * e : 3 * e + 3])
-            moments[c] = (mv[:, :, 0], mv[:, :, 1], 2)
-            offsets(c, mv[:, :, 0], 2)
+            moments[c] = (mv[:, :, 1], 2)
+            mean_of[c] = (mv[:, :, 0], 2)
 
         rstds = {}
 
         def rstd_of(c):
-            mean, var, n = moments[c]
+            var, n = moments[c]
             rstds[c] = small.tile([P, n], F32, name="rstd%d" % n)
             nc.scalar.activation(out=rstds[c][:], in_=var, func=ACT.Abs_reciprocal_sqrt, bias=eps[:, 0:1], scale=1.0)
 
         def factors_of(c):
-            mean, var, n = moments[c]
+            var, n = moments[c]
             rstd, mgn = rstds[c], mgns[c]
-            at = slice(2 * c, 2 * c + n)
             sc = small.tile([P, n], F32, name="sc%d" % n)
             bi = small.tile([P, n], F32, name="bi%d" % n)
-            if n == 2:
-                for e in range(2):
-                    col = slice(e, e + 1)
-                    k_col = slice(2 * c + e, 2 * c + e + 1)
-                    nc.scalar.activation(out=sc[:, col], in_=gam_f[:, k_col], func=ACT.Copy, scale=rstd[:, col])
-                    nc.scalar.activation(
-                        out=bi[:, col], in_=mgn[:, col], func=ACT.Identity, scale=rstd[:, col], bias=bet_f[:, k_col]
-                    )
-            else:
-                ms = small.tile([P, n], F32, name="ms")
-                nc.gpsimd.tensor_tensor(out=sc[:], in0=rstd[:], in1=gam_f[:, at], op=ALU.mult)
-                nc.gpsimd.tensor_tensor(out=ms[:], in0=rstd[:], in1=mgn[:], op=ALU.mult)
-                nc.gpsimd.tensor_tensor(out=bi[:], in0=bet_f[:, at], in1=ms[:], op=ALU.add)
+            for j in range(n):
+                col = slice(j, j + 1)
+                k_col = slice(2 * c + j, 2 * c + j + 1)
+                nc.scalar.activation(out=sc[:, col], in_=gam_f[:, k_col], func=ACT.Copy, scale=rstd[:, col])
+                nc.scalar.activation(
+                    out=bi[:, col], in_=mgn[:, col], func=ACT.Identity, scale=rstd[:, col], bias=bet_f[:, k_col]
+                )
             for j in range(n // 2):
                 factors[c + j] = (sc[:, 2 * j : 2 * j + 2], bi[:, 2 * j : 2 * j + 2])
 
@@ -364,7 +357,7 @@ def tile_simclr_pa_kernel(tc, y_lin, gamma, beta, W2, b2, out):
         def inverse_norm(m):
             ss = norms[m]
             cl = small.tile([P, 1], F32, name="cl")
-            nc.gpsimd.tensor_scalar(
+            nc.vector.tensor_scalar(
                 out=cl[:], in0=ss[:, 0:1], scalar1=ss[:, 1:2], scalar2=L2_EPS_SQ, op0=ALU.add, op1=ALU.max
             )
             inverse[m] = small.tile([P, 1], F32, name="rn")
@@ -394,23 +387,26 @@ def tile_simclr_pa_kernel(tc, y_lin, gamma, beta, W2, b2, out):
         transpose_half(1, 1)
         gamma_beta()
         moments_from_stats(0)
+        offsets(0)
         rstd_of(0)
         factors_of(0)
+        stats_half(1, 0)
         affine(0, 0)
         affine(0, 1)
         gram(1)
         sums(1)
-        stats_half(1, 0)
         stats_half(1, 1)
         moments_from_stats(1)
         means(1)
         rstd_of(1)
+        diagonals(1)
+        offsets(1)
         factors_of(1)
         affine(1, 0)
         transpose_half(2, 0)
         transpose_half(3, 0)
-        diagonals(1)
         variances(1)
+        offsets(2)
         rstd_of(2)
         factors_of(2)
         affine(1, 1)
@@ -421,9 +417,10 @@ def tile_simclr_pa_kernel(tc, y_lin, gamma, beta, W2, b2, out):
         sums(2)
         means(2)
         affine(3, 0)
-        regroup(0, 1, "vector")
         diagonals(2)
+        regroup(0, 1, "vector")
         variances(2)
+        offsets(4)
         weights_transpose(0, 0)
         weights_transpose(1, 0)
         rstd_of(4)
@@ -440,9 +437,10 @@ def tile_simclr_pa_kernel(tc, y_lin, gamma, beta, W2, b2, out):
         affine(4, 0)
         means(3)
         regroup(1, 0, "vector")
-        weights_exit(2, 0, "vector")
         diagonals(3)
+        weights_exit(2, 0, "vector")
         variances(3)
+        offsets(6)
         affine(5, 0)
         rstd_of(6)
         factors_of(6)
@@ -480,18 +478,6 @@ def tile_simclr_pa_kernel(tc, y_lin, gamma, beta, W2, b2, out):
         affine(4, 1)
         weights_transpose(0, 3)
         weights_transpose(1, 3)
-        open_tile(0, 0)
-        open_tile(1, 0)
-        open_tile(2, 0)
-        open_tile(3, 0)
-        matmul_pass(0, 0, 0)
-        matmul_pass(1, 0, 0)
-        matmul_pass(2, 0, 0)
-        matmul_pass(3, 0, 0)
-        matmul_pass(0, 0, 1)
-        matmul_pass(1, 0, 1)
-        matmul_pass(2, 0, 1)
-        matmul_pass(3, 0, 1)
         weights_exit(0, 3, "scalar")
         weights_exit(1, 3, "scalar")
         weights_transpose(2, 3)
@@ -504,12 +490,24 @@ def tile_simclr_pa_kernel(tc, y_lin, gamma, beta, W2, b2, out):
         affine(5, 1)
         affine(6, 1)
         affine(7, 1)
+        open_tile(0, 0)
+        matmul_pass(0, 0, 0)
+        matmul_pass(0, 0, 1)
         matmul_pass(0, 0, 2)
         matmul_pass(0, 0, 3)
+        open_tile(1, 0)
+        matmul_pass(1, 0, 0)
+        matmul_pass(1, 0, 1)
         matmul_pass(1, 0, 2)
         matmul_pass(1, 0, 3)
+        open_tile(2, 0)
+        matmul_pass(2, 0, 0)
+        matmul_pass(2, 0, 1)
         matmul_pass(2, 0, 2)
         matmul_pass(2, 0, 3)
+        open_tile(3, 0)
+        matmul_pass(3, 0, 0)
+        matmul_pass(3, 0, 1)
         matmul_pass(3, 0, 2)
         matmul_pass(3, 0, 3)
         quantise_w(1, 0, 2)
@@ -535,17 +533,17 @@ def tile_simclr_pa_kernel(tc, y_lin, gamma, beta, W2, b2, out):
         matmul_pass(3, 1, 2)
         matmul_pass(3, 1, 3)
         regroup(2, 1, "vector")
-        quantise_a(1, 0, 2)
-        regroup(3, 1, "vector")
         add_bias(0, 0)
         square(0, 0)
+        quantise_a(1, 0, 2)
         add_bias(1, 0)
         square(1, 0)
-        quantise_a(1, 2, 2)
+        regroup(3, 1, "vector")
         add_bias(2, 0)
         square(2, 0)
         add_bias(3, 0)
         square(3, 0)
+        quantise_a(1, 2, 2)
         tiles = [(m, 1) for m in range(4)] + [(m, h) for m in range(4, 8) for h in range(2)]
         for n in range(len(tiles) + 3):
             if 4 <= n < len(tiles):

@@ -188,8 +188,11 @@ def tile_simclr_pa_kernel(tc, y_lin, gamma, beta, W2, b2, out):
                 op=ALU.mult,
             )
             give_bank(i)
+            squares[g] = dg
+
+        def diagonal_sums(g):
             ey2 = small.tile([P, 4], F32, name="ey2")
-            nc.vector.tensor_reduce(out=ey2[:], in_=dg[:], op=ALU.add, axis=AXIS.X)
+            nc.vector.tensor_reduce(out=ey2[:], in_=squares[g][:], op=ALU.add, axis=AXIS.X)
             squares[g] = ey2
 
         def variances(g):
@@ -197,8 +200,11 @@ def tile_simclr_pa_kernel(tc, y_lin, gamma, beta, W2, b2, out):
             ey2 = squares[g]
             var = small.tile([P, 4], F32, name="var")
             nc.vector.tensor_tensor(out=var[:], in0=ey2[:], in1=sq[:], op=ALU.subtract)
-            nc.scalar.activation(out=var[:], in_=var[:], func=ACT.Relu, scale=1.0 / B)
             moments[2 * g] = (var[:], 4)
+
+        def clip_variances(g):
+            var = moments[2 * g][0]
+            nc.scalar.activation(out=var, in_=var, func=ACT.Relu, scale=1.0 / B)
 
         stats = {}
 
@@ -239,19 +245,23 @@ def tile_simclr_pa_kernel(tc, y_lin, gamma, beta, W2, b2, out):
             for j in range(n // 2):
                 factors[c + j] = (sc[:, 2 * j : 2 * j + 2], bi[:, 2 * j : 2 * j + 2])
 
-        def affine(c, h):
+        def affine_one(c, h, e):
             sc, bi = factors[c]
             i, yT = y_banks[(c, h)]
             pairs = yT[:].bitcast(BF16).rearrange("p (b e) -> p b e", e=2)
+            nc.scalar.activation(
+                out=planes[(c // 2, h)][:, 2 * (c % 2) + e, :],
+                in_=pairs[:, :, e],
+                func=ACT.Relu,
+                bias=bi[:, e : e + 1],
+                scale=sc[:, e : e + 1],
+            )
+            if e == 1:
+                give_bank(i)
+
+        def affine(c, h):
             for e in range(2):
-                nc.scalar.activation(
-                    out=planes[(c // 2, h)][:, 2 * (c % 2) + e, :],
-                    in_=pairs[:, :, e],
-                    func=ACT.Relu,
-                    bias=bi[:, e : e + 1],
-                    scale=sc[:, e : e + 1],
-                )
-            give_bank(i)
+                affine_one(c, h, e)
 
         w_banks = {}
 
@@ -391,90 +401,110 @@ def tile_simclr_pa_kernel(tc, y_lin, gamma, beta, W2, b2, out):
         rstd_of(0)
         factors_of(0)
         stats_half(1, 0)
-        affine(0, 0)
-        affine(0, 1)
-        gram(1)
-        sums(1)
+        affine_one(0, 0, 0)
+        affine_one(0, 0, 1)
         stats_half(1, 1)
+        affine_one(0, 1, 0)
         moments_from_stats(1)
-        means(1)
-        rstd_of(1)
-        diagonals(1)
         offsets(1)
+        affine_one(0, 1, 1)
+        rstd_of(1)
         factors_of(1)
-        affine(1, 0)
         transpose_half(2, 0)
+        transpose_half(2, 1)
+        stats_half(2, 0)
+        affine_one(1, 0, 0)
+        affine_one(1, 0, 1)
+        stats_half(2, 1)
         transpose_half(3, 0)
-        variances(1)
+        gram(2)
+        sums(2)
+        transpose_half(3, 1)
+        affine_one(1, 1, 0)
+        moments_from_stats(2)
         offsets(2)
+        affine_one(1, 1, 1)
         rstd_of(2)
         factors_of(2)
-        affine(1, 1)
-        regroup(0, 0, "vector")
-        affine(2, 0)
-        gram(2)
-        transpose_half(2, 1)
-        sums(2)
+        stats_half(3, 0)
+        regroup(0, 0, "gpsimd")
+        affine_one(2, 0, 0)
         means(2)
-        affine(3, 0)
+        affine_one(2, 0, 1)
+        stats_half(3, 1)
+        affine_one(2, 1, 0)
+        moments_from_stats(3)
+        offsets(3)
+        affine_one(2, 1, 1)
+        rstd_of(3)
+        factors_of(3)
         diagonals(2)
-        regroup(0, 1, "vector")
-        variances(2)
-        offsets(4)
-        weights_transpose(0, 0)
-        weights_transpose(1, 0)
-        rstd_of(4)
-        factors_of(4)
-        affine(2, 1)
+        regroup(0, 1, "gpsimd")
         gram(3)
         sums(3)
+        affine_one(3, 0, 0)
+        affine_one(3, 0, 1)
+        diagonal_sums(2)
+        offsets(4)
+        affine_one(3, 1, 0)
+        variances(2)
+        weights_transpose(0, 0)
+        weights_transpose(1, 0)
+        affine_one(3, 1, 1)
+        clip_variances(2)
         weights_exit(0, 0, "vector")
-        weights_exit(1, 0, "vector")
         transpose_half(4, 0)
         transpose_half(5, 0)
-        weights_transpose(2, 0)
-        weights_transpose(3, 0)
-        affine(4, 0)
+        weights_exit(1, 0, "vector")
+        rstd_of(4)
+        factors_of(4)
+        affine_one(4, 0, 0)
         means(3)
-        regroup(1, 0, "vector")
+        affine_one(4, 0, 1)
         diagonals(3)
-        weights_exit(2, 0, "vector")
-        variances(3)
-        offsets(6)
-        affine(5, 0)
-        rstd_of(6)
-        factors_of(6)
-        weights_exit(3, 0, "vector")
+        regroup(1, 0, "vector")
+        diagonal_sums(3)
         transpose_half(6, 0)
         transpose_half(7, 0)
+        affine_one(5, 0, 0)
+        offsets(6)
+        weights_transpose(2, 0)
+        weights_transpose(3, 0)
+        weights_exit(2, 0, "vector")
+        variances(3)
+        affine_one(5, 0, 1)
+        clip_variances(3)
+        weights_exit(3, 0, "vector")
         weights_transpose(0, 1)
         weights_transpose(1, 1)
-        weights_exit(0, 1, "vector")
-        affine(6, 0)
+        weights_exit(0, 1, "scalar")
+        rstd_of(6)
+        factors_of(6)
         weights_exit(1, 1, "scalar")
+        regroup(1, 1, "vector")
         weights_transpose(2, 1)
         weights_transpose(3, 1)
-        affine(7, 0)
+        affine_one(6, 0, 0)
+        affine_one(6, 0, 1)
         weights_exit(2, 1, "vector")
-        weights_exit(3, 1, "scalar")
         quantise_a(0, 0, 2)
+        affine_one(7, 0, 0)
+        affine_one(7, 0, 1)
+        weights_exit(3, 1, "scalar")
         regroup(2, 0, "vector")
         quantise_w(0, 0, 2)
         regroup(3, 0, "vector")
-        transpose_half(3, 1)
-        affine(3, 1)
-        quantise_w(0, 2, 2)
-        quantise_a(0, 2, 2)
         weights_transpose(0, 2)
         weights_transpose(1, 2)
         weights_exit(0, 2, "scalar")
         weights_exit(1, 2, "scalar")
+        quantise_w(0, 2, 2)
         weights_transpose(2, 2)
         weights_transpose(3, 2)
         weights_exit(2, 2, "scalar")
         weights_exit(3, 2, "scalar")
+        quantise_a(0, 2, 2)
         transpose_half(4, 1)
-        regroup(1, 1, "vector")
         affine(4, 1)
         weights_transpose(0, 3)
         weights_transpose(1, 3)

@@ -91,17 +91,15 @@ def tile_simclr_pa_kernel(tc, y_lin, gamma, beta, W2, b2, out):
         ngam_f = keep.tile([P, 2 * UNITS], F32, name="ngam_f")
         bet_f = keep.tile([P, 2 * UNITS], F32, name="bet_f")
 
-        misc = {}
-
         def gamma_beta():
-            misc["bank"], misc["tile"] = take_bank()
-            gbT = misc["tile"]
+            i, gbT = take_bank()
             nc.tensor.transpose(out=gbT[:, 0:P], in_=vec_rows["gamma"][:].bitcast(F32), identity=ident[:])
             nc.tensor.transpose(out=gbT[:, P : 2 * P], in_=vec_rows["beta"][:].bitcast(F32), identity=ident[:])
             pairs = gbT[:].bitcast(BF16)
             nc.scalar.copy(out=gam_f[:], in_=pairs[:, 0 : 2 * UNITS])
             nc.scalar.activation(out=ngam_f[:], in_=pairs[:, 0 : 2 * UNITS], func=ACT.Copy, scale=-1.0)
             nc.scalar.copy(out=bet_f[:], in_=pairs[:, 2 * P : 2 * P + 2 * UNITS])
+            give_bank(i)
 
         planes = {}
         a_groups = {}
@@ -147,36 +145,35 @@ def tile_simclr_pa_kernel(tc, y_lin, gamma, beta, W2, b2, out):
         raw = {}
         squares = {}
 
-        def gram(g):
-            i, gr = take_bank()
-            for u in range(2):
-                for e in range(2):
-                    at = (2 * u + e) * P
-                    for r in range(8):
-                        cols = y_sb[g][:, r, u * UNIT_K + e : (u + 1) * UNIT_K : 2]
-                        nc.tensor.matmul(out=gr[:, at : at + P], lhsT=cols, rhs=cols, start=(r == 0), stop=(r == 7))
-            gram_banks[g] = (i, gr)
+        sum_banks = {}
 
-        def sums(g):
-            for u in range(2):
-                for e in range(2):
-                    at = 2 * P + 4 * g + 2 * u + e
-                    for r in range(8):
-                        cols = y_sb[g][:, r, u * UNIT_K + e : (u + 1) * UNIT_K : 2]
-                        nc.tensor.matmul(
-                            out=misc["tile"][:, at : at + 1], lhsT=cols, rhs=ones[:], start=(r == 0), stop=(r == 7)
-                        )
+        def gram(g, j):
+            if j == 0:
+                gram_banks[g], sum_banks[g] = take_bank(), take_bank()
+            u, e = divmod(j, 2)
+            tiles = [y_sb[g][:, r, u * UNIT_K + e : (u + 1) * UNIT_K : 2] for r in range(8)]
+            for r in range(8):
+                nc.tensor.matmul(
+                    out=gram_banks[g][1][:, j * P : (j + 1) * P],
+                    lhsT=tiles[r],
+                    rhs=tiles[r],
+                    start=(r == 0),
+                    stop=(r == 7),
+                )
+            for r in range(8):
+                nc.tensor.matmul(
+                    out=sum_banks[g][1][:, j : j + 1], lhsT=tiles[r], rhs=ones[:], start=(r == 0), stop=(r == 7)
+                )
 
         def means(g):
-            at = 2 * P + 4 * g
+            i, column_sums = sum_banks[g]
             mean = small.tile([P, 4], F32, name="mean")
             sq = small.tile([P, 4], F32, name="sq4")
-            nc.scalar.activation(out=mean[:], in_=misc["tile"][:, at : at + 4], func=ACT.Copy, scale=1.0 / B)
-            nc.scalar.activation(out=sq[:], in_=misc["tile"][:, at : at + 4], func=ACT.Square, scale=1.0 / 32)
+            nc.scalar.activation(out=mean[:], in_=column_sums[:, 0:4], func=ACT.Copy, scale=1.0 / B)
+            nc.scalar.activation(out=sq[:], in_=column_sums[:, 0:4], func=ACT.Square, scale=1.0 / 32)
             raw[g] = (mean, sq)
             mean_of[2 * g] = (mean[:], 4)
-            if g == PASSES - 1:
-                give_bank(misc["bank"])
+            give_bank(i)
 
         def diagonals(g):
             i, gr = gram_banks[g]
@@ -417,9 +414,9 @@ def tile_simclr_pa_kernel(tc, y_lin, gamma, beta, W2, b2, out):
         affine_one(1, 0, 1)
         stats_half(2, 1)
         transpose_half(3, 0)
-        gram(2)
-        sums(2)
+        gram(2, 0)
         transpose_half(3, 1)
+        gram(2, 1)
         affine_one(1, 1, 0)
         moments_from_stats(2)
         offsets(2)
@@ -429,59 +426,63 @@ def tile_simclr_pa_kernel(tc, y_lin, gamma, beta, W2, b2, out):
         stats_half(3, 0)
         regroup(0, 0, "gpsimd")
         affine_one(2, 0, 0)
-        means(2)
+        gram(2, 2)
         affine_one(2, 0, 1)
         stats_half(3, 1)
         affine_one(2, 1, 0)
         moments_from_stats(3)
         offsets(3)
         affine_one(2, 1, 1)
+        transpose_half(4, 0)
+        gram(2, 3)
         rstd_of(3)
         factors_of(3)
+        means(2)
         diagonals(2)
         regroup(0, 1, "gpsimd")
-        gram(3)
-        sums(3)
+        transpose_half(5, 0)
+        gram(3, 0)
         affine_one(3, 0, 0)
         affine_one(3, 0, 1)
         diagonal_sums(2)
         offsets(4)
+        weights_transpose(0, 0)
+        gram(3, 1)
         affine_one(3, 1, 0)
         variances(2)
-        weights_transpose(0, 0)
         weights_transpose(1, 0)
         affine_one(3, 1, 1)
+        regroup(1, 0, "gpsimd")
         clip_variances(2)
+        gram(3, 2)
         weights_exit(0, 0, "vector")
-        transpose_half(4, 0)
-        transpose_half(5, 0)
         weights_exit(1, 0, "vector")
         rstd_of(4)
         factors_of(4)
-        affine_one(4, 0, 0)
-        means(3)
-        affine_one(4, 0, 1)
-        diagonals(3)
-        regroup(1, 0, "vector")
-        diagonal_sums(3)
         transpose_half(6, 0)
+        gram(3, 3)
+        affine_one(4, 0, 0)
+        affine_one(4, 0, 1)
+        means(3)
         transpose_half(7, 0)
-        affine_one(5, 0, 0)
-        offsets(6)
+        diagonals(3)
         weights_transpose(2, 0)
         weights_transpose(3, 0)
         weights_exit(2, 0, "vector")
+        diagonal_sums(3)
+        affine_one(5, 0, 0)
+        offsets(6)
         variances(3)
+        weights_exit(3, 0, "vector")
+        regroup(1, 1, "gpsimd")
         affine_one(5, 0, 1)
         clip_variances(3)
-        weights_exit(3, 0, "vector")
         weights_transpose(0, 1)
         weights_transpose(1, 1)
-        weights_exit(0, 1, "scalar")
+        weights_exit(0, 1, "vector")
         rstd_of(6)
         factors_of(6)
-        weights_exit(1, 1, "scalar")
-        regroup(1, 1, "vector")
+        weights_exit(1, 1, "vector")
         weights_transpose(2, 1)
         weights_transpose(3, 1)
         affine_one(6, 0, 0)
@@ -494,6 +495,8 @@ def tile_simclr_pa_kernel(tc, y_lin, gamma, beta, W2, b2, out):
         regroup(2, 0, "vector")
         quantise_w(0, 0, 2)
         regroup(3, 0, "vector")
+        transpose_half(4, 1)
+        affine(4, 1)
         weights_transpose(0, 2)
         weights_transpose(1, 2)
         weights_exit(0, 2, "scalar")
@@ -504,8 +507,6 @@ def tile_simclr_pa_kernel(tc, y_lin, gamma, beta, W2, b2, out):
         weights_exit(2, 2, "scalar")
         weights_exit(3, 2, "scalar")
         quantise_a(0, 2, 2)
-        transpose_half(4, 1)
-        affine(4, 1)
         weights_transpose(0, 3)
         weights_transpose(1, 3)
         weights_exit(0, 3, "scalar")

@@ -28,7 +28,11 @@ L2_EPS_SQ = 1e-24
 
 FLOPS = 2 * B * K * N
 
+WHOLE = (slice(0, HALF),)
+HALVES = (slice(0, QUARTER), slice(QUARTER, HALF))
+
 SPLIT = (("scalar", 384), ("vector", 640))
+GPSIMD = (("gpsimd", 512), ("gpsimd", 512))
 
 
 def tile_simclr_pa_kernel(tc, y_lin, gamma, beta, W2, b2, out):
@@ -147,23 +151,30 @@ def tile_simclr_pa_kernel(tc, y_lin, gamma, beta, W2, b2, out):
 
         sum_banks = {}
 
+        def y_columns(g, j, r):
+            u, e = divmod(j, 2)
+            return y_sb[g][:, r, u * UNIT_K + e : (u + 1) * UNIT_K : 2]
+
         def gram(g, j):
             if j == 0:
-                gram_banks[g], sum_banks[g] = take_bank(), take_bank()
-            u, e = divmod(j, 2)
-            tiles = [y_sb[g][:, r, u * UNIT_K + e : (u + 1) * UNIT_K : 2] for r in range(8)]
+                gram_banks[g] = take_bank()
             for r in range(8):
+                cols = y_columns(g, j, r)
                 nc.tensor.matmul(
-                    out=gram_banks[g][1][:, j * P : (j + 1) * P],
-                    lhsT=tiles[r],
-                    rhs=tiles[r],
-                    start=(r == 0),
-                    stop=(r == 7),
+                    out=gram_banks[g][1][:, j * P : (j + 1) * P], lhsT=cols, rhs=cols, start=(r == 0), stop=(r == 7)
                 )
-            for r in range(8):
-                nc.tensor.matmul(
-                    out=sum_banks[g][1][:, j : j + 1], lhsT=tiles[r], rhs=ones[:], start=(r == 0), stop=(r == 7)
-                )
+
+        def sums(g):
+            sum_banks[g] = take_bank()
+            for j in range(4):
+                for r in range(8):
+                    nc.tensor.matmul(
+                        out=sum_banks[g][1][:, j : j + 1],
+                        lhsT=y_columns(g, j, r),
+                        rhs=ones[:],
+                        start=(r == 0),
+                        stop=(r == 7),
+                    )
 
         def means(g):
             i, column_sums = sum_banks[g]
@@ -326,46 +337,56 @@ def tile_simclr_pa_kernel(tc, y_lin, gamma, beta, W2, b2, out):
         def open_tile(m, h):
             accs[(m, h)] = take_bank()
 
-        def matmul_pass(m, h, g):
+        def matmul_pass(m, h, g, part=slice(0, HALF)):
             rows = slice((m % 4) * P, (m % 4 + 1) * P)
             nc.tensor.matmul_mx(
-                out=accs[(m, h)][1][:],
+                out=accs[(m, h)][1][:, part],
                 lhsT=a_codes[:, m // 4, g, rows].bitcast(FP8X4),
                 lhsT_scale=a_scales[:, m // 4, g, rows],
-                rhs=w_codes[:, h, g, :].bitcast(FP8X4),
-                rhs_scale=w_scales[:, h, g, :],
+                rhs=w_codes[:, h, g, part].bitcast(FP8X4),
+                rhs_scale=w_scales[:, h, g, part],
                 start=(g == 0),
                 stop=(g == PASSES - 1),
             )
 
-        def matmul_tile(m, h):
+        def matmul_tile(m, h, parts):
             open_tile(m, h)
-            for g in range(PASSES):
-                matmul_pass(m, h, g)
+            for part in parts:
+                for g in range(PASSES):
+                    matmul_pass(m, h, g, part)
 
-        def add_bias(m, h):
+        def add_bias(m, h, parts=WHOLE):
             if m not in norms:
-                norms[m] = small.tile([P, 2], F32, name="ss")
+                norms[m] = small.tile([P, 3], F32, name="ss")
                 if m % 2 == 0:
                     pair = keep.tile([P, 2, N], F32, name="p%d" % (m // 2), tag="w%d" % (m // 2))
                     p_tiles[m], p_tiles[m + 1] = pair[:, 0, :], pair[:, 1, :]
-            cols = slice(h * HALF, (h + 1) * HALF)
             i, acc = accs[(m, h)]
-            nc.vector.tensor_tensor(out=p_tiles[m][:, cols], in0=acc[:], in1=b2_bc[:, cols], op=ALU.add)
+            for part in parts:
+                cols = slice(h * HALF + part.start, h * HALF + part.stop)
+                nc.vector.tensor_tensor(out=p_tiles[m][:, cols], in0=acc[:, part], in1=b2_bc[:, cols], op=ALU.add)
             give_bank(i)
 
-        def square(m, h):
-            cols = slice(h * HALF, (h + 1) * HALF)
-            sq = junk.tile([P, HALF], BF16, name="sq")
-            nc.scalar.activation(out=sq[:], in_=p_tiles[m][:, cols], func=ACT.Square, accum_out=norms[m][:, h : h + 1])
+        def square(m, h, parts=WHOLE):
+            for x, part in enumerate(parts):
+                cols = slice(h * HALF + part.start, h * HALF + part.stop)
+                sq = junk.tile([P, HALF], BF16, name="sq")
+                nc.scalar.activation(
+                    out=sq[:, part],
+                    in_=p_tiles[m][:, cols],
+                    func=ACT.Square,
+                    accum_out=norms[m][:, h + x : h + x + 1],
+                )
 
         inverse = {}
 
-        def inverse_norm(m):
+        def inverse_norm(m, parts=2):
             ss = norms[m]
+            if parts > 2:
+                nc.vector.tensor_tensor(out=ss[:, 0:1], in0=ss[:, 0:1], in1=ss[:, 1:2], op=ALU.add)
             cl = small.tile([P, 1], F32, name="cl")
             nc.vector.tensor_scalar(
-                out=cl[:], in0=ss[:, 0:1], scalar1=ss[:, 1:2], scalar2=L2_EPS_SQ, op0=ALU.add, op1=ALU.max
+                out=cl[:], in0=ss[:, 0:1], scalar1=ss[:, parts - 1 : parts], scalar2=L2_EPS_SQ, op0=ALU.add, op1=ALU.max
             )
             inverse[m] = small.tile([P, 1], F32, name="rn")
             nc.scalar.activation(out=inverse[m][:], in_=cl[:], func=ACT.Abs_reciprocal_sqrt)
@@ -415,8 +436,11 @@ def tile_simclr_pa_kernel(tc, y_lin, gamma, beta, W2, b2, out):
         stats_half(2, 1)
         transpose_half(3, 0)
         gram(2, 0)
-        transpose_half(3, 1)
         gram(2, 1)
+        transpose_half(3, 1)
+        gram(2, 2)
+        gram(2, 3)
+        sums(2)
         affine_one(1, 1, 0)
         moments_from_stats(2)
         offsets(2)
@@ -426,50 +450,49 @@ def tile_simclr_pa_kernel(tc, y_lin, gamma, beta, W2, b2, out):
         stats_half(3, 0)
         regroup(0, 0, "gpsimd")
         affine_one(2, 0, 0)
-        gram(2, 2)
+        means(2)
         affine_one(2, 0, 1)
         stats_half(3, 1)
         affine_one(2, 1, 0)
         moments_from_stats(3)
         offsets(3)
         affine_one(2, 1, 1)
-        transpose_half(4, 0)
-        gram(2, 3)
         rstd_of(3)
         factors_of(3)
-        means(2)
         diagonals(2)
         regroup(0, 1, "gpsimd")
-        transpose_half(5, 0)
         gram(3, 0)
+        gram(3, 1)
         affine_one(3, 0, 0)
         affine_one(3, 0, 1)
         diagonal_sums(2)
         offsets(4)
-        weights_transpose(0, 0)
-        gram(3, 1)
         affine_one(3, 1, 0)
         variances(2)
+        weights_transpose(0, 0)
+        gram(3, 2)
+        gram(3, 3)
         weights_transpose(1, 0)
+        sums(3)
         affine_one(3, 1, 1)
         regroup(1, 0, "gpsimd")
         clip_variances(2)
-        gram(3, 2)
         weights_exit(0, 0, "vector")
+        transpose_half(4, 0)
+        transpose_half(5, 0)
         weights_exit(1, 0, "vector")
         rstd_of(4)
         factors_of(4)
-        transpose_half(6, 0)
-        gram(3, 3)
         affine_one(4, 0, 0)
-        affine_one(4, 0, 1)
         means(3)
-        transpose_half(7, 0)
+        affine_one(4, 0, 1)
         diagonals(3)
         weights_transpose(2, 0)
         weights_transpose(3, 0)
         weights_exit(2, 0, "vector")
         diagonal_sums(3)
+        transpose_half(6, 0)
+        transpose_half(7, 0)
         affine_one(5, 0, 0)
         offsets(6)
         variances(3)
@@ -482,7 +505,7 @@ def tile_simclr_pa_kernel(tc, y_lin, gamma, beta, W2, b2, out):
         weights_exit(0, 1, "vector")
         rstd_of(6)
         factors_of(6)
-        weights_exit(1, 1, "vector")
+        weights_exit(1, 1, "scalar")
         weights_transpose(2, 1)
         weights_transpose(3, 1)
         affine_one(6, 0, 0)
@@ -500,7 +523,7 @@ def tile_simclr_pa_kernel(tc, y_lin, gamma, beta, W2, b2, out):
         weights_transpose(0, 2)
         weights_transpose(1, 2)
         weights_exit(0, 2, "scalar")
-        weights_exit(1, 2, "scalar")
+        weights_exit(1, 2, "vector")
         quantise_w(0, 2, 2)
         weights_transpose(2, 2)
         weights_transpose(3, 2)
@@ -577,12 +600,14 @@ def tile_simclr_pa_kernel(tc, y_lin, gamma, beta, W2, b2, out):
         quantise_a(1, 2, 2)
         tiles = [(m, 1) for m in range(4)] + [(m, h) for m in range(4, 8) for h in range(2)]
         for n in range(len(tiles) + 3):
-            if 4 <= n < len(tiles):
-                matmul_tile(tiles[n][0], tiles[n][1])
             if n < len(tiles):
-                add_bias(tiles[n][0], tiles[n][1])
-                square(tiles[n][0], tiles[n][1])
+                m, h = tiles[n]
+                parts = HALVES if n == len(tiles) - 1 else WHOLE
+                if n >= 4:
+                    matmul_tile(m, h, parts)
+                add_bias(m, h, parts)
+                square(m, h, parts)
             if 1 <= n < len(tiles) + 1 and tiles[n - 1][1] == 1:
-                inverse_norm(tiles[n - 1][0])
+                inverse_norm(tiles[n - 1][0], 3 if n == len(tiles) else 2)
             if 2 <= n < len(tiles) + 2 and tiles[n - 2][1] == 1:
-                scale_rows(tiles[n - 2][0], SPLIT)
+                scale_rows(tiles[n - 2][0], GPSIMD if tiles[n - 2][0] in (0, 1, 3, 4) else SPLIT)

from contextlib import ExitStack

import concourse.mybir as mybir
from concourse.masks import make_identity

F32 = mybir.dt.float32
BF16 = mybir.dt.bfloat16
U32 = mybir.dt.uint32
U8 = mybir.dt.uint8
FP8X4 = mybir.dt.float8_e4m3fn_x4
ACT = mybir.ActivationFunctionType
ALU = mybir.AluOpType
AXIS = mybir.AxisListType

P = 128
B = 1024
K = 2048
N = 1024
K_PASS = 512
PASSES = K // K_PASS
UNITS = 2 * PASSES
UNIT_K = K // UNITS
HALF = 512
QUARTER = 256
BANKS = 8
BN_EPS = 1e-5
L2_EPS_SQ = 1e-24

FLOPS = 2 * B * K * N

WHOLE = (slice(0, HALF),)
HALVES = (slice(0, QUARTER), slice(QUARTER, HALF))

SPLIT = (("scalar", 384), ("vector", 640))
GPSIMD = (("gpsimd", 512), ("gpsimd", 512))


def tile_simclr_pa_kernel(tc, y_lin, gamma, beta, W2, b2, out):
    nc = tc.nc
    with ExitStack() as ctx:
        keep = ctx.enter_context(tc.tile_pool(name="keep", bufs=1))
        small = ctx.enter_context(tc.tile_pool(name="small", bufs=UNITS))
        junk = ctx.enter_context(tc.tile_pool(name="junk", bufs=2))
        psum = ctx.enter_context(tc.psum_pool(name="psum", bufs=1))
        ctx.enter_context(tc.manual_schedule())

        free_banks = list(range(BANKS))
        taken = [0]

        def take_bank():
            i = free_banks[taken[0]]
            taken[0] += 1
            return i, psum.tile([P, HALF], F32, name="bank%d" % i, tag="bank%d" % i)

        def give_bank(i):
            free_banks.append(i)

        ident = keep.tile([P, P], F32, name="ident")
        make_identity(nc, ident[:])
        ones = keep.tile([P, 1], BF16, name="ones")
        nc.vector.memset(ones[:], 1.0)
        eps = keep.tile([P, 1], F32, name="eps")
        nc.vector.memset(eps[:], BN_EPS)
        warm = keep.tile([P, 1], F32, name="warm")
        nc.scalar.activation(out=warm[:], in_=eps[:], func=ACT.Abs_reciprocal_sqrt)
        vec_rows = {}
        for name in ("gamma", "beta"):
            vec_rows[name] = keep.tile([P, UNIT_K], BF16, name="%s_rows" % name)
            nc.vector.memset(vec_rows[name][:].bitcast(F32), 0.0)

        y_view = y_lin.rearrange("(r p) k -> p r k", p=P)
        w_view = W2.rearrange("(r p) k -> p r k", p=P)
        y_first = {}
        for c in range(2):
            for h in range(2):
                y_first[(c, h)] = keep.tile([P, 4, UNIT_K], BF16, name="y_first%d%d" % (c, h))
                nc.sync.dma_start(
                    out=y_first[(c, h)][:], in_=y_view[:, 4 * h : 4 * h + 4, c * UNIT_K : (c + 1) * UNIT_K]
                )
            if c == 0:
                nc.sync.dma_start(out=vec_rows["gamma"][0:UNITS, :], in_=gamma.rearrange("(c w) -> c w", w=UNIT_K))
                nc.sync.dma_start(out=vec_rows["beta"][0:UNITS, :], in_=beta.rearrange("(c w) -> c w", w=UNIT_K))
        y_sb = {}
        for g in range(1, PASSES):
            y_sb[g] = keep.tile([P, 8, K_PASS], BF16, name="y%d" % g)
            nc.sync.dma_start(out=y_sb[g][:], in_=y_view[:, :, g * K_PASS : (g + 1) * K_PASS])
        w_sb = {}
        for r in range(0, 8, 2):
            w_sb[r // 2] = keep.tile([P, 2, K], BF16, name="w%d" % (r // 2))
            nc.sync.dma_start(out=w_sb[r // 2][:], in_=w_view[:, r : r + 2, :])
        b2_bc = keep.tile([P, N], BF16, name="b2_bc")
        nc.sync.dma_start(out=b2_bc[:], in_=b2.partition_broadcast(P))

        gam_f = keep.tile([P, 2 * UNITS], F32, name="gam_f")
        ngam_f = keep.tile([P, 2 * UNITS], F32, name="ngam_f")
        bet_f = keep.tile([P, 2 * UNITS], F32, name="bet_f")

        def gamma_beta():
            i, gbT = take_bank()
            nc.tensor.transpose(out=gbT[:, 0:P], in_=vec_rows["gamma"][:].bitcast(F32), identity=ident[:])
            nc.tensor.transpose(out=gbT[:, P : 2 * P], in_=vec_rows["beta"][:].bitcast(F32), identity=ident[:])
            pairs = gbT[:].bitcast(BF16)
            nc.scalar.copy(out=gam_f[:], in_=pairs[:, 0 : 2 * UNITS])
            nc.scalar.activation(out=ngam_f[:], in_=pairs[:, 0 : 2 * UNITS], func=ACT.Copy, scale=-1.0)
            nc.scalar.copy(out=bet_f[:], in_=pairs[:, 2 * P : 2 * P + 2 * UNITS])
            give_bank(i)

        planes = {}
        a_groups = {}
        w_groups = {}
        for h in range(2):
            a_all = keep.tile([P, PASSES, HALF, 4], BF16, name="ag%d" % h, align_bytes=64)
            w_all = keep.tile([P, PASSES, HALF, 4], BF16, name="wg%d" % h, align_bytes=64)
            for g in range(PASSES):
                a_groups[(g, h)] = a_all[:, g]
                w_groups[(g, h)] = w_all[:, g]
                planes[(g, h)] = keep.tile([P, 4, HALF], BF16, name="planes%d%d" % (g, h))
            a_groups[h], w_groups[h] = a_all, w_all
        a_codes = keep.tile([P, 2, PASSES, HALF], U32, name="a_codes", align_bytes=64)
        a_scales = keep.tile([P, 2, PASSES, HALF], U8, name="a_scales", align_bytes=64)
        w_codes = keep.tile([P, 2, PASSES, HALF], U32, name="w_codes", align_bytes=64)
        w_scales = keep.tile([P, 2, PASSES, HALF], U8, name="w_scales", align_bytes=64)

        y_banks = {}
        gram_banks = {}
        factors = {}

        def y_words(c, r):
            g, u = divmod(c, 2)
            if g == 0:
                return y_first[(c, r // 4)][:, r % 4, :].bitcast(F32)
            return y_sb[g][:, r, :].bitcast(F32)[:, u * P : (u + 1) * P]

        def transpose_half(c, h):
            i, yT = take_bank()
            for j in range(4):
                nc.tensor.transpose(out=yT[:, j * P : (j + 1) * P], in_=y_words(c, 4 * h + j), identity=ident[:])
            y_banks[(c, h)] = (i, yT)

        moments = {}
        mgns = {}
        mean_of = {}

        def offsets(c):
            mean, n = mean_of[c]
            mgns[c] = small.tile([P, n], F32, name="mgn%d" % n)
            nc.vector.tensor_tensor(out=mgns[c][:], in0=mean, in1=ngam_f[:, 2 * c : 2 * c + n], op=ALU.mult)

        raw = {}
        squares = {}

        sum_banks = {}

        def y_columns(g, j, r):
            u, e = divmod(j, 2)
            return y_sb[g][:, r, u * UNIT_K + e : (u + 1) * UNIT_K : 2]

        def gram(g, j):
            if j == 0:
                gram_banks[g] = take_bank()
            for r in range(8):
                cols = y_columns(g, j, r)
                nc.tensor.matmul(
                    out=gram_banks[g][1][:, j * P : (j + 1) * P], lhsT=cols, rhs=cols, start=(r == 0), stop=(r == 7)
                )

        def sums(g):
            sum_banks[g] = take_bank()
            for j in range(4):
                for r in range(8):
                    nc.tensor.matmul(
                        out=sum_banks[g][1][:, j : j + 1],
                        lhsT=y_columns(g, j, r),
                        rhs=ones[:],
                        start=(r == 0),
                        stop=(r == 7),
                    )

        def means(g):
            i, column_sums = sum_banks[g]
            mean = small.tile([P, 4], F32, name="mean")
            sq = small.tile([P, 4], F32, name="sq4")
            nc.scalar.activation(out=mean[:], in_=column_sums[:, 0:4], func=ACT.Copy, scale=1.0 / B)
            nc.scalar.activation(out=sq[:], in_=column_sums[:, 0:4], func=ACT.Square, scale=1.0 / 32)
            raw[g] = (mean, sq)
            mean_of[2 * g] = (mean[:], 4)
            give_bank(i)

        def diagonals(g):
            i, gr = gram_banks[g]
            dg = junk.tile([P, 4, P], F32, name="dg")
            nc.vector.tensor_tensor(
                out=dg[:],
                in0=gr[:].rearrange("p (t k) -> p t k", t=4),
                in1=ident[:].unsqueeze(1).to_broadcast([P, 4, P]),
                op=ALU.mult,
            )
            give_bank(i)
            squares[g] = dg

        def diagonal_sums(g):
            ey2 = small.tile([P, 4], F32, name="ey2")
            nc.vector.tensor_reduce(out=ey2[:], in_=squares[g][:], op=ALU.add, axis=AXIS.X)
            squares[g] = ey2

        def variances(g):
            mean, sq = raw[g]
            ey2 = squares[g]
            var = small.tile([P, 4], F32, name="var")
            nc.vector.tensor_tensor(out=var[:], in0=ey2[:], in1=sq[:], op=ALU.subtract)
            moments[2 * g] = (var[:], 4)

        def clip_variances(g):
            var = moments[2 * g][0]
            nc.scalar.activation(out=var, in_=var, func=ACT.Relu, scale=1.0 / B)

        stats = {}

        def stats_half(c, h):
            if h == 0:
                stats[c] = small.tile([P, 4, 6], F32, name="st")
            pairs = y_banks[(c, h)][1][:].bitcast(BF16)
            for j in range(2):
                nc.vector.bn_stats(out=stats[c][:, 2 * h + j, :], in_=pairs[:, j * HALF : (j + 1) * HALF])

        def moments_from_stats(c):
            st = stats[c]
            mv = small.tile([P, 2, 2], F32, name="mv")
            for e in range(2):
                nc.vector.bn_aggr(out=mv[:, e, :], in_=st[:, :, 3 * e : 3 * e + 3])
            moments[c] = (mv[:, :, 1], 2)
            mean_of[c] = (mv[:, :, 0], 2)

        rstds = {}

        def rstd_of(c):
            var, n = moments[c]
            rstds[c] = small.tile([P, n], F32, name="rstd%d" % n)
            nc.scalar.activation(out=rstds[c][:], in_=var, func=ACT.Abs_reciprocal_sqrt, bias=eps[:, 0:1], scale=1.0)

        def factors_of(c):
            var, n = moments[c]
            rstd, mgn = rstds[c], mgns[c]
            sc = small.tile([P, n], F32, name="sc%d" % n)
            bi = small.tile([P, n], F32, name="bi%d" % n)
            for j in range(n):
                col = slice(j, j + 1)
                k_col = slice(2 * c + j, 2 * c + j + 1)
                nc.scalar.activation(out=sc[:, col], in_=gam_f[:, k_col], func=ACT.Copy, scale=rstd[:, col])
                nc.scalar.activation(
                    out=bi[:, col], in_=mgn[:, col], func=ACT.Identity, scale=rstd[:, col], bias=bet_f[:, k_col]
                )
            for j in range(n // 2):
                factors[c + j] = (sc[:, 2 * j : 2 * j + 2], bi[:, 2 * j : 2 * j + 2])

        def affine_one(c, h, e):
            sc, bi = factors[c]
            i, yT = y_banks[(c, h)]
            pairs = yT[:].bitcast(BF16).rearrange("p (b e) -> p b e", e=2)
            nc.scalar.activation(
                out=planes[(c // 2, h)][:, 2 * (c % 2) + e, :],
                in_=pairs[:, :, e],
                func=ACT.Relu,
                bias=bi[:, e : e + 1],
                scale=sc[:, e : e + 1],
            )
            if e == 1:
                give_bank(i)

        def affine(c, h):
            for e in range(2):
                affine_one(c, h, e)

        w_banks = {}

        def weights_transpose(g, q):
            i, wT = take_bank()
            halves = wT[:].rearrange("p (u n) -> p u n", u=2)
            for j in range(2):
                for u in range(2):
                    w0 = g * 2 * P + u * P
                    nc.tensor.transpose(
                        out=halves[:, u, j * P : (j + 1) * P],
                        in_=w_sb[q][:, j, :].bitcast(F32)[:, w0 : w0 + P],
                        identity=ident[:],
                    )
            w_banks[(g, q)] = (i, halves)

        def weights_exit(g, q, engine):
            i, halves = w_banks[(g, q)]
            words = (
                w_groups[(g, q // 2)].rearrange("p n t -> p (n t)").bitcast(F32).rearrange("p (n u) -> p n u", u=2)
            )
            dst = words[:, (q % 2) * QUARTER : (q % 2 + 1) * QUARTER, :]
            if engine == "vector":
                nc.vector.tensor_copy(out=dst, in_=halves.rearrange("p u n -> p n u"))
            else:
                nc.scalar.copy(out=dst, in_=halves.rearrange("p u n -> p n u"))
            give_bank(i)

        def quantise(groups, codes, scales, h, g, n):
            part = slice(g, g + n)
            nc.vector.quantize_mx(
                out=codes[:, h, part, :].rearrange("p g n -> p (g n)").bitcast(FP8X4),
                scales=scales[:, h, part, :].rearrange("p g n -> p (g n)"),
                in_=groups[h][:, part].rearrange("p g n t -> p (g n t)"),
            )

        def quantise_w(h, g, n):
            quantise(w_groups, w_codes, w_scales, h, g, n)

        def quantise_a(h, g, n):
            quantise(a_groups, a_codes, a_scales, h, g, n)

        def regroup(g, h, engine):
            src, dst = planes[(g, h)], a_groups[(g, h)]
            if engine == "gpsimd":
                for s in range(2):
                    part = slice(s * QUARTER, (s + 1) * QUARTER)
                    nc.gpsimd.tensor_scalar(
                        out=dst[:, part, :],
                        in0=src[:, :, part].rearrange("p t b -> p b t"),
                        scalar1=1.0,
                        scalar2=0.0,
                        op0=ALU.mult,
                        op1=ALU.add,
                    )
            else:
                nc.vector.tensor_copy(
                    out=dst.rearrange("p (c i) t -> p c t i", i=4), in_=src[:].rearrange("p t (c i) -> p c t i", i=4)
                )

        accs = {}
        p_tiles = {}
        norms = {}

        def open_tile(m, h):
            accs[(m, h)] = take_bank()

        def matmul_pass(m, h, g, part=slice(0, HALF)):
            rows = slice((m % 4) * P, (m % 4 + 1) * P)
            nc.tensor.matmul_mx(
                out=accs[(m, h)][1][:, part],
                lhsT=a_codes[:, m // 4, g, rows].bitcast(FP8X4),
                lhsT_scale=a_scales[:, m // 4, g, rows],
                rhs=w_codes[:, h, g, part].bitcast(FP8X4),
                rhs_scale=w_scales[:, h, g, part],
                start=(g == 0),
                stop=(g == PASSES - 1),
            )

        def matmul_tile(m, h, parts):
            open_tile(m, h)
            for part in parts:
                for g in range(PASSES):
                    matmul_pass(m, h, g, part)

        def add_bias(m, h, parts=WHOLE):
            if m not in norms:
                norms[m] = small.tile([P, 3], F32, name="ss")
                if m % 2 == 0:
                    pair = keep.tile([P, 2, N], F32, name="p%d" % (m // 2), tag="w%d" % (m // 2))
                    p_tiles[m], p_tiles[m + 1] = pair[:, 0, :], pair[:, 1, :]
            i, acc = accs[(m, h)]
            for part in parts:
                cols = slice(h * HALF + part.start, h * HALF + part.stop)
                nc.vector.tensor_tensor(out=p_tiles[m][:, cols], in0=acc[:, part], in1=b2_bc[:, cols], op=ALU.add)
            give_bank(i)

        def square(m, h, parts=WHOLE):
            for x, part in enumerate(parts):
                cols = slice(h * HALF + part.start, h * HALF + part.stop)
                sq = junk.tile([P, HALF], BF16, name="sq")
                nc.scalar.activation(
                    out=sq[:, part],
                    in_=p_tiles[m][:, cols],
                    func=ACT.Square,
                    accum_out=norms[m][:, h + x : h + x + 1],
                )

        inverse = {}

        def inverse_norm(m, parts=2):
            ss = norms[m]
            if parts > 2:
                nc.vector.tensor_tensor(out=ss[:, 0:1], in0=ss[:, 0:1], in1=ss[:, 1:2], op=ALU.add)
            cl = small.tile([P, 1], F32, name="cl")
            nc.vector.tensor_scalar(
                out=cl[:], in0=ss[:, 0:1], scalar1=ss[:, parts - 1 : parts], scalar2=L2_EPS_SQ, op0=ALU.add, op1=ALU.max
            )
            inverse[m] = small.tile([P, 1], F32, name="rn")
            nc.scalar.activation(out=inverse[m][:], in_=cl[:], func=ACT.Abs_reciprocal_sqrt)

        def scale_rows(m, shares):
            pb, rn = p_tiles[m], inverse[m][:, 0:1]
            start = 0
            for engine, width in shares:
                cols = slice(start, start + width)
                start += width
                if engine == "scalar":
                    nc.scalar.activation(out=pb[:, cols], in_=pb[:, cols], func=ACT.Copy, scale=rn)
                elif engine == "vector":
                    nc.vector.tensor_scalar_mul(out=pb[:, cols], in0=pb[:, cols], scalar1=rn)
                else:
                    nc.gpsimd.tensor_scalar(
                        out=pb[:, cols], in0=pb[:, cols], scalar1=rn, scalar2=0.0, op0=ALU.mult, op1=ALU.add
                    )
                nc.sync.dma_start(out=out[m * P : (m + 1) * P, cols], in_=pb[:, cols])

        transpose_half(0, 0)
        transpose_half(0, 1)
        stats_half(0, 0)
        stats_half(0, 1)
        transpose_half(1, 0)
        transpose_half(1, 1)
        gamma_beta()
        moments_from_stats(0)
        offsets(0)
        rstd_of(0)
        factors_of(0)
        stats_half(1, 0)
        affine_one(0, 0, 0)
        affine_one(0, 0, 1)
        stats_half(1, 1)
        affine_one(0, 1, 0)
        moments_from_stats(1)
        offsets(1)
        affine_one(0, 1, 1)
        rstd_of(1)
        factors_of(1)
        transpose_half(2, 0)
        transpose_half(2, 1)
        stats_half(2, 0)
        affine_one(1, 0, 0)
        affine_one(1, 0, 1)
        stats_half(2, 1)
        transpose_half(3, 0)
        gram(2, 0)
        gram(2, 1)
        transpose_half(3, 1)
        gram(2, 2)
        gram(2, 3)
        sums(2)
        affine_one(1, 1, 0)
        moments_from_stats(2)
        offsets(2)
        affine_one(1, 1, 1)
        rstd_of(2)
        factors_of(2)
        stats_half(3, 0)
        regroup(0, 0, "gpsimd")
        affine_one(2, 0, 0)
        means(2)
        affine_one(2, 0, 1)
        stats_half(3, 1)
        affine_one(2, 1, 0)
        moments_from_stats(3)
        offsets(3)
        affine_one(2, 1, 1)
        rstd_of(3)
        factors_of(3)
        diagonals(2)
        regroup(0, 1, "gpsimd")
        gram(3, 0)
        gram(3, 1)
        affine_one(3, 0, 0)
        affine_one(3, 0, 1)
        diagonal_sums(2)
        offsets(4)
        affine_one(3, 1, 0)
        variances(2)
        weights_transpose(0, 0)
        gram(3, 2)
        gram(3, 3)
        weights_transpose(1, 0)
        sums(3)
        affine_one(3, 1, 1)
        regroup(1, 0, "gpsimd")
        clip_variances(2)
        weights_exit(0, 0, "vector")
        transpose_half(4, 0)
        transpose_half(5, 0)
        weights_exit(1, 0, "vector")
        rstd_of(4)
        factors_of(4)
        affine_one(4, 0, 0)
        means(3)
        affine_one(4, 0, 1)
        diagonals(3)
        weights_transpose(2, 0)
        weights_transpose(3, 0)
        weights_exit(2, 0, "vector")
        diagonal_sums(3)
        transpose_half(6, 0)
        transpose_half(7, 0)
        affine_one(5, 0, 0)
        offsets(6)
        variances(3)
        weights_exit(3, 0, "vector")
        regroup(1, 1, "gpsimd")
        affine_one(5, 0, 1)
        clip_variances(3)
        weights_transpose(0, 1)
        weights_transpose(1, 1)
        weights_exit(0, 1, "vector")
        rstd_of(6)
        factors_of(6)
        weights_exit(1, 1, "scalar")
        weights_transpose(2, 1)
        weights_transpose(3, 1)
        affine_one(6, 0, 0)
        affine_one(6, 0, 1)
        weights_exit(2, 1, "vector")
        quantise_a(0, 0, 2)
        affine_one(7, 0, 0)
        affine_one(7, 0, 1)
        weights_exit(3, 1, "scalar")
        regroup(2, 0, "vector")
        quantise_w(0, 0, 2)
        regroup(3, 0, "vector")
        transpose_half(4, 1)
        affine(4, 1)
        weights_transpose(0, 2)
        weights_transpose(1, 2)
        weights_exit(0, 2, "scalar")
        weights_exit(1, 2, "vector")
        quantise_w(0, 2, 2)
        weights_transpose(2, 2)
        weights_transpose(3, 2)
        weights_exit(2, 2, "scalar")
        weights_exit(3, 2, "scalar")
        quantise_a(0, 2, 2)
        weights_transpose(0, 3)
        weights_transpose(1, 3)
        weights_exit(0, 3, "scalar")
        weights_exit(1, 3, "scalar")
        weights_transpose(2, 3)
        weights_transpose(3, 3)
        weights_exit(2, 3, "scalar")
        weights_exit(3, 3, "scalar")
        transpose_half(5, 1)
        transpose_half(6, 1)
        transpose_half(7, 1)
        affine(5, 1)
        affine(6, 1)
        affine(7, 1)
        open_tile(0, 0)
        matmul_pass(0, 0, 0)
        matmul_pass(0, 0, 1)
        matmul_pass(0, 0, 2)
        matmul_pass(0, 0, 3)
        open_tile(1, 0)
        matmul_pass(1, 0, 0)
        matmul_pass(1, 0, 1)
        matmul_pass(1, 0, 2)
        matmul_pass(1, 0, 3)
        open_tile(2, 0)
        matmul_pass(2, 0, 0)
        matmul_pass(2, 0, 1)
        matmul_pass(2, 0, 2)
        matmul_pass(2, 0, 3)
        open_tile(3, 0)
        matmul_pass(3, 0, 0)
        matmul_pass(3, 0, 1)
        matmul_pass(3, 0, 2)
        matmul_pass(3, 0, 3)
        quantise_w(1, 0, 2)
        open_tile(0, 1)
        matmul_pass(0, 1, 0)
        matmul_pass(0, 1, 1)
        quantise_w(1, 2, 2)
        matmul_pass(0, 1, 2)
        matmul_pass(0, 1, 3)
        open_tile(1, 1)
        matmul_pass(1, 1, 0)
        matmul_pass(1, 1, 1)
        matmul_pass(1, 1, 2)
        matmul_pass(1, 1, 3)
        open_tile(2, 1)
        matmul_pass(2, 1, 0)
        matmul_pass(2, 1, 1)
        matmul_pass(2, 1, 2)
        matmul_pass(2, 1, 3)
        open_tile(3, 1)
        matmul_pass(3, 1, 0)
        matmul_pass(3, 1, 1)
        matmul_pass(3, 1, 2)
        matmul_pass(3, 1, 3)
        regroup(2, 1, "vector")
        add_bias(0, 0)
        square(0, 0)
        quantise_a(1, 0, 2)
        add_bias(1, 0)
        square(1, 0)
        regroup(3, 1, "vector")
        add_bias(2, 0)
        square(2, 0)
        add_bias(3, 0)
        square(3, 0)
        quantise_a(1, 2, 2)
        tiles = [(m, 1) for m in range(4)] + [(m, h) for m in range(4, 8) for h in range(2)]
        for n in range(len(tiles) + 3):
            if n < len(tiles):
                m, h = tiles[n]
                parts = HALVES if n == len(tiles) - 1 else WHOLE
                if n >= 4:
                    matmul_tile(m, h, parts)
                add_bias(m, h, parts)
                square(m, h, parts)
            if 1 <= n < len(tiles) + 1 and tiles[n - 1][1] == 1:
                inverse_norm(tiles[n - 1][0], 3 if n == len(tiles) else 2)
            if 2 <= n < len(tiles) + 2 and tiles[n - 2][1] == 1:
                scale_rows(tiles[n - 2][0], GPSIMD if tiles[n - 2][0] in (0, 1, 3, 4) else SPLIT)
